import numpy as np
import ml_dtypes


def mxq(x, axis, fmt="e4m3"):
    dtype, down = {"e4m3": (ml_dtypes.float8_e4m3fn, 7), "e5m2": (ml_dtypes.float8_e5m2, 14)}[fmt]
    v = np.moveaxis(np.asarray(x, np.float32).astype(ml_dtypes.bfloat16).astype(np.float64), axis, -1)
    blocks = v.reshape(v.shape[:-1] + (-1, 32))
    amax = np.abs(blocks).max(-1, keepdims=True)
    byte = np.maximum(np.where(amax > 0, np.frexp(amax)[1] - 1 + 127, 0) - down, 1)
    scale = np.exp2(byte - 127.0)
    codes = (blocks / scale).astype(np.float32).astype(dtype).astype(np.float64)
    return np.moveaxis((codes * scale).reshape(v.shape), -1, axis)


WIDE = False


def mx_kscale(k):
    if not WIDE:
        return np.ones(k)
    levels = np.array([10, -10, 5, -5, 0])
    a = np.random.permutation(np.resize(levels, k // 512 * 4)).reshape(k // 512, 4)
    idx = np.arange(k)
    return np.exp2(a[idx // 512, idx % 128 // 32])


BF16 = ml_dtypes.bfloat16


def bf(x):
    return np.asarray(x, np.float32).astype(BF16)


def f64(x):
    return np.asarray(x).astype(np.float64)


B, CIN, R, COUT, H, W, D, KS = 2, 512, 512, 256, 16, 16, 16, 3
P = H * W * D
PAD = (KS - 1) // 2


def slice_in_dim(t, a, b, axis):
    idx = [slice(None)] * t.ndim
    idx[axis] = slice(a, b)
    return t[tuple(idx)]


def axis_contract(t, U, axis):
    L = t.shape[axis] - (KS - 1)
    rshape = (1, U.shape[1], 1, 1, 1)
    acc = slice_in_dim(t, 0, L, axis) * U[0].reshape(rshape)
    for k in range(1, KS):
        acc = acc + slice_in_dim(t, k, k + L, axis) * U[k].reshape(rshape)
    return acc


def setup_inputs():
    s, t = mx_kscale(CIN), mx_kscale(R)
    return {"x": bf(np.random.standard_normal((B, CIN, H, W, D)) * s[None, :, None, None, None]),
            "U_kh": bf(np.random.standard_normal((KS, R)) / np.sqrt(KS)),
            "U_kw": bf(np.random.standard_normal((KS, R)) / np.sqrt(KS)),
            "U_kd": bf(np.random.standard_normal((KS, R)) / np.sqrt(KS)),
            "U_c_in": bf(np.random.standard_normal((CIN, R)) / np.sqrt(CIN) / s[:, None] * t[None, :]),
            "U_c_out": bf(np.random.standard_normal((R, COUT)) / np.sqrt(R) / t[:, None]),
            "bias": bf(np.random.standard_normal(COUT) * 0.5)}


def reference(x, U_kh, U_kw, U_kd, U_c_in, U_c_out, bias):
    xq = mxq(f64(x), 1, "e4m3").reshape(B, CIN, P)
    y = (mxq(f64(U_c_in), 0, "e4m3").T @ xq).reshape(B, R, H, W, D)
    y = np.pad(y, ((0, 0), (0, 0), (PAD, PAD), (PAD, PAD), (PAD, PAD)))
    y = axis_contract(y, f64(U_kh), 2)
    y = axis_contract(y, f64(U_kw), 3)
    y = axis_contract(y, f64(U_kd), 4)
    out = (mxq(f64(U_c_out), 0, "e4m3").T @ mxq(y, 1, "e4m3").reshape(B, R, P)).reshape(B, COUT, H, W, D)
    return out + f64(bias)[None, :, None, None, None]

@@ -1,0 +1,290 @@
+from contextlib import ExitStack
+
+import concourse.mybir as mybir
+
+FLOPS = 2 * 512 * 512 * 8192 + 2 * 512 * 256 * 8192 + 2 * 9 * 512 * 8192
+
+F32 = mybir.dt.float32
+BF16 = mybir.dt.bfloat16
+U32 = mybir.dt.uint32
+U8 = mybir.dt.uint8
+FP8X4 = mybir.dt.float8_e4m3fn_x4
+ACTF = mybir.ActivationFunctionType
+ALU = mybir.AluOpType
+
+P = 128
+SLICE = 256
+SLAB = 1024
+HALF = 512
+N_SLABS = 8
+N_UNITS = 32
+
+
+def tile_lowrankconv3d_t_kernel(tc, x, U_kh, U_kw, U_kd, U_c_in, U_c_out, bias, out):
+    nc = tc.nc
+    xv = [x[b].rearrange("(p j) h w d -> p j (h w d)", j=4) for b in range(2)]
+    ov = [out[b].rearrange("o h w d -> o (h w d)") for b in range(2)]
+
+    with ExitStack() as ctx:
+        const = ctx.enter_context(tc.tile_pool(name="const", bufs=1))
+        rawp = ctx.enter_context(tc.tile_pool(name="rawp", bufs=3))
+        xgp = ctx.enter_context(tc.tile_pool(name="xgp", bufs=3))
+        y1p = ctx.enter_context(tc.tile_pool(name="y1p", bufs=3))
+        y2p = ctx.enter_context(tc.tile_pool(name="y2p", bufs=3))
+        ep = ctx.enter_context(tc.tile_pool(name="ep", bufs=2))
+        ygp = ctx.enter_context(tc.tile_pool(name="ygp", bufs=2))
+        yqp = ctx.enter_context(tc.tile_pool(name="yqp", bufs=2))
+        osp = ctx.enter_context(tc.tile_pool(name="osp", bufs=4))
+        pyp = ctx.enter_context(tc.psum_pool(name="pyp", bufs=6))
+        pop = ctx.enter_context(tc.psum_pool(name="pop", bufs=2))
+        ctx.enter_context(tc.manual_schedule())
+
+        xq = const.tile([P, N_SLABS * SLAB], U32, align_bytes=64, name="xq")
+        xs = const.tile([P, N_SLABS * SLAB], U8, align_bytes=64, name="xs")
+        w_raw = const.tile([P, 4, 512], BF16, name="w_raw")
+        w_grp = const.tile([P, 512, 4], BF16, align_bytes=64, name="w_grp")
+        wq = const.tile([P, 512], U32, align_bytes=64, name="wq")
+        ws = const.tile([P, 512], U8, align_bytes=64, name="ws")
+        v_raw = const.tile([P, 4, 256], BF16, name="v_raw")
+        v_grp = const.tile([P, 256, 4], BF16, align_bytes=64, name="v_grp")
+        vq = const.tile([P, 256], U32, align_bytes=64, name="vq")
+        vs = const.tile([P, 256], U8, align_bytes=64, name="vs")
+        cb_h = const.tile([P, 3, 4], BF16, name="cb_h")
+        cb_w = const.tile([P, 3, 4], BF16, name="cb_w")
+        cb_d = const.tile([P, 3, 4], BF16, name="cb_d")
+        cf = const.tile([P, 3, 3, 4], F32, name="cf")
+        bias_b = const.tile([P, 2], BF16, name="bias_b")
+        bias_f = const.tile([P, 2], F32, name="bias_f")
+
+        raw = {}
+        xg = {}
+        pb = {}
+        y1 = {}
+        y2 = {}
+        ee = {}
+        yg = {}
+        yq = {}
+        ys = {}
+        po = {}
+
+        def coef(f, k, t):
+            return cf[:, f, k, t : t + 1]
+
+        def load_raw(s):
+            b, sl = divmod(s, 4)
+            r = rawp.tile([P, 4, SLAB], BF16, name="raw")
+            nc.sync.dma_start(out=r[:], in_=xv[b][:, :, sl * SLAB : (sl + 1) * SLAB])
+            raw[s] = r
+
+        def regroup_x(s, half, on_vector):
+            g = xgp.tile([P, HALF, 4], BF16, align_bytes=64, name="xg")
+            src = raw[s][:, :, half * HALF : (half + 1) * HALF].rearrange("p t (c i) -> p c t i", i=4)
+            dst = g[:].rearrange("p (c i) t -> p c t i", i=4)
+            if on_vector:
+                nc.vector.tensor_copy(out=dst, in_=src)
+            else:
+                nc.scalar.copy(out=dst, in_=src)
+            xg[(s, half)] = g
+
+        def quant_x(s, half):
+            c0 = s * SLAB + half * HALF
+            nc.vector.quantize_mx(
+                out=xq[:, c0 : c0 + HALF].bitcast(FP8X4),
+                scales=xs[:, c0 : c0 + HALF],
+                in_=xg[(s, half)][:].rearrange("p w j -> p (w j)"),
+            )
+
+        def mm1(u):
+            s, t = divmod(u, 4)
+            b, sl = divmod(s, 4)
+            h0 = sl * 4
+            banks = []
+            for k in range(3):
+                lo = h0 - 1 + 2 * k
+                o0, n = 0, 512
+                if lo < 0:
+                    lo, o0, n = 0, SLICE, SLICE
+                elif lo + 1 > 15:
+                    n = SLICE
+                c0 = b * 4096 + lo * SLICE
+                bank = pyp.tile([P, 512], F32, name="pb")
+                nc.tensor.matmul_mx(
+                    out=bank[:, o0 : o0 + n],
+                    lhsT=wq[:, t * P : (t + 1) * P].bitcast(FP8X4),
+                    lhsT_scale=ws[:, t * P : (t + 1) * P],
+                    rhs=xq[:, c0 : c0 + n].bitcast(FP8X4),
+                    rhs_scale=xs[:, c0 : c0 + n],
+                    start=True,
+                    stop=True,
+                )
+                banks.append(bank)
+            pb[u] = banks
+
+        def scale_copy(dst, src, c):
+            nc.scalar.activation(out=dst, in_=src, func=ACTF.Copy, scale=c)
+
+        def mac(acc, src, c):
+            nc.vector.scalar_tensor_tensor(out=acc, in0=src, scalar=c, in1=acc, op0=ALU.mult, op1=ALU.add)
+
+        def a_h(u):
+            t = u % 4
+            a = y1p.tile([P, SLAB], F32, name="y1")
+            b0, b1, b2 = pb[u]
+            c = coef(0, 1, t)
+            scale_copy(a[:, 0:256], b0[:, 256:512], c)
+            scale_copy(a[:, 256:768], b1[:, :], c)
+            scale_copy(a[:, 768:1024], b2[:, 0:256], c)
+            y1[u] = a
+
+        def v_h(u):
+            s, t = divmod(u, 4)
+            sl = s % 4
+            a = y1[u]
+            b0, b1, b2 = pb[u]
+            c = coef(0, 0, t)
+            if sl == 0:
+                mac(a[:, 256:512], b0[:, 256:512], c)
+            else:
+                mac(a[:, 0:512], b0[:, :], c)
+            mac(a[:, 512:1024], b1[:, :], c)
+            c = coef(0, 2, t)
+            mac(a[:, 0:512], b1[:, :], c)
+            if sl == 3:
+                mac(a[:, 512:768], b2[:, 0:256], c)
+            else:
+                mac(a[:, 512:1024], b2[:, :], c)
+
+        def a_w(u):
+            a = y2p.tile([P, SLAB], F32, name="y2")
+            scale_copy(a[:], y1[u][:], coef(1, 1, u % 4))
+            y2[u] = a
+
+        def v_w(u):
+            t = u % 4
+            src = y1[u][:].rearrange("p (s q) -> p s q", q=SLICE)
+            acc = y2[u][:].rearrange("p (s q) -> p s q", q=SLICE)
+            mac(acc[:, :, 16:256], src[:, :, 0:240], coef(1, 0, t))
+            mac(acc[:, :, 0:240], src[:, :, 16:256], coef(1, 2, t))
+
+        def a_d(u):
+            s, t = divmod(u, 4)
+            if t == 0:
+                e = ep.tile([P, 4, SLAB], F32, name="ee")
+                ee[s] = e
+            scale_copy(ee[s][:, t, :], y2[u][:], coef(2, 1, t))
+
+        def v_d(u):
+            s, t = divmod(u, 4)
+            src = y2[u][:].rearrange("p (q d) -> p q d", d=16)
+            acc = ee[s][:, t, :].rearrange("p (q d) -> p q d", d=16)
+            mac(acc[:, :, 1:16], src[:, :, 0:15], coef(2, 0, t))
+            mac(acc[:, :, 0:15], src[:, :, 1:16], coef(2, 2, t))
+
+        def regroup_y(s, half):
+            g = ygp.tile([P, HALF, 4], BF16, align_bytes=64, name="yg")
+            src = ee[s][:, :, half * HALF : (half + 1) * HALF].rearrange("p t (c i) -> p c t i", i=4)
+            nc.scalar.copy(out=g[:].rearrange("p (c i) t -> p c t i", i=4), in_=src)
+            yg[(s, half)] = g
+
+        def quant_y(s, half):
+            q = yqp.tile([P, HALF], U32, align_bytes=64, name="yq")
+            sc = yqp.tile([P, HALF], U8, align_bytes=64, name="ys")
+            nc.vector.quantize_mx(
+                out=q[:].bitcast(FP8X4), scales=sc[:], in_=yg[(s, half)][:].rearrange("p w j -> p (w j)")
+            )
+            yq[(s, half)] = q
+            ys[(s, half)] = sc
+
+        def mm2(s, half):
+            banks = []
+            for ot in range(2):
+                bank = pop.tile([P, HALF], F32, name="po")
+                nc.tensor.matmul_mx(
+                    out=bank[:],
+                    lhsT=vq[:, ot * P : (ot + 1) * P].bitcast(FP8X4),
+                    lhsT_scale=vs[:, ot * P : (ot + 1) * P],
+                    rhs=yq[(s, half)][:].bitcast(FP8X4),
+                    rhs_scale=ys[(s, half)][:],
+                    start=True,
+                    stop=True,
+                )
+                banks.append(bank)
+            po[(s, half)] = banks
+
+        def evac(s, half):
+            b, sl = divmod(s, 4)
+            p0 = sl * SLAB + half * HALF
+            for ot in range(2):
+                o = osp.tile([P, HALF], F32, name="osb")
+                nc.scalar.activation(
+                    out=o[:], in_=po[(s, half)][ot][:], func=ACTF.Identity, bias=bias_f[:, ot : ot + 1], scale=1.0
+                )
+                nc.sync.dma_start(out=ov[b][ot * P : (ot + 1) * P, p0 : p0 + HALF], in_=o[:])
+
+        nc.sync.dma_start(out=w_raw[:], in_=U_c_in.rearrange("(p j) r -> p j r", j=4))
+        load_raw(0)
+        nc.sync.dma_start(out=cb_h[:], in_=U_kh.rearrange("k (m t) -> m k t", t=4))
+        nc.sync.dma_start(out=cb_w[:], in_=U_kw.rearrange("k (m t) -> m k t", t=4))
+        nc.sync.dma_start(out=cb_d[:], in_=U_kd.rearrange("k (m t) -> m k t", t=4))
+        load_raw(1)
+        nc.sync.dma_start(out=v_raw[:], in_=U_c_out.rearrange("(p j) o -> p j o", j=4))
+        with nc.allow_non_contiguous_dma(reason="256 bias values, one per partition and output tile"):
+            nc.sync.dma_start(out=bias_b[:], in_=bias.rearrange("(j p) -> p j", p=P))
+        load_raw(2)
+
+        nc.vector.tensor_copy(
+            out=w_grp[:].rearrange("p (t m) j -> p t m j", t=4),
+            in_=w_raw[:].rearrange("p j (m t) -> p t m j", t=4),
+        )
+        regroup_x(0, 0, True)
+        regroup_x(0, 1, False)
+        regroup_x(1, 0, False)
+        regroup_x(1, 1, False)
+        nc.vector.quantize_mx(out=wq[:].bitcast(FP8X4), scales=ws[:], in_=w_grp[:].rearrange("p r j -> p (r j)"))
+        quant_x(0, 0)
+        nc.vector.tensor_copy(out=cf[:, 0, :, :], in_=cb_h[:])
+        nc.vector.tensor_copy(out=cf[:, 1, :, :], in_=cb_w[:])
+        nc.vector.tensor_copy(out=cf[:, 2, :, :], in_=cb_d[:])
+        quant_x(0, 1)
+        nc.vector.tensor_copy(out=v_grp[:], in_=v_raw[:].rearrange("p j o -> p o j"))
+        quant_x(1, 0)
+        nc.vector.tensor_copy(out=bias_f[:], in_=bias_b[:])
+        nc.vector.quantize_mx(out=vq[:].bitcast(FP8X4), scales=vs[:], in_=v_grp[:].rearrange("p o j -> p (o j)"))
+        quant_x(1, 1)
+
+        for i in range(-1, N_UNITS + 6):
+            s, j = divmod(i, 4)
+            if j == 0 and s >= 0 and s + 3 < N_SLABS:
+                load_raw(s + 3)
+            if 0 <= i + 1 < N_UNITS:
+                mm1(i + 1)
+            if j == 0 and 0 <= s - 2 < N_SLABS:
+                mm2(s - 2, 0)
+            if j == 1 and 0 <= s - 2 < N_SLABS:
+                mm2(s - 2, 1)
+            if 0 <= i < N_UNITS:
+                a_h(i)
+            if 0 <= i - 1 < N_UNITS:
+                a_w(i - 1)
+            if 0 <= i - 2 < N_UNITS:
+                a_d(i - 2)
+            if j < 2 and i >= 0 and s + 2 < N_SLABS:
+                regroup_x(s + 2, j, False)
+            if j < 2 and 0 <= s - 2 < N_SLABS:
+                evac(s - 2, j)
+            if j >= 2 and 0 <= s - 1 < N_SLABS:
+                regroup_y(s - 1, j - 2)
+            if 0 <= i < N_UNITS:
+                v_h(i)
+            if 0 <= i - 1 < N_UNITS:
+                v_w(i - 1)
+            if 0 <= i - 2 < N_UNITS:
+                v_d(i - 2)
+            if j == 0 and 0 <= s - 2 < N_SLABS:
+                quant_y(s - 2, 1)
+            if j == 1 and i >= 0 and s + 2 < N_SLABS:
+                quant_x(s + 2, 0)
+            if j == 2 and i >= 0 and s + 2 < N_SLABS:
+                quant_x(s + 2, 1)
+            if j == 3 and 0 <= s - 1 < N_SLABS:
+                quant_y(s - 1, 0)

@@ -28,7 +28,8 @@ def tile_lowrankconv3d_t_kernel(tc, x, U_kh, U_kw, U_kd, U_c_in, U_c_out, bias, 
     with ExitStack() as ctx:
         const = ctx.enter_context(tc.tile_pool(name="const", bufs=1))
         rawp = ctx.enter_context(tc.tile_pool(name="rawp", bufs=3))
-        xgp = ctx.enter_context(tc.tile_pool(name="xgp", bufs=3))
+        xgp = ctx.enter_context(tc.tile_pool(name="xgp", bufs=1))
+        xg0p = ctx.enter_context(tc.tile_pool(name="xg0p", bufs=6))
         y1p = ctx.enter_context(tc.tile_pool(name="y1p", bufs=3))
         y2p = ctx.enter_context(tc.tile_pool(name="y2p", bufs=3))
         ep = ctx.enter_context(tc.tile_pool(name="ep", bufs=2))
@@ -70,28 +71,38 @@ def tile_lowrankconv3d_t_kernel(tc, x, U_kh, U_kw, U_kd, U_c_in, U_c_out, bias, 
         def coef(f, k, t):
             return cf[:, f, k, t : t + 1]
 
-        def load_raw(s):
+        def load_raw(s, pieces):
             b, sl = divmod(s, 4)
             r = rawp.tile([P, 4, SLAB], BF16, name="raw")
-            nc.sync.dma_start(out=r[:], in_=xv[b][:, :, sl * SLAB : (sl + 1) * SLAB])
+            w = SLAB // pieces
+            for k in range(pieces):
+                nc.sync.dma_start(
+                    out=r[:, :, k * w : (k + 1) * w], in_=xv[b][:, :, sl * SLAB + k * w : sl * SLAB + (k + 1) * w]
+                )
             raw[s] = r
 
-        def regroup_x(s, half, on_vector):
-            g = xgp.tile([P, HALF, 4], BF16, align_bytes=64, name="xg")
-            src = raw[s][:, :, half * HALF : (half + 1) * HALF].rearrange("p t (c i) -> p c t i", i=4)
-            dst = g[:].rearrange("p (c i) t -> p c t i", i=4)
-            if on_vector:
-                nc.vector.tensor_copy(out=dst, in_=src)
+        def regroup_x(n, eng):
+            s, q = divmod(n, 4)
+            if eng == "g1":
+                g = xgp.tile([P, SLICE, 4], BF16, align_bytes=64, name="xg")
             else:
+                g = xg0p.tile([P, SLICE, 4], BF16, align_bytes=64, name="xg0")
+            src = raw[s][:, :, q * SLICE : (q + 1) * SLICE].rearrange("p t (c i) -> p c t i", i=4)
+            dst = g[:].rearrange("p (c i) t -> p c t i", i=4)
+            if eng == "v":
+                nc.vector.tensor_copy(out=dst, in_=src)
+            elif eng == "a":
                 nc.scalar.copy(out=dst, in_=src)
-            xg[(s, half)] = g
+            else:
+                nc.gpsimd.tensor_scalar(out=dst, in0=src, scalar1=1.0, scalar2=0.0, op0=ALU.mult, op1=ALU.add)
+            xg[n] = g
 
-        def quant_x(s, half):
-            c0 = s * SLAB + half * HALF
+        def quant_x(n):
+            c0 = n * SLICE
             nc.vector.quantize_mx(
-                out=xq[:, c0 : c0 + HALF].bitcast(FP8X4),
-                scales=xs[:, c0 : c0 + HALF],
-                in_=xg[(s, half)][:].rearrange("p w j -> p (w j)"),
+                out=xq[:, c0 : c0 + SLICE].bitcast(FP8X4),
+                scales=xs[:, c0 : c0 + SLICE],
+                in_=xg[n][:].rearrange("p w j -> p (w j)"),
             )
 
         def mm1(u):
@@ -159,12 +170,14 @@ def tile_lowrankconv3d_t_kernel(tc, x, U_kh, U_kw, U_kd, U_c_in, U_c_out, bias, 
             scale_copy(a[:], y1[u][:], coef(1, 1, u % 4))
             y2[u] = a
 
-        def v_w(u):
+        def v_w(u, k):
             t = u % 4
             src = y1[u][:].rearrange("p (s q) -> p s q", q=SLICE)
             acc = y2[u][:].rearrange("p (s q) -> p s q", q=SLICE)
-            mac(acc[:, :, 16:256], src[:, :, 0:240], coef(1, 0, t))
-            mac(acc[:, :, 0:240], src[:, :, 16:256], coef(1, 2, t))
+            if k == 0:
+                mac(acc[:, :, 16:256], src[:, :, 0:240], coef(1, 0, t))
+            else:
+                mac(acc[:, :, 0:240], src[:, :, 16:256], coef(1, 2, t))
 
         def a_d(u):
             s, t = divmod(u, 4)
@@ -173,18 +186,28 @@ def tile_lowrankconv3d_t_kernel(tc, x, U_kh, U_kw, U_kd, U_c_in, U_c_out, bias, 
                 ee[s] = e
             scale_copy(ee[s][:, t, :], y2[u][:], coef(2, 1, t))
 
-        def v_d(u):
+        def v_d(u, k):
             s, t = divmod(u, 4)
             src = y2[u][:].rearrange("p (q d) -> p q d", d=16)
             acc = ee[s][:, t, :].rearrange("p (q d) -> p q d", d=16)
-            mac(acc[:, :, 1:16], src[:, :, 0:15], coef(2, 0, t))
-            mac(acc[:, :, 0:15], src[:, :, 1:16], coef(2, 2, t))
+            if k == 0:
+                mac(acc[:, :, 1:16], src[:, :, 0:15], coef(2, 0, t))
+            else:
+                mac(acc[:, :, 0:15], src[:, :, 1:16], coef(2, 2, t))
 
-        def regroup_y(s, half):
-            g = ygp.tile([P, HALF, 4], BF16, align_bytes=64, name="yg")
-            src = ee[s][:, :, half * HALF : (half + 1) * HALF].rearrange("p t (c i) -> p c t i", i=4)
-            nc.scalar.copy(out=g[:].rearrange("p (c i) t -> p c t i", i=4), in_=src)
-            yg[(s, half)] = g
+        def regroup_y(s, half, first, count, eng):
+            if first == 0:
+                g = ygp.tile([P, HALF, 4], BF16, align_bytes=64, name="yg")
+                yg[(s, half)] = g
+            g = yg[(s, half)]
+            lo = first * SLICE
+            hi = lo + count * SLICE
+            src = ee[s][:, :, half * HALF + lo : half * HALF + hi].rearrange("p t (c i) -> p c t i", i=4)
+            dst = g[:, lo:hi, :].rearrange("p (c i) t -> p c t i", i=4)
+            if eng == "v":
+                nc.vector.tensor_copy(out=dst, in_=src)
+            else:
+                nc.scalar.copy(out=dst, in_=src)
 
         def quant_y(s, half):
             q = yqp.tile([P, HALF], U32, align_bytes=64, name="yq")
@@ -195,10 +218,13 @@ def tile_lowrankconv3d_t_kernel(tc, x, U_kh, U_kw, U_kd, U_c_in, U_c_out, bias, 
             yq[(s, half)] = q
             ys[(s, half)] = sc
 
-        def mm2(s, half):
+        def mm2(s, half, spare_banks):
             banks = []
             for ot in range(2):
-                bank = pop.tile([P, HALF], F32, name="po")
+                if spare_banks:
+                    bank = pyp.tile([P, HALF], F32, name="pb")
+                else:
+                    bank = pop.tile([P, HALF], F32, name="po")
                 nc.tensor.matmul_mx(
                     out=bank[:],
                     lhsT=vq[:, ot * P : (ot + 1) * P].bitcast(FP8X4),
@@ -211,80 +237,96 @@ def tile_lowrankconv3d_t_kernel(tc, x, U_kh, U_kw, U_kd, U_c_in, U_c_out, bias, 
                 banks.append(bank)
             po[(s, half)] = banks
 
-        def evac(s, half):
+        def evac(s, half, share):
             b, sl = divmod(s, 4)
             p0 = sl * SLAB + half * HALF
             for ot in range(2):
                 o = osp.tile([P, HALF], F32, name="osb")
-                nc.scalar.activation(
-                    out=o[:], in_=po[(s, half)][ot][:], func=ACTF.Identity, bias=bias_f[:, ot : ot + 1], scale=1.0
-                )
+                if share and ot == 1:
+                    nc.vector.tensor_scalar_add(out=o[:], in0=po[(s, half)][ot][:], scalar1=bias_f[:, ot : ot + 1])
+                else:
+                    nc.scalar.activation(
+                        out=o[:], in_=po[(s, half)][ot][:], func=ACTF.Identity, bias=bias_f[:, ot : ot + 1], scale=1.0
+                    )
                 nc.sync.dma_start(out=ov[b][ot * P : (ot + 1) * P, p0 : p0 + HALF], in_=o[:])
 
+        nc.scalar.dma_start(out=cb_h[:], in_=U_kh.rearrange("k (m t) -> m k t", t=4))
+        nc.scalar.dma_start(out=cb_w[:], in_=U_kw.rearrange("k (m t) -> m k t", t=4))
+        nc.scalar.dma_start(out=cb_d[:], in_=U_kd.rearrange("k (m t) -> m k t", t=4))
         nc.sync.dma_start(out=w_raw[:], in_=U_c_in.rearrange("(p j) r -> p j r", j=4))
-        load_raw(0)
-        nc.sync.dma_start(out=cb_h[:], in_=U_kh.rearrange("k (m t) -> m k t", t=4))
-        nc.sync.dma_start(out=cb_w[:], in_=U_kw.rearrange("k (m t) -> m k t", t=4))
-        nc.sync.dma_start(out=cb_d[:], in_=U_kd.rearrange("k (m t) -> m k t", t=4))
-        load_raw(1)
-        nc.sync.dma_start(out=v_raw[:], in_=U_c_out.rearrange("(p j) o -> p j o", j=4))
+        load_raw(0, 2)
+        load_raw(1, 2)
         with nc.allow_non_contiguous_dma(reason="256 bias values, one per partition and output tile"):
-            nc.sync.dma_start(out=bias_b[:], in_=bias.rearrange("(j p) -> p j", p=P))
-        load_raw(2)
+            nc.scalar.dma_start(out=bias_b[:], in_=bias.rearrange("(j p) -> p j", p=P))
+        nc.scalar.dma_start(out=v_raw[:], in_=U_c_out.rearrange("(p j) o -> p j o", j=4))
+        load_raw(2, 1)
 
+        nc.vector.tensor_copy(out=cf[:, 0, :, :], in_=cb_h[:])
+        nc.vector.tensor_copy(out=cf[:, 1, :, :], in_=cb_w[:])
+        nc.vector.tensor_copy(out=cf[:, 2, :, :], in_=cb_d[:])
         nc.vector.tensor_copy(
             out=w_grp[:].rearrange("p (t m) j -> p t m j", t=4),
             in_=w_raw[:].rearrange("p j (m t) -> p t m j", t=4),
         )
-        regroup_x(0, 0, True)
-        regroup_x(0, 1, False)
-        regroup_x(1, 0, False)
-        regroup_x(1, 1, False)
+        regroup_x(0, "a")
+        regroup_x(1, "v")
+        regroup_x(2, "a")
         nc.vector.quantize_mx(out=wq[:].bitcast(FP8X4), scales=ws[:], in_=w_grp[:].rearrange("p r j -> p (r j)"))
-        quant_x(0, 0)
-        nc.vector.tensor_copy(out=cf[:, 0, :, :], in_=cb_h[:])
-        nc.vector.tensor_copy(out=cf[:, 1, :, :], in_=cb_w[:])
-        nc.vector.tensor_copy(out=cf[:, 2, :, :], in_=cb_d[:])
-        quant_x(0, 1)
+        quant_x(0)
+        regroup_x(3, "v")
+        regroup_x(4, "a")
+        quant_x(1)
+        quant_x(2)
+        regroup_x(5, "g0")
+        quant_x(3)
+        quant_x(4)
         nc.vector.tensor_copy(out=v_grp[:], in_=v_raw[:].rearrange("p j o -> p o j"))
-        quant_x(1, 0)
         nc.vector.tensor_copy(out=bias_f[:], in_=bias_b[:])
+        quant_x(5)
         nc.vector.quantize_mx(out=vq[:].bitcast(FP8X4), scales=vs[:], in_=v_grp[:].rearrange("p o j -> p (o j)"))
-        quant_x(1, 1)
 
-        for i in range(-1, N_UNITS + 6):
+        last = N_SLABS - 1
+        for i in range(-1, N_UNITS + 2):
             s, j = divmod(i, 4)
             if j == 0 and s >= 0 and s + 3 < N_SLABS:
-                load_raw(s + 3)
+                load_raw(s + 3, 1)
             if 0 <= i + 1 < N_UNITS:
                 mm1(i + 1)
-            if j == 0 and 0 <= s - 2 < N_SLABS:
-                mm2(s - 2, 0)
-            if j == 1 and 0 <= s - 2 < N_SLABS:
-                mm2(s - 2, 1)
+            if j < 2 and 0 <= s - 2 < last:
+                mm2(s - 2, j, False)
+            if i >= 0 and i + 6 < 32:
+                regroup_x(i + 6, "g1")
             if 0 <= i < N_UNITS:
                 a_h(i)
             if 0 <= i - 1 < N_UNITS:
                 a_w(i - 1)
+            if j < 2 and 0 <= s - 2 < last:
+                evac(s - 2, j, False)
+            if j >= 2 and 0 <= s - 1 < last:
+                regroup_y(s - 1, j - 2, 0, 2, "a")
             if 0 <= i - 2 < N_UNITS:
                 a_d(i - 2)
-            if j < 2 and i >= 0 and s + 2 < N_SLABS:
-                regroup_x(s + 2, j, False)
-            if j < 2 and 0 <= s - 2 < N_SLABS:
-                evac(s - 2, j)
-            if j >= 2 and 0 <= s - 1 < N_SLABS:
-                regroup_y(s - 1, j - 2)
             if 0 <= i < N_UNITS:
                 v_h(i)
-            if 0 <= i - 1 < N_UNITS:
-                v_w(i - 1)
-            if 0 <= i - 2 < N_UNITS:
-                v_d(i - 2)
-            if j == 0 and 0 <= s - 2 < N_SLABS:
+            for k in (0, 2):
+                if 0 <= i - 1 < N_UNITS:
+                    v_w(i - 1, k)
+                if 0 <= i - 2 < N_UNITS:
+                    v_d(i - 2, k)
+            if j == 0 and 0 <= s - 2 < last:
                 quant_y(s - 2, 1)
-            if j == 1 and i >= 0 and s + 2 < N_SLABS:
-                quant_x(s + 2, 0)
-            if j == 2 and i >= 0 and s + 2 < N_SLABS:
-                quant_x(s + 2, 1)
-            if j == 3 and 0 <= s - 1 < N_SLABS:
+            if j == 3 and 0 <= s - 1 < last:
                 quant_y(s - 1, 0)
+            if i >= 0 and i + 6 < 32:
+                quant_x(i + 6)
+
+        regroup_y(last, 0, 0, 1, "v")
+        regroup_y(last, 0, 1, 1, "a")
+        regroup_y(last, 1, 0, 1, "a")
+        regroup_y(last, 1, 1, 1, "v")
+        quant_y(last, 0)
+        quant_y(last, 1)
+        mm2(last, 0, False)
+        mm2(last, 1, True)
+        evac(last, 0, True)
+        evac(last, 1, True)

@@ -18,6 +18,7 @@ SLAB = 1024
 HALF = 512
 N_SLABS = 8
 N_UNITS = 32
+G_UNITS = 30
 
 
 def tile_lowrankconv3d_t_kernel(tc, x, U_kh, U_kw, U_kd, U_c_in, U_c_out, bias, out):
@@ -28,8 +29,9 @@ def tile_lowrankconv3d_t_kernel(tc, x, U_kh, U_kw, U_kd, U_c_in, U_c_out, bias, 
     with ExitStack() as ctx:
         const = ctx.enter_context(tc.tile_pool(name="const", bufs=1))
         rawp = ctx.enter_context(tc.tile_pool(name="rawp", bufs=3))
-        xgp = ctx.enter_context(tc.tile_pool(name="xgp", bufs=1))
-        xg0p = ctx.enter_context(tc.tile_pool(name="xg0p", bufs=6))
+        xgp = ctx.enter_context(tc.tile_pool(name="xgp", bufs=3))
+        xg0p = ctx.enter_context(tc.tile_pool(name="xg0p", bufs=7))
+        pdp = ctx.enter_context(tc.tile_pool(name="pdp", bufs=2))
         y1p = ctx.enter_context(tc.tile_pool(name="y1p", bufs=3))
         y2p = ctx.enter_context(tc.tile_pool(name="y2p", bufs=3))
         ep = ctx.enter_context(tc.tile_pool(name="ep", bufs=2))
@@ -67,6 +69,7 @@ def tile_lowrankconv3d_t_kernel(tc, x, U_kh, U_kw, U_kd, U_c_in, U_c_out, bias, 
         yq = {}
         ys = {}
         po = {}
+        pd = {}
 
         def coef(f, k, t):
             return cf[:, f, k, t : t + 1]
@@ -81,20 +84,18 @@ def tile_lowrankconv3d_t_kernel(tc, x, U_kh, U_kw, U_kd, U_c_in, U_c_out, bias, 
                 )
             raw[s] = r
 
-        def regroup_x(n, eng):
+        def regroup_x(n, eng, early):
             s, q = divmod(n, 4)
-            if eng == "g1":
-                g = xgp.tile([P, SLICE, 4], BF16, align_bytes=64, name="xg")
-            else:
+            if early:
                 g = xg0p.tile([P, SLICE, 4], BF16, align_bytes=64, name="xg0")
+            else:
+                g = xgp.tile([P, SLICE, 4], BF16, align_bytes=64, name="xg")
             src = raw[s][:, :, q * SLICE : (q + 1) * SLICE].rearrange("p t (c i) -> p c t i", i=4)
             dst = g[:].rearrange("p (c i) t -> p c t i", i=4)
             if eng == "v":
                 nc.vector.tensor_copy(out=dst, in_=src)
-            elif eng == "a":
-                nc.scalar.copy(out=dst, in_=src)
             else:
-                nc.gpsimd.tensor_scalar(out=dst, in0=src, scalar1=1.0, scalar2=0.0, op0=ALU.mult, op1=ALU.add)
+                nc.scalar.copy(out=dst, in_=src)
             xg[n] = g
 
         def quant_x(n):
@@ -186,6 +187,18 @@ def tile_lowrankconv3d_t_kernel(tc, x, U_kh, U_kw, U_kd, U_c_in, U_c_out, bias, 
                 ee[s] = e
             scale_copy(ee[s][:, t, :], y2[u][:], coef(2, 1, t))
 
+        def a_d2(u):
+            t = u % 4
+            pr = pdp.tile([P, 64, 16], F32, name="pd")
+            src = y2[u][:].rearrange("p (q d) -> p q d", d=16)
+            scale_copy(pr[:, :, 0:15], src[:, :, 1:16], coef(2, 2, t))
+            pd[u] = pr
+
+        def g_d2(u):
+            s, t = divmod(u, 4)
+            acc = ee[s][:, t, :].rearrange("p (q d) -> p q d", d=16)
+            nc.gpsimd.tensor_tensor(out=acc[:, :, 0:15], in0=acc[:, :, 0:15], in1=pd[u][:, :, 0:15], op=ALU.add)
+
         def v_d(u, k):
             s, t = divmod(u, 4)
             src = y2[u][:].rearrange("p (q d) -> p q d", d=16)
@@ -250,6 +263,19 @@ def tile_lowrankconv3d_t_kernel(tc, x, U_kh, U_kw, U_kd, U_c_in, U_c_out, bias, 
                     )
                 nc.sync.dma_start(out=ov[b][ot * P : (ot + 1) * P, p0 : p0 + HALF], in_=o[:])
 
+        def regroup_w(t):
+            nc.vector.tensor_copy(
+                out=w_grp[:, t * P : (t + 1) * P, :],
+                in_=w_raw[:].rearrange("p j (m t) -> p t m j", t=4)[:, t, :, :],
+            )
+
+        def quant_w(t):
+            nc.vector.quantize_mx(
+                out=wq[:, t * P : (t + 1) * P].bitcast(FP8X4),
+                scales=ws[:, t * P : (t + 1) * P],
+                in_=w_grp[:, t * P : (t + 1) * P, :].rearrange("p r j -> p (r j)"),
+            )
+
         nc.scalar.dma_start(out=cb_h[:], in_=U_kh.rearrange("k (m t) -> m k t", t=4))
         nc.scalar.dma_start(out=cb_w[:], in_=U_kw.rearrange("k (m t) -> m k t", t=4))
         nc.scalar.dma_start(out=cb_d[:], in_=U_kd.rearrange("k (m t) -> m k t", t=4))
@@ -264,26 +290,20 @@ def tile_lowrankconv3d_t_kernel(tc, x, U_kh, U_kw, U_kd, U_c_in, U_c_out, bias, 
         nc.vector.tensor_copy(out=cf[:, 0, :, :], in_=cb_h[:])
         nc.vector.tensor_copy(out=cf[:, 1, :, :], in_=cb_w[:])
         nc.vector.tensor_copy(out=cf[:, 2, :, :], in_=cb_d[:])
-        nc.vector.tensor_copy(
-            out=w_grp[:].rearrange("p (t m) j -> p t m j", t=4),
-            in_=w_raw[:].rearrange("p j (m t) -> p t m j", t=4),
-        )
-        regroup_x(0, "a")
-        regroup_x(1, "v")
-        regroup_x(2, "a")
-        nc.vector.quantize_mx(out=wq[:].bitcast(FP8X4), scales=ws[:], in_=w_grp[:].rearrange("p r j -> p (r j)"))
+        regroup_w(0)
+        regroup_x(0, "a", True)
+        regroup_x(1, "v", True)
+        regroup_x(2, "a", True)
+        quant_w(0)
         quant_x(0)
-        regroup_x(3, "v")
-        regroup_x(4, "a")
+        regroup_x(3, "v", True)
         quant_x(1)
+        regroup_x(4, "a", True)
+        regroup_w(1)
         quant_x(2)
-        regroup_x(5, "g0")
         quant_x(3)
+        quant_w(1)
         quant_x(4)
-        nc.vector.tensor_copy(out=v_grp[:], in_=v_raw[:].rearrange("p j o -> p o j"))
-        nc.vector.tensor_copy(out=bias_f[:], in_=bias_b[:])
-        quant_x(5)
-        nc.vector.quantize_mx(out=vq[:].bitcast(FP8X4), scales=vs[:], in_=v_grp[:].rearrange("p o j -> p (o j)"))
 
         last = N_SLABS - 1
         for i in range(-1, N_UNITS + 2):
@@ -294,8 +314,6 @@ def tile_lowrankconv3d_t_kernel(tc, x, U_kh, U_kw, U_kd, U_c_in, U_c_out, bias, 
                 mm1(i + 1)
             if j < 2 and 0 <= s - 2 < last:
                 mm2(s - 2, j, False)
-            if i >= 0 and i + 6 < 32:
-                regroup_x(i + 6, "g1")
             if 0 <= i < N_UNITS:
                 a_h(i)
             if 0 <= i - 1 < N_UNITS:
@@ -304,21 +322,46 @@ def tile_lowrankconv3d_t_kernel(tc, x, U_kh, U_kw, U_kd, U_c_in, U_c_out, bias, 
                 evac(s - 2, j, False)
             if j >= 2 and 0 <= s - 1 < last:
                 regroup_y(s - 1, j - 2, 0, 2, "a")
+            if j == 0 and i >= 0 and i + 7 < 32:
+                regroup_x(i + 7, "a", False)
             if 0 <= i - 2 < N_UNITS:
                 a_d(i - 2)
+            if 0 <= i - 2 < G_UNITS:
+                a_d2(i - 2)
             if 0 <= i < N_UNITS:
                 v_h(i)
-            for k in (0, 2):
-                if 0 <= i - 1 < N_UNITS:
-                    v_w(i - 1, k)
-                if 0 <= i - 2 < N_UNITS:
-                    v_d(i - 2, k)
+            if 0 <= i - 1 < N_UNITS:
+                v_w(i - 1, 0)
+            if i == -1:
+                regroup_w(2)
+                regroup_w(3)
+                quant_w(2)
+                nc.vector.tensor_copy(out=v_grp[:], in_=v_raw[:].rearrange("p j o -> p o j"))
+                quant_w(3)
+                nc.vector.tensor_copy(out=bias_f[:], in_=bias_b[:])
+                nc.vector.quantize_mx(
+                    out=vq[:].bitcast(FP8X4), scales=vs[:], in_=v_grp[:].rearrange("p o j -> p (o j)")
+                )
+            if i == 0:
+                regroup_x(5, "v", True)
+                regroup_x(6, "v", True)
+                quant_x(5)
+            if j != 0 and i >= 0 and i + 7 < 32:
+                regroup_x(i + 7, "v", False)
             if j == 0 and 0 <= s - 2 < last:
                 quant_y(s - 2, 1)
             if j == 3 and 0 <= s - 1 < last:
                 quant_y(s - 1, 0)
             if i >= 0 and i + 6 < 32:
                 quant_x(i + 6)
+            if 0 <= i - 1 < N_UNITS:
+                v_w(i - 1, 2)
+            if 0 <= i - 2 < N_UNITS:
+                v_d(i - 2, 0)
+            if G_UNITS <= i - 2 < N_UNITS:
+                v_d(i - 2, 2)
+            if 0 <= i - 2 < G_UNITS:
+                g_d2(i - 2)
 
         regroup_y(last, 0, 0, 1, "v")
         regroup_y(last, 0, 1, 1, "a")

@@ -74,7 +74,7 @@ def tile_lowrankconv3d_t_kernel(tc, x, U_kh, U_kw, U_kd, U_c_in, U_c_out, bias, 
         def coef(f, k, t):
             return cf[:, f, k, t : t + 1]
 
-        def load_raw(s, pieces):
+        def load_raw(s, pieces, weights_second):
             b, sl = divmod(s, 4)
             r = rawp.tile([P, 4, SLAB], BF16, name="raw")
             w = SLAB // pieces
@@ -82,6 +82,8 @@ def tile_lowrankconv3d_t_kernel(tc, x, U_kh, U_kw, U_kd, U_c_in, U_c_out, bias, 
                 nc.sync.dma_start(
                     out=r[:, :, k * w : (k + 1) * w], in_=xv[b][:, :, sl * SLAB + k * w : sl * SLAB + (k + 1) * w]
                 )
+                if weights_second and k == 0:
+                    nc.sync.dma_start(out=w_raw[:], in_=U_c_in.rearrange("(p j) r -> p j r", j=4))
             raw[s] = r
 
         def regroup_x(n, eng, early):
@@ -279,37 +281,36 @@ def tile_lowrankconv3d_t_kernel(tc, x, U_kh, U_kw, U_kd, U_c_in, U_c_out, bias, 
         nc.scalar.dma_start(out=cb_h[:], in_=U_kh.rearrange("k (m t) -> m k t", t=4))
         nc.scalar.dma_start(out=cb_w[:], in_=U_kw.rearrange("k (m t) -> m k t", t=4))
         nc.scalar.dma_start(out=cb_d[:], in_=U_kd.rearrange("k (m t) -> m k t", t=4))
-        nc.sync.dma_start(out=w_raw[:], in_=U_c_in.rearrange("(p j) r -> p j r", j=4))
-        load_raw(0, 2)
-        load_raw(1, 2)
+        load_raw(0, 2, True)
+        load_raw(1, 2, False)
         with nc.allow_non_contiguous_dma(reason="256 bias values, one per partition and output tile"):
             nc.scalar.dma_start(out=bias_b[:], in_=bias.rearrange("(j p) -> p j", p=P))
         nc.scalar.dma_start(out=v_raw[:], in_=U_c_out.rearrange("(p j) o -> p j o", j=4))
-        load_raw(2, 1)
+        load_raw(2, 1, False)
 
+        regroup_x(0, "v", True)
+        regroup_x(1, "a", True)
+        regroup_w(0)
+        quant_x(0)
+        quant_w(0)
+        quant_x(1)
+        regroup_x(2, "v", True)
+        regroup_x(3, "a", True)
         nc.vector.tensor_copy(out=cf[:, 0, :, :], in_=cb_h[:])
         nc.vector.tensor_copy(out=cf[:, 1, :, :], in_=cb_w[:])
         nc.vector.tensor_copy(out=cf[:, 2, :, :], in_=cb_d[:])
-        regroup_w(0)
-        regroup_x(0, "a", True)
-        regroup_x(1, "v", True)
-        regroup_x(2, "a", True)
-        quant_w(0)
-        quant_x(0)
-        regroup_x(3, "v", True)
-        quant_x(1)
-        regroup_x(4, "a", True)
-        regroup_w(1)
         quant_x(2)
         quant_x(3)
-        quant_w(1)
+        regroup_x(4, "v", True)
+        regroup_w(1)
         quant_x(4)
+        quant_w(1)
 
         last = N_SLABS - 1
         for i in range(-1, N_UNITS + 2):
             s, j = divmod(i, 4)
             if j == 0 and s >= 0 and s + 3 < N_SLABS:
-                load_raw(s + 3, 1)
+                load_raw(s + 3, 1, False)
             if 0 <= i + 1 < N_UNITS:
                 mm1(i + 1)
             if j < 2 and 0 <= s - 2 < last:
@@ -322,8 +323,6 @@ def tile_lowrankconv3d_t_kernel(tc, x, U_kh, U_kw, U_kd, U_c_in, U_c_out, bias, 
                 evac(s - 2, j, False)
             if j >= 2 and 0 <= s - 1 < last:
                 regroup_y(s - 1, j - 2, 0, 2, "a")
-            if j == 0 and i >= 0 and i + 7 < 32:
-                regroup_x(i + 7, "a", False)
             if 0 <= i - 2 < N_UNITS:
                 a_d(i - 2)
             if 0 <= i - 2 < G_UNITS:
@@ -346,7 +345,7 @@ def tile_lowrankconv3d_t_kernel(tc, x, U_kh, U_kw, U_kd, U_c_in, U_c_out, bias, 
                 regroup_x(5, "v", True)
                 regroup_x(6, "v", True)
                 quant_x(5)
-            if j != 0 and i >= 0 and i + 7 < 32:
+            if i >= 0 and i + 7 < 32:
                 regroup_x(i + 7, "v", False)
             if j == 0 and 0 <= s - 2 < last:
                 quant_y(s - 2, 1)

@@ -18,7 +18,7 @@ SLAB = 1024
 HALF = 512
 N_SLABS = 8
 N_UNITS = 32
-G_UNITS = 30
+G_UNITS = 29
 
 
 def tile_lowrankconv3d_t_kernel(tc, x, U_kh, U_kw, U_kd, U_c_in, U_c_out, bias, out):
@@ -307,22 +307,26 @@ def tile_lowrankconv3d_t_kernel(tc, x, U_kh, U_kw, U_kd, U_c_in, U_c_out, bias, 
         quant_w(1)
 
         last = N_SLABS - 1
-        for i in range(-1, N_UNITS + 2):
+        for i in range(-1, N_UNITS + 3):
             s, j = divmod(i, 4)
             if j == 0 and s >= 0 and s + 3 < N_SLABS:
                 load_raw(s + 3, 1, False)
             if 0 <= i + 1 < N_UNITS:
                 mm1(i + 1)
-            if j < 2 and 0 <= s - 2 < last:
-                mm2(s - 2, j, False)
+            if j in (1, 2) and 0 <= s - 2 < last:
+                mm2(s - 2, j - 1, False)
             if 0 <= i < N_UNITS:
                 a_h(i)
             if 0 <= i - 1 < N_UNITS:
                 a_w(i - 1)
-            if j < 2 and 0 <= s - 2 < last:
-                evac(s - 2, j, False)
-            if j >= 2 and 0 <= s - 1 < last:
-                regroup_y(s - 1, j - 2, 0, 2, "a")
+            if j in (1, 2) and 0 <= s - 2 < last:
+                evac(s - 2, j - 1, False)
+            if j == 3 and 0 <= s - 1 < last:
+                regroup_y(s - 1, 0, 0, 2, "a")
+            if j == 0 and 0 <= s - 2 < last:
+                regroup_y(s - 2, 1, 0, 2, "a")
+            if j == 1 and i >= 0 and i + 7 < 32:
+                regroup_x(i + 7, "a", False)
             if 0 <= i - 2 < N_UNITS:
                 a_d(i - 2)
             if 0 <= i - 2 < G_UNITS:
@@ -345,12 +349,10 @@ def tile_lowrankconv3d_t_kernel(tc, x, U_kh, U_kw, U_kd, U_c_in, U_c_out, bias, 
                 regroup_x(5, "v", True)
                 regroup_x(6, "v", True)
                 quant_x(5)
-            if i >= 0 and i + 7 < 32:
+            if j != 1 and i >= 0 and i + 7 < 32:
                 regroup_x(i + 7, "v", False)
-            if j == 0 and 0 <= s - 2 < last:
-                quant_y(s - 2, 1)
-            if j == 3 and 0 <= s - 1 < last:
-                quant_y(s - 1, 0)
+            if j < 2 and 0 <= s - 2 < last:
+                quant_y(s - 2, j)
             if i >= 0 and i + 6 < 32:
                 quant_x(i + 6)
             if 0 <= i - 1 < N_UNITS:

@@ -30,7 +30,7 @@ def tile_lowrankconv3d_t_kernel(tc, x, U_kh, U_kw, U_kd, U_c_in, U_c_out, bias, 
         const = ctx.enter_context(tc.tile_pool(name="const", bufs=1))
         rawp = ctx.enter_context(tc.tile_pool(name="rawp", bufs=3))
         xgp = ctx.enter_context(tc.tile_pool(name="xgp", bufs=3))
-        xg0p = ctx.enter_context(tc.tile_pool(name="xg0p", bufs=7))
+        xg0p = ctx.enter_context(tc.tile_pool(name="xg0p", bufs=6))
         pdp = ctx.enter_context(tc.tile_pool(name="pdp", bufs=2))
         y1p = ctx.enter_context(tc.tile_pool(name="y1p", bufs=3))
         y2p = ctx.enter_context(tc.tile_pool(name="y2p", bufs=3))
@@ -70,6 +70,7 @@ def tile_lowrankconv3d_t_kernel(tc, x, U_kh, U_kw, U_kd, U_c_in, U_c_out, bias, 
         ys = {}
         po = {}
         pd = {}
+        xc = {}
 
         def coef(f, k, t):
             return cf[:, f, k, t : t + 1]
@@ -86,12 +87,9 @@ def tile_lowrankconv3d_t_kernel(tc, x, U_kh, U_kw, U_kd, U_c_in, U_c_out, bias, 
                     nc.sync.dma_start(out=w_raw[:], in_=U_c_in.rearrange("(p j) r -> p j r", j=4))
             raw[s] = r
 
-        def regroup_x(n, eng, early):
+        def regroup_x(n, eng):
             s, q = divmod(n, 4)
-            if early:
-                g = xg0p.tile([P, SLICE, 4], BF16, align_bytes=64, name="xg0")
-            else:
-                g = xgp.tile([P, SLICE, 4], BF16, align_bytes=64, name="xg")
+            g = xg0p.tile([P, SLICE, 4], BF16, align_bytes=64, name="xg0")
             src = raw[s][:, :, q * SLICE : (q + 1) * SLICE].rearrange("p t (c i) -> p c t i", i=4)
             dst = g[:].rearrange("p (c i) t -> p c t i", i=4)
             if eng == "v":
@@ -106,6 +104,29 @@ def tile_lowrankconv3d_t_kernel(tc, x, U_kh, U_kw, U_kd, U_c_in, U_c_out, bias, 
                 out=xq[:, c0 : c0 + SLICE].bitcast(FP8X4),
                 scales=xs[:, c0 : c0 + SLICE],
                 in_=xg[n][:].rearrange("p w j -> p (w j)"),
+            )
+
+        def regroup_c(c, first, count, eng):
+            if first == 0:
+                g = xgp.tile([P, HALF, 4], BF16, align_bytes=64, name="xc")
+                xc[c] = g
+            g = xc[c]
+            lo = first * SLICE
+            hi = lo + count * SLICE
+            base = (c % 2) * HALF
+            src = raw[c // 2][:, :, base + lo : base + hi].rearrange("p t (c i) -> p c t i", i=4)
+            dst = g[:, lo:hi, :].rearrange("p (c i) t -> p c t i", i=4)
+            if eng == "v":
+                nc.vector.tensor_copy(out=dst, in_=src)
+            else:
+                nc.scalar.copy(out=dst, in_=src)
+
+        def quant_c(c):
+            c0 = c * HALF
+            nc.vector.quantize_mx(
+                out=xq[:, c0 : c0 + HALF].bitcast(FP8X4),
+                scales=xs[:, c0 : c0 + HALF],
+                in_=xc[c][:].rearrange("p w j -> p (w j)"),
             )
 
         def mm1(u):
@@ -288,20 +309,20 @@ def tile_lowrankconv3d_t_kernel(tc, x, U_kh, U_kw, U_kd, U_c_in, U_c_out, bias, 
         nc.scalar.dma_start(out=v_raw[:], in_=U_c_out.rearrange("(p j) o -> p j o", j=4))
         load_raw(2, 1, False)
 
-        regroup_x(0, "v", True)
-        regroup_x(1, "a", True)
+        regroup_x(0, "v")
+        regroup_x(1, "a")
         regroup_w(0)
         quant_x(0)
         quant_w(0)
         quant_x(1)
-        regroup_x(2, "v", True)
-        regroup_x(3, "a", True)
+        regroup_x(2, "v")
+        regroup_x(3, "a")
         nc.vector.tensor_copy(out=cf[:, 0, :, :], in_=cb_h[:])
         nc.vector.tensor_copy(out=cf[:, 1, :, :], in_=cb_w[:])
         nc.vector.tensor_copy(out=cf[:, 2, :, :], in_=cb_d[:])
         quant_x(2)
         quant_x(3)
-        regroup_x(4, "v", True)
+        regroup_x(4, "v")
         regroup_w(1)
         quant_x(4)
         quant_w(1)
@@ -325,8 +346,10 @@ def tile_lowrankconv3d_t_kernel(tc, x, U_kh, U_kw, U_kd, U_c_in, U_c_out, bias, 
                 regroup_y(s - 1, 0, 0, 2, "a")
             if j == 0 and 0 <= s - 2 < last:
                 regroup_y(s - 2, 1, 0, 2, "a")
-            if j == 1 and i >= 0 and i + 7 < 32:
-                regroup_x(i + 7, "a", False)
+            if i in (0, 1):
+                regroup_c(4, i, 1, "a")
+            if j in (1, 2) and s >= 0 and 2 * s + 6 < 16:
+                regroup_c(2 * s + 6, j - 1, 1, "a")
             if 0 <= i - 2 < N_UNITS:
                 a_d(i - 2)
             if 0 <= i - 2 < G_UNITS:
@@ -346,15 +369,19 @@ def tile_lowrankconv3d_t_kernel(tc, x, U_kh, U_kw, U_kd, U_c_in, U_c_out, bias, 
                     out=vq[:].bitcast(FP8X4), scales=vs[:], in_=v_grp[:].rearrange("p o j -> p (o j)")
                 )
             if i == 0:
-                regroup_x(5, "v", True)
-                regroup_x(6, "v", True)
+                regroup_x(5, "v")
+            if j == 0 and s >= 0 and 2 * s + 3 < 16:
+                regroup_c(2 * s + 3, 0, 2, "v")
+            if i == 1:
                 quant_x(5)
-            if j != 1 and i >= 0 and i + 7 < 32:
-                regroup_x(i + 7, "v", False)
             if j < 2 and 0 <= s - 2 < last:
                 quant_y(s - 2, j)
-            if i >= 0 and i + 6 < 32:
-                quant_x(i + 6)
+            if i == 2:
+                quant_c(4)
+            if j == 2 and s >= 0 and 2 * s + 3 < 16:
+                quant_c(2 * s + 3)
+            if j == 3 and s >= 0 and 2 * s + 6 < 16:
+                quant_c(2 * s + 6)
             if 0 <= i - 1 < N_UNITS:
                 v_w(i - 1, 2)
             if 0 <= i - 2 < N_UNITS:

@@ -40,7 +40,6 @@ def tile_lowrankconv3d_t_kernel(tc, x, U_kh, U_kw, U_kd, U_c_in, U_c_out, bias, 
         osp = ctx.enter_context(tc.tile_pool(name="osp", bufs=4))
         pyp = ctx.enter_context(tc.psum_pool(name="pyp", bufs=6))
         pop = ctx.enter_context(tc.psum_pool(name="pop", bufs=2))
-        ctx.enter_context(tc.manual_schedule())
 
         xq = const.tile([P, N_SLABS * SLAB], U32, align_bytes=64, name="xq")
         xs = const.tile([P, N_SLABS * SLAB], U8, align_bytes=64, name="xs")

@@ -31,13 +31,13 @@ def tile_lowrankconv3d_t_kernel(tc, x, U_kh, U_kw, U_kd, U_c_in, U_c_out, bias, 
         rawp = ctx.enter_context(tc.tile_pool(name="rawp", bufs=3))
         xgp = ctx.enter_context(tc.tile_pool(name="xgp", bufs=3))
         xg0p = ctx.enter_context(tc.tile_pool(name="xg0p", bufs=6))
-        pdp = ctx.enter_context(tc.tile_pool(name="pdp", bufs=2))
-        y1p = ctx.enter_context(tc.tile_pool(name="y1p", bufs=3))
-        y2p = ctx.enter_context(tc.tile_pool(name="y2p", bufs=3))
+        pdp = ctx.enter_context(tc.tile_pool(name="pdp", bufs=3))
+        y1p = ctx.enter_context(tc.tile_pool(name="y1p", bufs=4))
+        y2p = ctx.enter_context(tc.tile_pool(name="y2p", bufs=4))
         ep = ctx.enter_context(tc.tile_pool(name="ep", bufs=2))
         ygp = ctx.enter_context(tc.tile_pool(name="ygp", bufs=2))
         yqp = ctx.enter_context(tc.tile_pool(name="yqp", bufs=2))
-        osp = ctx.enter_context(tc.tile_pool(name="osp", bufs=4))
+        osp = ctx.enter_context(tc.tile_pool(name="osp", bufs=6))
         pyp = ctx.enter_context(tc.psum_pool(name="pyp", bufs=6))
         pop = ctx.enter_context(tc.psum_pool(name="pop", bufs=2))
 
@@ -84,6 +84,7 @@ def tile_lowrankconv3d_t_kernel(tc, x, U_kh, U_kw, U_kd, U_c_in, U_c_out, bias, 
                 )
                 if weights_second and k == 0:
                     nc.sync.dma_start(out=w_raw[:], in_=U_c_in.rearrange("(p j) r -> p j r", j=4))
+                    nc.sync.dma_start(out=cb_h[:], in_=U_kh.rearrange("k (m t) -> m k t", t=4))
             raw[s] = r
 
         def regroup_x(n, eng):
@@ -106,26 +107,28 @@ def tile_lowrankconv3d_t_kernel(tc, x, U_kh, U_kw, U_kd, U_c_in, U_c_out, bias, 
             )
 
         def regroup_c(c, first, count, eng):
-            if first == 0:
-                g = xgp.tile([P, HALF, 4], BF16, align_bytes=64, name="xc")
-                xc[c] = g
-            g = xc[c]
+            pr, side = divmod(c - 3, 2)
+            if pr not in xc:
+                g = xgp.tile([P, 2 * HALF, 4], BF16, align_bytes=64, name="xc")
+                xc[pr] = g
+            g = xc[pr]
             lo = first * SLICE
             hi = lo + count * SLICE
             base = (c % 2) * HALF
             src = raw[c // 2][:, :, base + lo : base + hi].rearrange("p t (c i) -> p c t i", i=4)
-            dst = g[:, lo:hi, :].rearrange("p (c i) t -> p c t i", i=4)
+            dst = g[:, side * HALF + lo : side * HALF + hi, :].rearrange("p (c i) t -> p c t i", i=4)
             if eng == "v":
                 nc.vector.tensor_copy(out=dst, in_=src)
             else:
                 nc.scalar.copy(out=dst, in_=src)
 
-        def quant_c(c):
-            c0 = c * HALF
+        def quant_pair(pr):
+            c0 = (2 * pr + 3) * HALF
+            n = 2 * HALF if 2 * pr + 4 < 16 else HALF
             nc.vector.quantize_mx(
-                out=xq[:, c0 : c0 + HALF].bitcast(FP8X4),
-                scales=xs[:, c0 : c0 + HALF],
-                in_=xc[c][:].rearrange("p w j -> p (w j)"),
+                out=xq[:, c0 : c0 + n].bitcast(FP8X4),
+                scales=xs[:, c0 : c0 + n],
+                in_=xc[pr][:, 0:n, :].rearrange("p w j -> p (w j)"),
             )
 
         def mm1(u):
@@ -231,27 +234,32 @@ def tile_lowrankconv3d_t_kernel(tc, x, U_kh, U_kw, U_kd, U_c_in, U_c_out, bias, 
                 mac(acc[:, :, 0:15], src[:, :, 1:16], coef(2, 2, t))
 
         def regroup_y(s, half, first, count, eng):
-            if first == 0:
-                g = ygp.tile([P, HALF, 4], BF16, align_bytes=64, name="yg")
-                yg[(s, half)] = g
-            g = yg[(s, half)]
-            lo = first * SLICE
+            if s not in yg:
+                g = ygp.tile([P, SLAB, 4], BF16, align_bytes=64, name="yg")
+                yg[s] = g
+            g = yg[s]
+            lo = half * HALF + first * SLICE
             hi = lo + count * SLICE
-            src = ee[s][:, :, half * HALF + lo : half * HALF + hi].rearrange("p t (c i) -> p c t i", i=4)
+            src = ee[s][:, :, lo:hi].rearrange("p t (c i) -> p c t i", i=4)
             dst = g[:, lo:hi, :].rearrange("p (c i) t -> p c t i", i=4)
             if eng == "v":
                 nc.vector.tensor_copy(out=dst, in_=src)
             else:
                 nc.scalar.copy(out=dst, in_=src)
 
-        def quant_y(s, half):
-            q = yqp.tile([P, HALF], U32, align_bytes=64, name="yq")
-            sc = yqp.tile([P, HALF], U8, align_bytes=64, name="ys")
+        def quant_y(s, half, count):
+            if s not in yq:
+                q = yqp.tile([P, SLAB], U32, align_bytes=64, name="yq")
+                sc = yqp.tile([P, SLAB], U8, align_bytes=64, name="ys")
+                yq[s] = q
+                ys[s] = sc
+            lo = half * HALF
+            hi = lo + count * HALF
             nc.vector.quantize_mx(
-                out=q[:].bitcast(FP8X4), scales=sc[:], in_=yg[(s, half)][:].rearrange("p w j -> p (w j)")
+                out=yq[s][:, lo:hi].bitcast(FP8X4),
+                scales=ys[s][:, lo:hi],
+                in_=yg[s][:, lo:hi, :].rearrange("p w j -> p (w j)"),
             )
-            yq[(s, half)] = q
-            ys[(s, half)] = sc
 
         def mm2(s, half, spare_banks):
             banks = []
@@ -264,8 +272,8 @@ def tile_lowrankconv3d_t_kernel(tc, x, U_kh, U_kw, U_kd, U_c_in, U_c_out, bias, 
                     out=bank[:],
                     lhsT=vq[:, ot * P : (ot + 1) * P].bitcast(FP8X4),
                     lhsT_scale=vs[:, ot * P : (ot + 1) * P],
-                    rhs=yq[(s, half)][:].bitcast(FP8X4),
-                    rhs_scale=ys[(s, half)][:],
+                    rhs=yq[s][:, half * HALF : (half + 1) * HALF].bitcast(FP8X4),
+                    rhs_scale=ys[s][:, half * HALF : (half + 1) * HALF],
                     start=True,
                     stop=True,
                 )
@@ -298,11 +306,10 @@ def tile_lowrankconv3d_t_kernel(tc, x, U_kh, U_kw, U_kd, U_c_in, U_c_out, bias, 
                 in_=w_grp[:, t * P : (t + 1) * P, :].rearrange("p r j -> p (r j)"),
             )
 
-        nc.scalar.dma_start(out=cb_h[:], in_=U_kh.rearrange("k (m t) -> m k t", t=4))
-        nc.scalar.dma_start(out=cb_w[:], in_=U_kw.rearrange("k (m t) -> m k t", t=4))
-        nc.scalar.dma_start(out=cb_d[:], in_=U_kd.rearrange("k (m t) -> m k t", t=4))
         load_raw(0, 2, True)
         load_raw(1, 2, False)
+        nc.sync.dma_start(out=cb_w[:], in_=U_kw.rearrange("k (m t) -> m k t", t=4))
+        nc.sync.dma_start(out=cb_d[:], in_=U_kd.rearrange("k (m t) -> m k t", t=4))
         with nc.allow_non_contiguous_dma(reason="256 bias values, one per partition and output tile"):
             nc.scalar.dma_start(out=bias_b[:], in_=bias.rearrange("(j p) -> p j", p=P))
         nc.scalar.dma_start(out=v_raw[:], in_=U_c_out.rearrange("(p j) o -> p j o", j=4))
@@ -327,20 +334,20 @@ def tile_lowrankconv3d_t_kernel(tc, x, U_kh, U_kw, U_kd, U_c_in, U_c_out, bias, 
         quant_w(1)
 
         last = N_SLABS - 1
-        for i in range(-1, N_UNITS + 3):
+        for i in range(-1, N_UNITS + 4):
             s, j = divmod(i, 4)
             if j == 0 and s >= 0 and s + 3 < N_SLABS:
                 load_raw(s + 3, 1, False)
             if 0 <= i + 1 < N_UNITS:
                 mm1(i + 1)
-            if j in (1, 2) and 0 <= s - 2 < last:
-                mm2(s - 2, j - 1, False)
+            if j in (2, 3) and 0 <= s - 2 < last:
+                mm2(s - 2, j - 2, False)
             if 0 <= i < N_UNITS:
                 a_h(i)
             if 0 <= i - 1 < N_UNITS:
                 a_w(i - 1)
-            if j in (1, 2) and 0 <= s - 2 < last:
-                evac(s - 2, j - 1, False)
+            if j in (2, 3) and 0 <= s - 2 < last:
+                evac(s - 2, j - 2, False)
             if j == 3 and 0 <= s - 1 < last:
                 regroup_y(s - 1, 0, 0, 2, "a")
             if j == 0 and 0 <= s - 2 < last:
@@ -373,14 +380,10 @@ def tile_lowrankconv3d_t_kernel(tc, x, U_kh, U_kw, U_kd, U_c_in, U_c_out, bias, 
                 regroup_c(2 * s + 3, 0, 2, "v")
             if i == 1:
                 quant_x(5)
-            if j < 2 and 0 <= s - 2 < last:
-                quant_y(s - 2, j)
-            if i == 2:
-                quant_c(4)
+            if j == 1 and 0 <= s - 2 < last:
+                quant_y(s - 2, 0, 2)
             if j == 2 and s >= 0 and 2 * s + 3 < 16:
-                quant_c(2 * s + 3)
-            if j == 3 and s >= 0 and 2 * s + 6 < 16:
-                quant_c(2 * s + 6)
+                quant_pair(s)
             if 0 <= i - 1 < N_UNITS:
                 v_w(i - 1, 2)
             if 0 <= i - 2 < N_UNITS:
@@ -394,8 +397,8 @@ def tile_lowrankconv3d_t_kernel(tc, x, U_kh, U_kw, U_kd, U_c_in, U_c_out, bias, 
         regroup_y(last, 0, 1, 1, "a")
         regroup_y(last, 1, 0, 1, "a")
         regroup_y(last, 1, 1, 1, "v")
-        quant_y(last, 0)
-        quant_y(last, 1)
+        quant_y(last, 0, 1)
+        quant_y(last, 1, 1)
         mm2(last, 0, False)
         mm2(last, 1, True)
         evac(last, 0, True)

@@ -1,6 +1,7 @@
 from contextlib import ExitStack
 
 import concourse.mybir as mybir
+from concourse.masks import make_identity
 
 FLOPS = 2 * 512 * 512 * 8192 + 2 * 512 * 256 * 8192 + 2 * 9 * 512 * 8192
 
@@ -11,14 +12,16 @@ U8 = mybir.dt.uint8
 FP8X4 = mybir.dt.float8_e4m3fn_x4
 ACTF = mybir.ActivationFunctionType
 ALU = mybir.AluOpType
+AX = mybir.AxisListType
 
 P = 128
 SLICE = 256
-SLAB = 1024
-HALF = 512
-N_SLABS = 8
-N_UNITS = 32
-G_UNITS = 29
+CHUNK = 512
+N_CHUNKS = 16
+N_STEPS = 2 * N_CHUNKS
+DROW = 20
+WSLICE = 272
+RING = 6
 
 
 def tile_lowrankconv3d_t_kernel(tc, x, U_kh, U_kw, U_kd, U_c_in, U_c_out, bias, out):
@@ -28,21 +31,19 @@ def tile_lowrankconv3d_t_kernel(tc, x, U_kh, U_kw, U_kd, U_c_in, U_c_out, bias, 
 
     with ExitStack() as ctx:
         const = ctx.enter_context(tc.tile_pool(name="const", bufs=1))
-        rawp = ctx.enter_context(tc.tile_pool(name="rawp", bufs=3))
+        rawp = ctx.enter_context(tc.tile_pool(name="rawp", bufs=5))
         xgp = ctx.enter_context(tc.tile_pool(name="xgp", bufs=3))
-        xg0p = ctx.enter_context(tc.tile_pool(name="xg0p", bufs=6))
-        pdp = ctx.enter_context(tc.tile_pool(name="pdp", bufs=3))
-        y1p = ctx.enter_context(tc.tile_pool(name="y1p", bufs=4))
-        y2p = ctx.enter_context(tc.tile_pool(name="y2p", bufs=4))
-        ep = ctx.enter_context(tc.tile_pool(name="ep", bufs=2))
+        y2p = ctx.enter_context(tc.tile_pool(name="y2p", bufs=RING))
+        ytp = ctx.enter_context(tc.tile_pool(name="ytp", bufs=3))
         ygp = ctx.enter_context(tc.tile_pool(name="ygp", bufs=2))
         yqp = ctx.enter_context(tc.tile_pool(name="yqp", bufs=2))
         osp = ctx.enter_context(tc.tile_pool(name="osp", bufs=6))
-        pyp = ctx.enter_context(tc.psum_pool(name="pyp", bufs=6))
-        pop = ctx.enter_context(tc.psum_pool(name="pop", bufs=2))
+        mbp = ctx.enter_context(tc.psum_pool(name="mbp", bufs=4))
+        tbp = ctx.enter_context(tc.psum_pool(name="tbp", bufs=2))
+        wop = ctx.enter_context(tc.psum_pool(name="wop", bufs=2))
 
-        xq = const.tile([P, N_SLABS * SLAB], U32, align_bytes=64, name="xq")
-        xs = const.tile([P, N_SLABS * SLAB], U8, align_bytes=64, name="xs")
+        xq = const.tile([P, N_CHUNKS * CHUNK], U32, align_bytes=64, name="xq")
+        xs = const.tile([P, N_CHUNKS * CHUNK], U8, align_bytes=64, name="xs")
         w_raw = const.tile([P, 4, 512], BF16, name="w_raw")
         w_grp = const.tile([P, 512, 4], BF16, align_bytes=64, name="w_grp")
         wq = const.tile([P, 512], U32, align_bytes=64, name="wq")
@@ -51,252 +52,77 @@ def tile_lowrankconv3d_t_kernel(tc, x, U_kh, U_kw, U_kd, U_c_in, U_c_out, bias, 
         v_grp = const.tile([P, 256, 4], BF16, align_bytes=64, name="v_grp")
         vq = const.tile([P, 256], U32, align_bytes=64, name="vq")
         vs = const.tile([P, 256], U8, align_bytes=64, name="vs")
-        cb_h = const.tile([P, 3, 4], BF16, name="cb_h")
-        cb_w = const.tile([P, 3, 4], BF16, name="cb_w")
-        cb_d = const.tile([P, 3, 4], BF16, name="cb_d")
-        cf = const.tile([P, 3, 3, 4], F32, name="cf")
+        ident = const.tile([P, P], F32, align_bytes=64, name="ident")
+        ident_b = const.tile([P, 16], BF16, name="ident_b")
+        k_rows = const.tile([P, 512], BF16, name="k_rows")
+        k_perm = const.tile([P, 4, P], BF16, name="k_perm")
+        cf = const.tile([P, 4, 16], F32, name="cf")
+        c_abs = const.tile([P, 4, 2, 3], F32, name="c_abs")
+        c_max = const.tile([P, 4, 2], F32, name="c_max")
+        c_small = const.tile([P, 4, 2], F32, name="c_small")
+        c_piv = const.tile([P, 4, 2], F32, name="c_piv")
+        c_rec = const.tile([P, 4, 2], F32, name="c_rec")
+        c_pp = const.tile([P, 4], F32, name="c_pp")
+        c_h = const.tile([P, 3, 4], F32, name="c_h")
+        c_r = const.tile([P, 2, 4, 2], F32, name="c_r")
         bias_b = const.tile([P, 2], BF16, name="bias_b")
         bias_f = const.tile([P, 2], F32, name="bias_f")
+        y1_ring = []
+        pa_ring = []
+        pc_ring = []
+        for n in range(RING):
+            a = const.tile([P, 4 + 32 * DROW], F32, align_bytes=64, name=f"y1_{n}")
+            y1_ring.append(a)
+            a = const.tile([P, 16 + 2 * WSLICE], F32, align_bytes=64, name=f"pa_{n}")
+            pa_ring.append(a)
+            a = const.tile([P, 16 + 2 * WSLICE], F32, align_bytes=64, name=f"pc_{n}")
+            pc_ring.append(a)
 
         raw = {}
         xg = {}
-        pb = {}
-        y1 = {}
+        mb = {}
         y2 = {}
-        ee = {}
+        yt = {}
+        wb = {}
+        tb = {}
         yg = {}
         yq = {}
         ys = {}
         po = {}
-        pd = {}
-        xc = {}
 
-        def coef(f, k, t):
-            return cf[:, f, k, t : t + 1]
+        def load_x(c0, n):
+            b, cc = divmod(c0, 8)
+            r = rawp.tile([P, 4, 2 * CHUNK], BF16, name="raw")
+            nc.sync.dma_start(out=r[:, :, 0 : n * CHUNK], in_=xv[b][:, :, cc * CHUNK : (cc + n) * CHUNK])
+            for k in range(n):
+                raw[c0 + k] = r[:, :, k * CHUNK : (k + 1) * CHUNK]
 
-        def load_raw(s, pieces, weights_second):
-            b, sl = divmod(s, 4)
-            r = rawp.tile([P, 4, SLAB], BF16, name="raw")
-            w = SLAB // pieces
-            for k in range(pieces):
-                nc.sync.dma_start(
-                    out=r[:, :, k * w : (k + 1) * w], in_=xv[b][:, :, sl * SLAB + k * w : sl * SLAB + (k + 1) * w]
-                )
-                if weights_second and k == 0:
-                    nc.sync.dma_start(out=w_raw[:], in_=U_c_in.rearrange("(p j) r -> p j r", j=4))
-                    nc.sync.dma_start(out=cb_h[:], in_=U_kh.rearrange("k (m t) -> m k t", t=4))
-            raw[s] = r
-
-        def regroup_x(n, eng):
-            s, q = divmod(n, 4)
-            g = xg0p.tile([P, SLICE, 4], BF16, align_bytes=64, name="xg0")
-            src = raw[s][:, :, q * SLICE : (q + 1) * SLICE].rearrange("p t (c i) -> p c t i", i=4)
-            dst = g[:].rearrange("p (c i) t -> p c t i", i=4)
-            if eng == "v":
-                nc.vector.tensor_copy(out=dst, in_=src)
-            else:
-                nc.scalar.copy(out=dst, in_=src)
-            xg[n] = g
-
-        def quant_x(n):
-            c0 = n * SLICE
-            nc.vector.quantize_mx(
-                out=xq[:, c0 : c0 + SLICE].bitcast(FP8X4),
-                scales=xs[:, c0 : c0 + SLICE],
-                in_=xg[n][:].rearrange("p w j -> p (w j)"),
-            )
-
-        def regroup_c(c, first, count, eng):
-            pr, side = divmod(c - 3, 2)
-            if pr not in xc:
-                g = xgp.tile([P, 2 * HALF, 4], BF16, align_bytes=64, name="xc")
-                xc[pr] = g
-            g = xc[pr]
-            lo = first * SLICE
-            hi = lo + count * SLICE
-            base = (c % 2) * HALF
-            src = raw[c // 2][:, :, base + lo : base + hi].rearrange("p t (c i) -> p c t i", i=4)
-            dst = g[:, side * HALF + lo : side * HALF + hi, :].rearrange("p (c i) t -> p c t i", i=4)
+        def regroup_x(c, side, eng):
+            if c not in xg:
+                g = xgp.tile([P, CHUNK, 4], BF16, align_bytes=64, name="xg")
+                xg[c] = g
+            lo = side * SLICE
+            src = raw[c][:, :, lo : lo + SLICE].rearrange("p t (c i) -> p c t i", i=4)
+            dst = xg[c][:, lo : lo + SLICE, :].rearrange("p (c i) t -> p c t i", i=4)
             if eng == "v":
                 nc.vector.tensor_copy(out=dst, in_=src)
             else:
                 nc.scalar.copy(out=dst, in_=src)
 
-        def quant_pair(pr):
-            c0 = (2 * pr + 3) * HALF
-            n = 2 * HALF if 2 * pr + 4 < 16 else HALF
+        def quant_x(c, first, count):
+            c0 = c * CHUNK + first * SLICE
+            n = count * SLICE
             nc.vector.quantize_mx(
                 out=xq[:, c0 : c0 + n].bitcast(FP8X4),
                 scales=xs[:, c0 : c0 + n],
-                in_=xc[pr][:, 0:n, :].rearrange("p w j -> p (w j)"),
+                in_=xg[c][:, first * SLICE : first * SLICE + n, :].rearrange("p w j -> p (w j)"),
             )
-
-        def mm1(u):
-            s, t = divmod(u, 4)
-            b, sl = divmod(s, 4)
-            h0 = sl * 4
-            banks = []
-            for k in range(3):
-                lo = h0 - 1 + 2 * k
-                o0, n = 0, 512
-                if lo < 0:
-                    lo, o0, n = 0, SLICE, SLICE
-                elif lo + 1 > 15:
-                    n = SLICE
-                c0 = b * 4096 + lo * SLICE
-                bank = pyp.tile([P, 512], F32, name="pb")
-                nc.tensor.matmul_mx(
-                    out=bank[:, o0 : o0 + n],
-                    lhsT=wq[:, t * P : (t + 1) * P].bitcast(FP8X4),
-                    lhsT_scale=ws[:, t * P : (t + 1) * P],
-                    rhs=xq[:, c0 : c0 + n].bitcast(FP8X4),
-                    rhs_scale=xs[:, c0 : c0 + n],
-                    start=True,
-                    stop=True,
-                )
-                banks.append(bank)
-            pb[u] = banks
-
-        def scale_copy(dst, src, c):
-            nc.scalar.activation(out=dst, in_=src, func=ACTF.Copy, scale=c)
-
-        def mac(acc, src, c):
-            nc.vector.scalar_tensor_tensor(out=acc, in0=src, scalar=c, in1=acc, op0=ALU.mult, op1=ALU.add)
-
-        def a_h(u):
-            t = u % 4
-            a = y1p.tile([P, SLAB], F32, name="y1")
-            b0, b1, b2 = pb[u]
-            c = coef(0, 1, t)
-            scale_copy(a[:, 0:256], b0[:, 256:512], c)
-            scale_copy(a[:, 256:768], b1[:, :], c)
-            scale_copy(a[:, 768:1024], b2[:, 0:256], c)
-            y1[u] = a
-
-        def v_h(u):
-            s, t = divmod(u, 4)
-            sl = s % 4
-            a = y1[u]
-            b0, b1, b2 = pb[u]
-            c = coef(0, 0, t)
-            if sl == 0:
-                mac(a[:, 256:512], b0[:, 256:512], c)
-            else:
-                mac(a[:, 0:512], b0[:, :], c)
-            mac(a[:, 512:1024], b1[:, :], c)
-            c = coef(0, 2, t)
-            mac(a[:, 0:512], b1[:, :], c)
-            if sl == 3:
-                mac(a[:, 512:768], b2[:, 0:256], c)
-            else:
-                mac(a[:, 512:1024], b2[:, :], c)
-
-        def a_w(u):
-            a = y2p.tile([P, SLAB], F32, name="y2")
-            scale_copy(a[:], y1[u][:], coef(1, 1, u % 4))
-            y2[u] = a
-
-        def v_w(u, k):
-            t = u % 4
-            src = y1[u][:].rearrange("p (s q) -> p s q", q=SLICE)
-            acc = y2[u][:].rearrange("p (s q) -> p s q", q=SLICE)
-            if k == 0:
-                mac(acc[:, :, 16:256], src[:, :, 0:240], coef(1, 0, t))
-            else:
-                mac(acc[:, :, 0:240], src[:, :, 16:256], coef(1, 2, t))
-
-        def a_d(u):
-            s, t = divmod(u, 4)
-            if t == 0:
-                e = ep.tile([P, 4, SLAB], F32, name="ee")
-                ee[s] = e
-            scale_copy(ee[s][:, t, :], y2[u][:], coef(2, 1, t))
-
-        def a_d2(u):
-            t = u % 4
-            pr = pdp.tile([P, 64, 16], F32, name="pd")
-            src = y2[u][:].rearrange("p (q d) -> p q d", d=16)
-            scale_copy(pr[:, :, 0:15], src[:, :, 1:16], coef(2, 2, t))
-            pd[u] = pr
-
-        def g_d2(u):
-            s, t = divmod(u, 4)
-            acc = ee[s][:, t, :].rearrange("p (q d) -> p q d", d=16)
-            nc.gpsimd.tensor_tensor(out=acc[:, :, 0:15], in0=acc[:, :, 0:15], in1=pd[u][:, :, 0:15], op=ALU.add)
-
-        def v_d(u, k):
-            s, t = divmod(u, 4)
-            src = y2[u][:].rearrange("p (q d) -> p q d", d=16)
-            acc = ee[s][:, t, :].rearrange("p (q d) -> p q d", d=16)
-            if k == 0:
-                mac(acc[:, :, 1:16], src[:, :, 0:15], coef(2, 0, t))
-            else:
-                mac(acc[:, :, 0:15], src[:, :, 1:16], coef(2, 2, t))
-
-        def regroup_y(s, half, first, count, eng):
-            if s not in yg:
-                g = ygp.tile([P, SLAB, 4], BF16, align_bytes=64, name="yg")
-                yg[s] = g
-            g = yg[s]
-            lo = half * HALF + first * SLICE
-            hi = lo + count * SLICE
-            src = ee[s][:, :, lo:hi].rearrange("p t (c i) -> p c t i", i=4)
-            dst = g[:, lo:hi, :].rearrange("p (c i) t -> p c t i", i=4)
-            if eng == "v":
-                nc.vector.tensor_copy(out=dst, in_=src)
-            else:
-                nc.scalar.copy(out=dst, in_=src)
-
-        def quant_y(s, half, count):
-            if s not in yq:
-                q = yqp.tile([P, SLAB], U32, align_bytes=64, name="yq")
-                sc = yqp.tile([P, SLAB], U8, align_bytes=64, name="ys")
-                yq[s] = q
-                ys[s] = sc
-            lo = half * HALF
-            hi = lo + count * HALF
-            nc.vector.quantize_mx(
-                out=yq[s][:, lo:hi].bitcast(FP8X4),
-                scales=ys[s][:, lo:hi],
-                in_=yg[s][:, lo:hi, :].rearrange("p w j -> p (w j)"),
-            )
-
-        def mm2(s, half, spare_banks):
-            banks = []
-            for ot in range(2):
-                if spare_banks:
-                    bank = pyp.tile([P, HALF], F32, name="pb")
-                else:
-                    bank = pop.tile([P, HALF], F32, name="po")
-                nc.tensor.matmul_mx(
-                    out=bank[:],
-                    lhsT=vq[:, ot * P : (ot + 1) * P].bitcast(FP8X4),
-                    lhsT_scale=vs[:, ot * P : (ot + 1) * P],
-                    rhs=yq[s][:, half * HALF : (half + 1) * HALF].bitcast(FP8X4),
-                    rhs_scale=ys[s][:, half * HALF : (half + 1) * HALF],
-                    start=True,
-                    stop=True,
-                )
-                banks.append(bank)
-            po[(s, half)] = banks
-
-        def evac(s, half, share):
-            b, sl = divmod(s, 4)
-            p0 = sl * SLAB + half * HALF
-            for ot in range(2):
-                o = osp.tile([P, HALF], F32, name="osb")
-                if share and ot == 1:
-                    nc.vector.tensor_scalar_add(out=o[:], in0=po[(s, half)][ot][:], scalar1=bias_f[:, ot : ot + 1])
-                else:
-                    nc.scalar.activation(
-                        out=o[:], in_=po[(s, half)][ot][:], func=ACTF.Identity, bias=bias_f[:, ot : ot + 1], scale=1.0
-                    )
-                nc.sync.dma_start(out=ov[b][ot * P : (ot + 1) * P, p0 : p0 + HALF], in_=o[:])
 
         def regroup_w(t):
+            u, h = divmod(t, 2)
             nc.vector.tensor_copy(
-                out=w_grp[:, t * P : (t + 1) * P, :],
-                in_=w_raw[:].rearrange("p j (m t) -> p t m j", t=4)[:, t, :, :],
+                out=w_grp[:, t * P : (t + 1) * P, :].rearrange("p (m e) j -> p m e j", e=2),
+                in_=w_raw[:].rearrange("p j (h m u e) -> p h u m e j", h=2, u=2, e=2)[:, h, u],
             )
 
         def quant_w(t):
@@ -306,100 +132,295 @@ def tile_lowrankconv3d_t_kernel(tc, x, U_kh, U_kw, U_kd, U_c_in, U_c_out, bias, 
                 in_=w_grp[:, t * P : (t + 1) * P, :].rearrange("p r j -> p (r j)"),
             )
 
-        load_raw(0, 2, True)
-        load_raw(1, 2, False)
-        nc.sync.dma_start(out=cb_w[:], in_=U_kw.rearrange("k (m t) -> m k t", t=4))
-        nc.sync.dma_start(out=cb_d[:], in_=U_kd.rearrange("k (m t) -> m k t", t=4))
+        def tiles_of(j):
+            return (2 * (j % 2), 2 * (j % 2) + 1)
+
+        def slot(j, i):
+            return (2 * j + i) % RING
+
+        def mm1(j):
+            c = j // 2
+            b, cc = divmod(c, 8)
+            for i, t in enumerate(tiles_of(j)):
+                banks = []
+                for side in range(2):
+                    lo, o0, n = 2 * cc - 1 + 2 * side, 0, CHUNK
+                    if lo < 0:
+                        lo, o0, n = 0, SLICE, SLICE
+                    elif lo == 15:
+                        n = SLICE
+                    c0 = b * 4096 + lo * SLICE
+                    bank = mbp.tile([P, CHUNK], F32, name="mb")
+                    nc.tensor.matmul_mx(
+                        out=bank[:, o0 : o0 + n],
+                        lhsT=wq[:, t * P : (t + 1) * P].bitcast(FP8X4),
+                        lhsT_scale=ws[:, t * P : (t + 1) * P],
+                        rhs=xq[:, c0 : c0 + n].bitcast(FP8X4),
+                        rhs_scale=xs[:, c0 : c0 + n],
+                        start=True,
+                        stop=True,
+                    )
+                    banks.append(bank)
+                mb[(j, i)] = banks
+
+        def y1_rows(j, i, off):
+            a = y1_ring[slot(j, i)]
+            if off == 0:
+                v = a[:, 4 : 4 + 32 * DROW].rearrange("p (q e) -> p q e", e=DROW)
+                return v[:, :, 0:16]
+            if off > 0:
+                v = a[:, 4 : 4 + 32 * DROW].rearrange("p (q e) -> p q e", e=DROW)
+                return v[:, :, 1:17]
+            v = a[:, 0 : 32 * DROW].rearrange("p (q e) -> p q e", e=DROW)
+            return v[:, :, 3:19]
+
+        def rows(v):
+            return v.rearrange("p (q d) -> p q d", d=16)
+
+        def mac(dst, acc, src, c):
+            nc.vector.scalar_tensor_tensor(out=dst, in0=src, scalar=c, in1=acc, op0=ALU.mult, op1=ALU.add)
+
+        def centre(j, i):
+            t = tiles_of(j)[i]
+            left, right = mb[(j, i)]
+            a = y1_rows(j, i, 0)
+            c = c_h[:, 1, t : t + 1]
+            nc.scalar.activation(out=a[:, 0:16, :], in_=rows(left[:, SLICE:CHUNK]), func=ACTF.Copy, scale=c)
+            nc.scalar.activation(out=a[:, 16:32, :], in_=rows(right[:, 0:SLICE]), func=ACTF.Copy, scale=c)
+
+        def h_left(j, i):
+            t = tiles_of(j)[i]
+            left = mb[(j, i)][0]
+            a = y1_rows(j, i, 0)
+            c = c_h[:, 0, t : t + 1]
+            if (j // 2) % 8 == 0:
+                mac(a[:, 16:32, :], a[:, 16:32, :], rows(left[:, SLICE:CHUNK]), c)
+            else:
+                mac(a, a, rows(left[:]), c)
+
+        def h_right(j, i):
+            t = tiles_of(j)[i]
+            right = mb[(j, i)][1]
+            a = y1_rows(j, i, 0)
+            c = c_h[:, 2, t : t + 1]
+            if (j // 2) % 8 == 7:
+                mac(a[:, 0:16, :], a[:, 0:16, :], rows(right[:, 0:SLICE]), c)
+            else:
+                mac(a, a, rows(right[:]), c)
+
+        def d_tap(j, i, k):
+            t = tiles_of(j)[i]
+            if k == 0:
+                a = y2p.tile([P, CHUNK], F32, align_bytes=64, name="y2")
+                y2[(j, i)] = a
+                mac(rows(a[:]), y1_rows(j, i, 0), y1_rows(j, i, -1), c_r[:, 0, t, 1:2])
+            else:
+                a = y2[(j, i)]
+                mac(rows(a[:]), rows(a[:]), y1_rows(j, i, 1), c_r[:, 1, t, 1:2])
+
+        def w_products(j, i):
+            t = tiles_of(j)[i]
+            src = y2[(j, i)][:].rearrange("p (s r) -> p s r", r=SLICE)
+            for k, ring in enumerate((pa_ring, pc_ring)):
+                dst = ring[slot(j, i)][:, 16 : 16 + 2 * WSLICE].rearrange("p (s r) -> p s r", r=WSLICE)
+                nc.gpsimd.tensor_scalar(
+                    out=dst[:, :, 0:SLICE],
+                    in0=src,
+                    scalar1=c_r[:, k, t, 0:1],
+                    scalar2=0.0,
+                    op0=ALU.mult,
+                    op1=ALU.add,
+                )
+
+        def w_sum(j, i):
+            bank = tbp.tile([P, CHUNK], F32, name="tb")
+            pa = pa_ring[slot(j, i)]
+            pc = pc_ring[slot(j, i)]
+            for q in range(4):
+                o = bank[:, q * P : (q + 1) * P]
+                base = 16 + (q // 2) * WSLICE + (q % 2) * P
+                parts = (y2[(j, i)][:, q * P : (q + 1) * P], pa[:, base - 16 : base - 16 + P], pc[:, base + 16 : base + 16 + P])
+                for k, part in enumerate(parts):
+                    nc.tensor.matmul(out=o, lhsT=part, rhs=ident[:], is_transpose=True, start=(k == 0), stop=(k == 2))
+            tb[(j, i)] = bank
+
+        def round_y3(j, i):
+            c = j // 2
+            t = tiles_of(j)[i]
+            if c not in yt:
+                a = ytp.tile([P, 4, 512], BF16, align_bytes=64, name="yt")
+                yt[c] = a
+            nc.scalar.copy(
+                out=yt[c][:, :, t * P : (t + 1) * P], in_=tb[(j, i)][:].rearrange("p (q r) -> p q r", q=4)
+            )
+
+        def turn_y3(c, k):
+            bank = wop.tile([P, CHUNK], F32, name="wo")
+            for q in range(2):
+                words = yt[c][:, 2 * k + q, :].bitcast(F32)
+                for u in range(2):
+                    nc.tensor.transpose(
+                        bank[:, (2 * q + u) * P : (2 * q + u + 1) * P], words[:, u * P : (u + 1) * P], ident[:]
+                    )
+            wb[(c, k)] = bank
+
+        def gather_y3(c, k, eng):
+            if c not in yg:
+                g = ygp.tile([P, CHUNK, 4], BF16, align_bytes=64, name="yg")
+                yg[c] = g
+            dst = (
+                yg[c][:, k * SLICE : (k + 1) * SLICE, :]
+                .rearrange("p n j -> p (n j)")
+                .bitcast(F32)
+                .rearrange("p (q n u) -> p q n u", q=2, u=2)
+            )
+            src = wb[(c, k)][:].rearrange("p (q u n) -> p q n u", q=2, u=2)
+            if eng == "v":
+                nc.vector.tensor_copy(out=dst, in_=src)
+            else:
+                nc.scalar.copy(out=dst, in_=src)
+
+        def quant_y(c):
+            q = yqp.tile([P, CHUNK], U32, align_bytes=64, name="yq")
+            sc = yqp.tile([P, CHUNK], U8, align_bytes=64, name="ys")
+            nc.vector.quantize_mx(out=q[:].bitcast(FP8X4), scales=sc[:], in_=yg[c][:].rearrange("p w j -> p (w j)"))
+            yq[c] = q
+            ys[c] = sc
+
+        def mm2(c, ot):
+            bank = wop.tile([P, CHUNK], F32, name="wo")
+            nc.tensor.matmul_mx(
+                out=bank[:],
+                lhsT=vq[:, ot * P : (ot + 1) * P].bitcast(FP8X4),
+                lhsT_scale=vs[:, ot * P : (ot + 1) * P],
+                rhs=yq[c][:].bitcast(FP8X4),
+                rhs_scale=ys[c][:],
+                start=True,
+                stop=True,
+            )
+            po[(c, ot)] = bank
+
+        def evac(c, ot, eng):
+            b, cc = divmod(c, 8)
+            o = osp.tile([P, CHUNK], F32, name="osb")
+            if eng == "v":
+                nc.vector.tensor_scalar_add(out=o[:], in0=po[(c, ot)][:], scalar1=bias_f[:, ot : ot + 1])
+            else:
+                nc.scalar.activation(
+                    out=o[:], in_=po[(c, ot)][:], func=ACTF.Identity, bias=bias_f[:, ot : ot + 1], scale=1.0
+                )
+            nc.sync.dma_start(out=ov[b][ot * P : (ot + 1) * P, cc * CHUNK : (cc + 1) * CHUNK], in_=o[:])
+
+        nc.vector.memset(k_rows[:], 0.0)
+        load_x(0, 1)
+        nc.sync.dma_start(out=w_raw[:], in_=U_c_in.rearrange("(p j) r -> p j r", j=4))
+        nc.scalar.dma_start(out=k_rows[0:3, :], in_=U_kh)
+        nc.scalar.dma_start(out=k_rows[3:6, :], in_=U_kw)
+        nc.scalar.dma_start(out=k_rows[6:9, :], in_=U_kd)
+        load_x(1, 1)
+        load_x(2, 2)
         with nc.allow_non_contiguous_dma(reason="256 bias values, one per partition and output tile"):
             nc.scalar.dma_start(out=bias_b[:], in_=bias.rearrange("(j p) -> p j", p=P))
         nc.scalar.dma_start(out=v_raw[:], in_=U_c_out.rearrange("(p j) o -> p j o", j=4))
-        load_raw(2, 1, False)
+        make_identity(nc, ident[:])
+        for n in range(RING):
+            nc.gpsimd.memset(y1_ring[n][:], 0.0)
+            nc.gpsimd.memset(pa_ring[n][:], 0.0)
+            nc.gpsimd.memset(pc_ring[n][:], 0.0)
 
-        regroup_x(0, "v")
-        regroup_x(1, "a")
+        nc.vector.tensor_copy(out=ident_b[:], in_=ident[:, 0:16])
+        for u in range(2):
+            nc.vector.tensor_copy(
+                out=k_perm[:, 2 * u : 2 * u + 2, :].rearrange("p h (m e) -> p h m e", e=2),
+                in_=k_rows[:].rearrange("p (h m u e) -> p u h m e", h=2, u=2, e=2)[:, u],
+            )
+        k_bank = wop.tile([P, 4, 16], F32, name="wo")
+        for t in range(4):
+            nc.tensor.matmul(k_bank[:, t, :], lhsT=k_perm[:, t, :], rhs=ident_b[:], start=True, stop=True)
+        nc.vector.tensor_copy(out=cf[:], in_=k_bank[:])
+        regroup_x(0, 0, "v")
+        regroup_x(0, 1, "a")
         regroup_w(0)
-        quant_x(0)
+        quant_x(0, 0, 1)
         quant_w(0)
-        quant_x(1)
-        regroup_x(2, "v")
-        regroup_x(3, "a")
-        nc.vector.tensor_copy(out=cf[:, 0, :, :], in_=cb_h[:])
-        nc.vector.tensor_copy(out=cf[:, 1, :, :], in_=cb_w[:])
-        nc.vector.tensor_copy(out=cf[:, 2, :, :], in_=cb_d[:])
-        quant_x(2)
-        quant_x(3)
-        regroup_x(4, "v")
+        taps = cf[:, :, 3:9].rearrange("p t (a k) -> p t a k", k=3)
+        nc.vector.tensor_scalar_mul(out=c_abs[:], in0=taps, scalar1=-1.0)
+        nc.vector.tensor_tensor(out=c_abs[:], in0=c_abs[:], in1=taps, op=ALU.max)
+        nc.vector.tensor_reduce(out=c_max[:], in_=c_abs[:], op=ALU.max, axis=AX.X)
+        nc.vector.tensor_scalar(
+            out=c_max[:], in0=c_max[:], scalar1=2.0**-32, scalar2=2.0**-100, op0=ALU.mult, op1=ALU.add
+        )
+        nc.vector.tensor_tensor(out=c_small[:], in0=c_abs[:, :, :, 1], in1=c_max[:], op=ALU.is_lt)
+        nc.vector.scalar_tensor_tensor(
+            out=c_small[:], in0=c_small[:], scalar=2.0, in1=c_max[:], op0=ALU.mult, op1=ALU.mult
+        )
+        nc.vector.tensor_tensor(out=c_piv[:], in0=taps[:, :, :, 1], in1=c_small[:], op=ALU.add)
+        nc.vector.reciprocal(out=c_rec[:], in_=c_piv[:])
+        nc.vector.tensor_tensor(out=c_pp[:], in0=c_piv[:, :, 0], in1=c_piv[:, :, 1], op=ALU.mult)
+        for k in (1, 0, 2):
+            nc.vector.tensor_tensor(out=c_h[:, k, :], in0=cf[:, :, k], in1=c_pp[:], op=ALU.mult)
+        for k in range(2):
+            nc.vector.tensor_tensor(out=c_r[:, k], in0=taps[:, :, :, 2 * k], in1=c_rec[:], op=ALU.mult)
+        quant_x(0, 1, 1)
+        regroup_x(1, 0, "v")
         regroup_w(1)
-        quant_x(4)
+        quant_x(1, 0, 1)
         quant_w(1)
+        regroup_x(1, 1, "a")
+        regroup_x(2, 0, "a")
+        regroup_x(2, 1, "a")
 
-        last = N_SLABS - 1
-        for i in range(-1, N_UNITS + 4):
-            s, j = divmod(i, 4)
-            if j == 0 and s >= 0 and s + 3 < N_SLABS:
-                load_raw(s + 3, 1, False)
-            if 0 <= i + 1 < N_UNITS:
-                mm1(i + 1)
-            if j in (2, 3) and 0 <= s - 2 < last:
-                mm2(s - 2, j - 2, False)
-            if 0 <= i < N_UNITS:
-                a_h(i)
-            if 0 <= i - 1 < N_UNITS:
-                a_w(i - 1)
-            if j in (2, 3) and 0 <= s - 2 < last:
-                evac(s - 2, j - 2, False)
-            if j == 3 and 0 <= s - 1 < last:
-                regroup_y(s - 1, 0, 0, 2, "a")
-            if j == 0 and 0 <= s - 2 < last:
-                regroup_y(s - 2, 1, 0, 2, "a")
-            if i in (0, 1):
-                regroup_c(4, i, 1, "a")
-            if j in (1, 2) and s >= 0 and 2 * s + 6 < 16:
-                regroup_c(2 * s + 6, j - 1, 1, "a")
-            if 0 <= i - 2 < N_UNITS:
-                a_d(i - 2)
-            if 0 <= i - 2 < G_UNITS:
-                a_d2(i - 2)
-            if 0 <= i < N_UNITS:
-                v_h(i)
-            if 0 <= i - 1 < N_UNITS:
-                v_w(i - 1, 0)
-            if i == -1:
+        for j in range(-1, N_STEPS + 5):
+            if j >= 0 and j % 4 == 0 and j // 2 + 4 < N_CHUNKS:
+                load_x(j // 2 + 4, 2)
+            if 0 <= j - 1 < N_STEPS:
+                for i in range(2):
+                    w_products(j - 1, i)
+                w_sum(j - 1, 0)
+                round_y3(j - 1, 0)
+            if 0 <= j < N_STEPS:
+                for i in range(2):
+                    h_left(j, i)
+                for i in range(2):
+                    h_right(j, i)
+            if j + 1 < N_STEPS:
+                mm1(j + 1)
+                for i in range(2):
+                    centre(j + 1, i)
+            if 0 <= j < N_STEPS:
+                for i in range(2):
+                    d_tap(j, i, 0)
+            if j == -1:
+                quant_x(1, 1, 1)
                 regroup_w(2)
                 regroup_w(3)
                 quant_w(2)
-                nc.vector.tensor_copy(out=v_grp[:], in_=v_raw[:].rearrange("p j o -> p o j"))
                 quant_w(3)
+                nc.vector.tensor_copy(out=v_grp[:], in_=v_raw[:].rearrange("p j o -> p o j"))
+                quant_x(2, 0, 2)
                 nc.vector.tensor_copy(out=bias_f[:], in_=bias_b[:])
                 nc.vector.quantize_mx(
                     out=vq[:].bitcast(FP8X4), scales=vs[:], in_=v_grp[:].rearrange("p o j -> p (o j)")
                 )
-            if i == 0:
-                regroup_x(5, "v")
-            if j == 0 and s >= 0 and 2 * s + 3 < 16:
-                regroup_c(2 * s + 3, 0, 2, "v")
-            if i == 1:
-                quant_x(5)
-            if j == 1 and 0 <= s - 2 < last:
-                quant_y(s - 2, 0, 2)
-            if j == 2 and s >= 0 and 2 * s + 3 < 16:
-                quant_pair(s)
-            if 0 <= i - 1 < N_UNITS:
-                v_w(i - 1, 2)
-            if 0 <= i - 2 < N_UNITS:
-                v_d(i - 2, 0)
-            if G_UNITS <= i - 2 < N_UNITS:
-                v_d(i - 2, 2)
-            if 0 <= i - 2 < G_UNITS:
-                g_d2(i - 2)
-
-        regroup_y(last, 0, 0, 1, "v")
-        regroup_y(last, 0, 1, 1, "a")
-        regroup_y(last, 1, 0, 1, "a")
-        regroup_y(last, 1, 1, 1, "v")
-        quant_y(last, 0, 1)
-        quant_y(last, 1, 1)
-        mm2(last, 0, False)
-        mm2(last, 1, True)
-        evac(last, 0, True)
-        evac(last, 1, True)
+            if j % 2 == 1 and j >= 1 and (j + 5) // 2 < N_CHUNKS:
+                quant_x((j + 5) // 2, 0, 2)
+            if j % 2 == 0 and 0 <= j // 2 - 2 < N_CHUNKS:
+                quant_y(j // 2 - 2)
+            if 0 <= j < N_STEPS:
+                for i in range(2):
+                    d_tap(j, i, 1)
+            if 0 <= j - 1 < N_STEPS:
+                w_sum(j - 1, 1)
+                round_y3(j - 1, 1)
+            if (j + 7) // 2 < N_CHUNKS and j >= -1:
+                regroup_x((j + 7) // 2, (j + 7) % 2, "a")
+            if j % 2 == 0 and 0 <= j // 2 - 2 < N_CHUNKS:
+                for ot in range(2):
+                    mm2(j // 2 - 2, ot)
+                for ot in range(2):
+                    evac(j // 2 - 2, ot, "a")
+            if j % 2 == 1 and 0 <= (j - 3) // 2 < N_CHUNKS:
+                for k in range(2):
+                    turn_y3((j - 3) // 2, k)
+                for k in range(2):
+                    gather_y3((j - 3) // 2, k, "a")

@@ -223,14 +223,17 @@ def tile_lowrankconv3d_t_kernel(tc, x, U_kh, U_kw, U_kd, U_c_in, U_c_out, bias, 
             src = y2[(j, i)][:].rearrange("p (s r) -> p s r", r=SLICE)
             for k, ring in enumerate((pa_ring, pc_ring)):
                 dst = ring[slot(j, i)][:, 16 : 16 + 2 * WSLICE].rearrange("p (s r) -> p s r", r=WSLICE)
-                nc.gpsimd.tensor_scalar(
-                    out=dst[:, :, 0:SLICE],
-                    in0=src,
-                    scalar1=c_r[:, k, t, 0:1],
-                    scalar2=0.0,
-                    op0=ALU.mult,
-                    op1=ALU.add,
-                )
+                if k == 0:
+                    nc.gpsimd.tensor_scalar(
+                        out=dst[:, :, 0:SLICE],
+                        in0=src,
+                        scalar1=c_r[:, k, t, 0:1],
+                        scalar2=0.0,
+                        op0=ALU.mult,
+                        op1=ALU.add,
+                    )
+                else:
+                    nc.scalar.activation(out=dst[:, :, 0:SLICE], in_=src, func=ACTF.Copy, scale=c_r[:, k, t, 0:1])
 
         def w_sum(j, i):
             bank = tbp.tile([P, CHUNK], F32, name="tb")

@@ -18,10 +18,12 @@ P = 128
 SLICE = 256
 CHUNK = 512
 N_CHUNKS = 16
-N_STEPS = 2 * N_CHUNKS
+GROUPS = ((2, 2, 4, 4, 4), (4, 4, 4, 2, 2))
 DROW = 20
 WSLICE = 272
-RING = 6
+RING = 4
+LATE = 2
+SCALED = 2
 
 
 def tile_lowrankconv3d_t_kernel(tc, x, U_kh, U_kw, U_kd, U_c_in, U_c_out, bias, out):
@@ -33,8 +35,7 @@ def tile_lowrankconv3d_t_kernel(tc, x, U_kh, U_kw, U_kd, U_c_in, U_c_out, bias, 
         const = ctx.enter_context(tc.tile_pool(name="const", bufs=1))
         rawp = ctx.enter_context(tc.tile_pool(name="rawp", bufs=5))
         xgp = ctx.enter_context(tc.tile_pool(name="xgp", bufs=3))
-        y2p = ctx.enter_context(tc.tile_pool(name="y2p", bufs=RING))
-        ytp = ctx.enter_context(tc.tile_pool(name="ytp", bufs=3))
+        ytp = ctx.enter_context(tc.tile_pool(name="ytp", bufs=4))
         ygp = ctx.enter_context(tc.tile_pool(name="ygp", bufs=2))
         yqp = ctx.enter_context(tc.tile_pool(name="yqp", bufs=2))
         osp = ctx.enter_context(tc.tile_pool(name="osp", bufs=6))
@@ -67,21 +68,24 @@ def tile_lowrankconv3d_t_kernel(tc, x, U_kh, U_kw, U_kd, U_c_in, U_c_out, bias, 
         c_r = const.tile([P, 2, 4, 2], F32, name="c_r")
         bias_b = const.tile([P, 2], BF16, name="bias_b")
         bias_f = const.tile([P, 2], F32, name="bias_f")
+        diag = const.tile([P, 4, P], F32, align_bytes=64, name="diag")
         y1_ring = []
+        y2_ring = []
         pa_ring = []
         pc_ring = []
         for n in range(RING):
-            a = const.tile([P, 4 + 32 * DROW], F32, align_bytes=64, name=f"y1_{n}")
+            a = const.tile([P, 8 + 64 * DROW], F32, align_bytes=64, name=f"y1_{n}")
             y1_ring.append(a)
-            a = const.tile([P, 16 + 2 * WSLICE], F32, align_bytes=64, name=f"pa_{n}")
+            a = const.tile([P, 16 + 4 * WSLICE], F32, align_bytes=64, name=f"y2_{n}")
+            y2_ring.append(a)
+            a = const.tile([P, 16 + 4 * WSLICE], F32, align_bytes=64, name=f"pa_{n}")
             pa_ring.append(a)
-            a = const.tile([P, 16 + 2 * WSLICE], F32, align_bytes=64, name=f"pc_{n}")
+            a = const.tile([P, 16 + 4 * WSLICE], F32, align_bytes=64, name=f"pc_{n}")
             pc_ring.append(a)
 
         raw = {}
         xg = {}
         mb = {}
-        y2 = {}
         yt = {}
         wb = {}
         tb = {}
@@ -132,130 +136,148 @@ def tile_lowrankconv3d_t_kernel(tc, x, U_kh, U_kw, U_kd, U_c_in, U_c_out, bias, 
                 in_=w_grp[:, t * P : (t + 1) * P, :].rearrange("p r j -> p (r j)"),
             )
 
-        def tiles_of(j):
-            return (2 * (j % 2), 2 * (j % 2) + 1)
-
-        def slot(j, i):
-            return (2 * j + i) % RING
+        steps = []
+        for b in range(2):
+            s0 = 0
+            for n in GROUPS[b]:
+                for t in range(4):
+                    steps.append((b, s0, n, t))
+                s0 += n
+        n_steps = len(steps)
 
         def mm1(j):
-            c = j // 2
-            b, cc = divmod(c, 8)
-            for i, t in enumerate(tiles_of(j)):
-                banks = []
-                for side in range(2):
-                    lo, o0, n = 2 * cc - 1 + 2 * side, 0, CHUNK
-                    if lo < 0:
-                        lo, o0, n = 0, SLICE, SLICE
-                    elif lo == 15:
-                        n = SLICE
-                    c0 = b * 4096 + lo * SLICE
-                    bank = mbp.tile([P, CHUNK], F32, name="mb")
-                    nc.tensor.matmul_mx(
-                        out=bank[:, o0 : o0 + n],
-                        lhsT=wq[:, t * P : (t + 1) * P].bitcast(FP8X4),
-                        lhsT_scale=ws[:, t * P : (t + 1) * P],
-                        rhs=xq[:, c0 : c0 + n].bitcast(FP8X4),
-                        rhs_scale=xs[:, c0 : c0 + n],
-                        start=True,
-                        stop=True,
-                    )
-                    banks.append(bank)
-                mb[(j, i)] = banks
+            b, s0, ns, t = steps[j]
+            banks = []
+            for k in range(ns // 2 + 1):
+                lo, o0, n = s0 - 1 + 2 * k, 0, CHUNK
+                if lo < 0:
+                    lo, o0, n = 0, SLICE, SLICE
+                elif lo == 15:
+                    n = SLICE
+                c0 = b * 4096 + lo * SLICE
+                bank = mbp.tile([P, CHUNK], F32, name="mb")
+                nc.tensor.matmul_mx(
+                    out=bank[:, o0 : o0 + n],
+                    lhsT=wq[:, t * P : (t + 1) * P].bitcast(FP8X4),
+                    lhsT_scale=ws[:, t * P : (t + 1) * P],
+                    rhs=xq[:, c0 : c0 + n].bitcast(FP8X4),
+                    rhs_scale=xs[:, c0 : c0 + n],
+                    start=True,
+                    stop=True,
+                )
+                banks.append(bank)
+            mb[j] = banks
 
-        def y1_rows(j, i, off):
-            a = y1_ring[slot(j, i)]
-            if off == 0:
-                v = a[:, 4 : 4 + 32 * DROW].rearrange("p (q e) -> p q e", e=DROW)
-                return v[:, :, 0:16]
-            if off > 0:
-                v = a[:, 4 : 4 + 32 * DROW].rearrange("p (q e) -> p q e", e=DROW)
-                return v[:, :, 1:17]
-            v = a[:, 0 : 32 * DROW].rearrange("p (q e) -> p q e", e=DROW)
-            return v[:, :, 3:19]
+        def y1_rows(j, off):
+            v = y1_ring[j % RING][:, 4 + off : 4 + off + 64 * DROW].rearrange("p (q e) -> p q e", e=DROW)
+            return v[:, :, 0:16]
 
         def rows(v):
             return v.rearrange("p (q d) -> p q d", d=16)
 
+        def slices(tile, first, count):
+            v = tile[:, 16 : 16 + 4 * WSLICE].rearrange("p (s r) -> p s r", r=WSLICE)
+            return v[:, first : first + count, 0:SLICE]
+
         def mac(dst, acc, src, c):
             nc.vector.scalar_tensor_tensor(out=dst, in0=src, scalar=c, in1=acc, op0=ALU.mult, op1=ALU.add)
 
-        def centre(j, i):
-            t = tiles_of(j)[i]
-            left, right = mb[(j, i)]
-            a = y1_rows(j, i, 0)
+        def centre(j):
+            b, s0, ns, t = steps[j]
+            banks = mb[j]
+            a = y1_rows(j, 0)
             c = c_h[:, 1, t : t + 1]
-            nc.scalar.activation(out=a[:, 0:16, :], in_=rows(left[:, SLICE:CHUNK]), func=ACTF.Copy, scale=c)
-            nc.scalar.activation(out=a[:, 16:32, :], in_=rows(right[:, 0:SLICE]), func=ACTF.Copy, scale=c)
+            nc.scalar.activation(out=a[:, 0:16, :], in_=rows(banks[0][:, SLICE:CHUNK]), func=ACTF.Copy, scale=c)
+            for k in range(1, ns // 2):
+                nc.scalar.activation(out=a[:, 32 * k - 16 : 32 * k + 16, :], in_=rows(banks[k][:]), func=ACTF.Copy, scale=c)
+            r = 16 * ns - 16
+            nc.scalar.activation(out=a[:, r : r + 16, :], in_=rows(banks[-1][:, 0:SLICE]), func=ACTF.Copy, scale=c)
 
-        def h_left(j, i):
-            t = tiles_of(j)[i]
-            left = mb[(j, i)][0]
-            a = y1_rows(j, i, 0)
+        def h_taps(j):
+            b, s0, ns, t = steps[j]
+            banks = mb[j]
+            a = y1_rows(j, 0)
             c = c_h[:, 0, t : t + 1]
-            if (j // 2) % 8 == 0:
-                mac(a[:, 16:32, :], a[:, 16:32, :], rows(left[:, SLICE:CHUNK]), c)
-            else:
-                mac(a, a, rows(left[:]), c)
-
-        def h_right(j, i):
-            t = tiles_of(j)[i]
-            right = mb[(j, i)][1]
-            a = y1_rows(j, i, 0)
-            c = c_h[:, 2, t : t + 1]
-            if (j // 2) % 8 == 7:
-                mac(a[:, 0:16, :], a[:, 0:16, :], rows(right[:, 0:SLICE]), c)
-            else:
-                mac(a, a, rows(right[:]), c)
-
-        def d_tap(j, i, k):
-            t = tiles_of(j)[i]
-            if k == 0:
-                a = y2p.tile([P, CHUNK], F32, align_bytes=64, name="y2")
-                y2[(j, i)] = a
-                mac(rows(a[:]), y1_rows(j, i, 0), y1_rows(j, i, -1), c_r[:, 0, t, 1:2])
-            else:
-                a = y2[(j, i)]
-                mac(rows(a[:]), rows(a[:]), y1_rows(j, i, 1), c_r[:, 1, t, 1:2])
-
-        def w_products(j, i):
-            t = tiles_of(j)[i]
-            src = y2[(j, i)][:].rearrange("p (s r) -> p s r", r=SLICE)
-            for k, ring in enumerate((pa_ring, pc_ring)):
-                dst = ring[slot(j, i)][:, 16 : 16 + 2 * WSLICE].rearrange("p (s r) -> p s r", r=WSLICE)
-                if k == 0:
-                    nc.gpsimd.tensor_scalar(
-                        out=dst[:, :, 0:SLICE],
-                        in0=src,
-                        scalar1=c_r[:, k, t, 0:1],
-                        scalar2=0.0,
-                        op0=ALU.mult,
-                        op1=ALU.add,
-                    )
+            for k in range(ns // 2):
+                lo, hi = 32 * k, 32 * k + 32
+                if k == 0 and s0 == 0:
+                    mac(a[:, 16:32, :], a[:, 16:32, :], rows(banks[0][:, SLICE:CHUNK]), c)
                 else:
-                    nc.scalar.activation(out=dst[:, :, 0:SLICE], in_=src, func=ACTF.Copy, scale=c_r[:, k, t, 0:1])
+                    mac(a[:, lo:hi, :], a[:, lo:hi, :], rows(banks[k][:]), c)
+            c = c_h[:, 2, t : t + 1]
+            for k in range(ns // 2):
+                lo, hi = 32 * k, 32 * k + 32
+                if k == ns // 2 - 1 and s0 + ns == 16:
+                    mac(a[:, lo : lo + 16, :], a[:, lo : lo + 16, :], rows(banks[k + 1][:, 0:SLICE]), c)
+                else:
+                    mac(a[:, lo:hi, :], a[:, lo:hi, :], rows(banks[k + 1][:]), c)
 
-        def w_sum(j, i):
+        def d_tap(j, k):
+            b, s0, ns, t = steps[j]
+            y2 = slices(y2_ring[j % RING], 0, ns).rearrange("p s (w d) -> p s w d", d=16)
+            off = -1 if k == 0 else 1
+            src = y1_rows(j, off)[:, 0 : 16 * ns, :].rearrange("p (s w) d -> p s w d", w=16)
+            acc = y1_rows(j, 0)[:, 0 : 16 * ns, :].rearrange("p (s w) d -> p s w d", w=16) if k == 0 else y2
+            mac(y2, acc, src, c_r[:, k, t, 1:2])
+
+        def scaled(ns):
+            return SCALED * ns // 4
+
+        def w_products(j):
+            b, s0, ns, t = steps[j]
+            dst = slices(pa_ring[j % RING], 0, ns)
+            src = slices(y2_ring[j % RING], 0, ns)
+            c = c_r[:, 0, t, 0:1]
+            if j >= n_steps - LATE:
+                nc.vector.tensor_scalar_mul(out=dst, in0=src, scalar1=c)
+            else:
+                nc.gpsimd.tensor_scalar(out=dst, in0=src, scalar1=c, scalar2=0.0, op0=ALU.mult, op1=ALU.add)
+            n = scaled(ns)
+            nc.scalar.activation(
+                out=slices(pc_ring[j % RING], n, ns - n),
+                in_=slices(y2_ring[j % RING], n, ns - n),
+                func=ACTF.Copy,
+                scale=c_r[:, 1, t, 0:1],
+            )
+
+        def w_sum(j, k):
+            b, s0, ns, t = steps[j]
             bank = tbp.tile([P, CHUNK], F32, name="tb")
-            pa = pa_ring[slot(j, i)]
-            pc = pc_ring[slot(j, i)]
+            y2 = y2_ring[j % RING]
+            pa = pa_ring[j % RING]
+            pc = pc_ring[j % RING]
             for q in range(4):
                 o = bank[:, q * P : (q + 1) * P]
-                base = 16 + (q // 2) * WSLICE + (q % 2) * P
-                parts = (y2[(j, i)][:, q * P : (q + 1) * P], pa[:, base - 16 : base - 16 + P], pc[:, base + 16 : base + 16 + P])
-                for k, part in enumerate(parts):
-                    nc.tensor.matmul(out=o, lhsT=part, rhs=ident[:], is_transpose=True, start=(k == 0), stop=(k == 2))
-            tb[(j, i)] = bank
+                s = 2 * k + q // 2
+                base = 16 + s * WSLICE + (q % 2) * P
+                nc.tensor.matmul(
+                    out=o, lhsT=y2[:, base : base + P], rhs=ident[:], is_transpose=True, start=True, stop=False
+                )
+                nc.tensor.matmul(
+                    out=o, lhsT=pa[:, base - 16 : base - 16 + P], rhs=ident[:], is_transpose=True, start=False, stop=False
+                )
+                if s < scaled(ns):
+                    nc.tensor.matmul(
+                        out=o, lhsT=y2[:, base + 16 : base + 16 + P], rhs=diag[:, t, :], start=False, stop=True
+                    )
+                else:
+                    nc.tensor.matmul(
+                        out=o, lhsT=pc[:, base + 16 : base + 16 + P], rhs=ident[:], is_transpose=True, start=False, stop=True
+                    )
+            tb[(j, k)] = bank
 
-        def round_y3(j, i):
-            c = j // 2
-            t = tiles_of(j)[i]
+        def round_y3(j, k):
+            b, s0, ns, t = steps[j]
+            c = 8 * b + s0 // 2 + k
             if c not in yt:
                 a = ytp.tile([P, 4, 512], BF16, align_bytes=64, name="yt")
                 yt[c] = a
-            nc.scalar.copy(
-                out=yt[c][:, :, t * P : (t + 1) * P], in_=tb[(j, i)][:].rearrange("p (q r) -> p q r", q=4)
-            )
+            dst = yt[c][:, :, t * P : (t + 1) * P]
+            src = tb[(j, k)][:].rearrange("p (q r) -> p q r", q=4)
+            if j >= n_steps - LATE and (j + k) % 2 == 0:
+                nc.vector.tensor_copy(out=dst, in_=src)
+            else:
+                nc.scalar.copy(out=dst, in_=src)
 
         def turn_y3(c, k):
             bank = wop.tile([P, CHUNK], F32, name="wo")
@@ -322,14 +344,18 @@ def tile_lowrankconv3d_t_kernel(tc, x, U_kh, U_kw, U_kd, U_c_in, U_c_out, bias, 
         nc.scalar.dma_start(out=k_rows[6:9, :], in_=U_kd)
         load_x(1, 1)
         load_x(2, 2)
+        load_x(4, 2)
         with nc.allow_non_contiguous_dma(reason="256 bias values, one per partition and output tile"):
             nc.scalar.dma_start(out=bias_b[:], in_=bias.rearrange("(j p) -> p j", p=P))
         nc.scalar.dma_start(out=v_raw[:], in_=U_c_out.rearrange("(p j) o -> p j o", j=4))
         make_identity(nc, ident[:])
         for n in range(RING):
             nc.gpsimd.memset(y1_ring[n][:], 0.0)
-            nc.gpsimd.memset(pa_ring[n][:], 0.0)
-            nc.gpsimd.memset(pc_ring[n][:], 0.0)
+            for ring in (y2_ring, pa_ring, pc_ring):
+                nc.gpsimd.memset(ring[n][:, 0:16], 0.0)
+                nc.gpsimd.memset(
+                    ring[n][:, 16 : 16 + 4 * WSLICE].rearrange("p (s r) -> p s r", r=WSLICE)[:, :, SLICE:WSLICE], 0.0
+                )
 
         nc.vector.tensor_copy(out=ident_b[:], in_=ident[:, 0:16])
         for u in range(2):
@@ -364,66 +390,92 @@ def tile_lowrankconv3d_t_kernel(tc, x, U_kh, U_kw, U_kd, U_c_in, U_c_out, bias, 
             nc.vector.tensor_tensor(out=c_h[:, k, :], in0=cf[:, :, k], in1=c_pp[:], op=ALU.mult)
         for k in range(2):
             nc.vector.tensor_tensor(out=c_r[:, k], in0=taps[:, :, :, 2 * k], in1=c_rec[:], op=ALU.mult)
+        for t in range(4):
+            nc.gpsimd.tensor_scalar(
+                out=diag[:, t, :], in0=ident[:], scalar1=c_r[:, 1, t, 0:1], scalar2=0.0, op0=ALU.mult, op1=ALU.add
+            )
         quant_x(0, 1, 1)
         regroup_x(1, 0, "v")
-        regroup_w(1)
-        quant_x(1, 0, 1)
-        quant_w(1)
         regroup_x(1, 1, "a")
-        regroup_x(2, 0, "a")
-        regroup_x(2, 1, "a")
+        quant_x(1, 0, 1)
+        regroup_w(1)
+        quant_w(1)
+        quant_x(1, 1, 1)
 
-        for j in range(-1, N_STEPS + 5):
-            if j >= 0 and j % 4 == 0 and j // 2 + 4 < N_CHUNKS:
-                load_x(j // 2 + 4, 2)
-            if 0 <= j - 1 < N_STEPS:
-                for i in range(2):
-                    w_products(j - 1, i)
-                w_sum(j - 1, 0)
-                round_y3(j - 1, 0)
-            if 0 <= j < N_STEPS:
-                for i in range(2):
-                    h_left(j, i)
-                for i in range(2):
-                    h_right(j, i)
-            if j + 1 < N_STEPS:
-                mm1(j + 1)
-                for i in range(2):
-                    centre(j + 1, i)
-            if 0 <= j < N_STEPS:
-                for i in range(2):
-                    d_tap(j, i, 0)
+        first_use = {}
+        complete = {}
+        for j, (b, s0, ns, t) in enumerate(steps):
+            for s in range(max(s0 - 1, 0), min(s0 + ns + 1, 16)):
+                first_use.setdefault(8 * b + s // 2, j)
+            for k in range(ns // 2):
+                complete[8 * b + s0 // 2 + k] = j
+        x_step = {}
+        for c in reversed(range(2, N_CHUNKS)):
+            at = first_use[c] - 2
+            x_step[c] = min(at, x_step[c + 1] - 2) if c + 1 in x_step else at
+        y_step = {}
+        for c in range(N_CHUNKS):
+            at = complete[c] + 3
+            y_step[c] = max(at, y_step[c - 1] + 2) if c else at
+        x_quant = {max(at, -1): [] for at in x_step.values()}
+        x_half = {}
+        for c in range(2, N_CHUNKS):
+            at = x_step[c]
+            x_quant[max(at, -1)].append(c)
+            for side in range(2):
+                x_half.setdefault(max(at - 2 + side, -1), []).append((c, side))
+        y_turn = {}
+        y_quant = {}
+        for c in range(N_CHUNKS):
+            y_turn.setdefault(y_step[c], []).append(c)
+            y_quant.setdefault(y_step[c] + 2, []).append(c)
+
+        for j in range(-1, n_steps + 7):
+            for c, side in x_half.get(j + 4, []) if j >= 0 else []:
+                if side == 0 and c % 2 == 0 and c > 7:
+                    load_x(c, 2)
             if j == -1:
-                quant_x(1, 1, 1)
-                regroup_w(2)
-                regroup_w(3)
-                quant_w(2)
-                quant_w(3)
+                load_x(6, 2)
+                for c, side in x_half.get(-1, []):
+                    regroup_x(c, side, "a")
+            if 0 <= j - 2 < n_steps:
+                w_products(j - 2)
+            if 0 <= j < n_steps:
+                h_taps(j)
+            if j + 1 < n_steps:
+                mm1(j + 1)
+                centre(j + 1)
+            if j == -1:
+                for t in (2, 3):
+                    regroup_w(t)
+                    quant_w(t)
                 nc.vector.tensor_copy(out=v_grp[:], in_=v_raw[:].rearrange("p j o -> p o j"))
-                quant_x(2, 0, 2)
                 nc.vector.tensor_copy(out=bias_f[:], in_=bias_b[:])
                 nc.vector.quantize_mx(
                     out=vq[:].bitcast(FP8X4), scales=vs[:], in_=v_grp[:].rearrange("p o j -> p (o j)")
                 )
-            if j % 2 == 1 and j >= 1 and (j + 5) // 2 < N_CHUNKS:
-                quant_x((j + 5) // 2, 0, 2)
-            if j % 2 == 0 and 0 <= j // 2 - 2 < N_CHUNKS:
-                quant_y(j // 2 - 2)
-            if 0 <= j < N_STEPS:
-                for i in range(2):
-                    d_tap(j, i, 1)
-            if 0 <= j - 1 < N_STEPS:
-                w_sum(j - 1, 1)
-                round_y3(j - 1, 1)
-            if (j + 7) // 2 < N_CHUNKS and j >= -1:
-                regroup_x((j + 7) // 2, (j + 7) % 2, "a")
-            if j % 2 == 0 and 0 <= j // 2 - 2 < N_CHUNKS:
+            for c in x_quant.get(j, []):
+                quant_x(c, 0, 2)
+            for c in y_quant.get(j, []):
+                quant_y(c)
+            if 0 <= j - 1 < n_steps:
+                d_tap(j - 1, 1)
+            if 0 <= j < n_steps:
+                d_tap(j, 0)
+            if 0 <= j - 2 < n_steps:
+                for k in range(steps[j - 2][2] // 2):
+                    w_sum(j - 2, k)
+                    round_y3(j - 2, k)
+            if j >= 0:
+                for c, side in x_half.get(j, []):
+                    regroup_x(c, side, "a")
+            for c in y_quant.get(j, []):
                 for ot in range(2):
-                    mm2(j // 2 - 2, ot)
+                    mm2(c, ot)
                 for ot in range(2):
-                    evac(j // 2 - 2, ot, "a")
-            if j % 2 == 1 and 0 <= (j - 3) // 2 < N_CHUNKS:
+                    evac(c, ot, "v" if c == N_CHUNKS - 1 and ot == 1 else "a")
+            for c in y_turn.get(j, []):
                 for k in range(2):
-                    turn_y3((j - 3) // 2, k)
+                    turn_y3(c, k)
                 for k in range(2):
-                    gather_y3((j - 3) // 2, k, "a")
+                    gather_y3(c, k, "v" if c == N_CHUNKS - 1 and k == 1 else "a")

@@ -21,9 +21,10 @@ N_CHUNKS = 16
 GROUPS = ((2, 2, 4, 4, 4), (4, 4, 4, 2, 2))
 DROW = 20
 WSLICE = 272
-RING = 4
+RING = 6
+P_RING = 4
 LATE = 2
-SCALED = 2
+G_COLS = 128
 
 
 def tile_lowrankconv3d_t_kernel(tc, x, U_kh, U_kw, U_kd, U_c_in, U_c_out, bias, out):
@@ -33,9 +34,11 @@ def tile_lowrankconv3d_t_kernel(tc, x, U_kh, U_kw, U_kd, U_c_in, U_c_out, bias, 
 
     with ExitStack() as ctx:
         const = ctx.enter_context(tc.tile_pool(name="const", bufs=1))
-        rawp = ctx.enter_context(tc.tile_pool(name="rawp", bufs=5))
+        rawp = ctx.enter_context(tc.tile_pool(name="rawp", bufs=3))
+        headp = ctx.enter_context(tc.tile_pool(name="headp", bufs=2))
         xgp = ctx.enter_context(tc.tile_pool(name="xgp", bufs=3))
-        ytp = ctx.enter_context(tc.tile_pool(name="ytp", bufs=4))
+        y2p = ctx.enter_context(tc.tile_pool(name="y2p", bufs=RING))
+        ytp = ctx.enter_context(tc.tile_pool(name="ytp", bufs=3))
         ygp = ctx.enter_context(tc.tile_pool(name="ygp", bufs=2))
         yqp = ctx.enter_context(tc.tile_pool(name="yqp", bufs=2))
         osp = ctx.enter_context(tc.tile_pool(name="osp", bufs=6))
@@ -66,18 +69,16 @@ def tile_lowrankconv3d_t_kernel(tc, x, U_kh, U_kw, U_kd, U_c_in, U_c_out, bias, 
         c_pp = const.tile([P, 4], F32, name="c_pp")
         c_h = const.tile([P, 3, 4], F32, name="c_h")
         c_r = const.tile([P, 2, 4, 2], F32, name="c_r")
+        warm = const.tile([P, 1], F32, name="warm")
         bias_b = const.tile([P, 2], BF16, name="bias_b")
         bias_f = const.tile([P, 2], F32, name="bias_f")
-        diag = const.tile([P, 4, P], F32, align_bytes=64, name="diag")
         y1_ring = []
-        y2_ring = []
         pa_ring = []
         pc_ring = []
         for n in range(RING):
             a = const.tile([P, 8 + 64 * DROW], F32, align_bytes=64, name=f"y1_{n}")
             y1_ring.append(a)
-            a = const.tile([P, 16 + 4 * WSLICE], F32, align_bytes=64, name=f"y2_{n}")
-            y2_ring.append(a)
+        for n in range(P_RING):
             a = const.tile([P, 16 + 4 * WSLICE], F32, align_bytes=64, name=f"pa_{n}")
             pa_ring.append(a)
             a = const.tile([P, 16 + 4 * WSLICE], F32, align_bytes=64, name=f"pc_{n}")
@@ -86,6 +87,7 @@ def tile_lowrankconv3d_t_kernel(tc, x, U_kh, U_kw, U_kd, U_c_in, U_c_out, bias, 
         raw = {}
         xg = {}
         mb = {}
+        y2 = {}
         yt = {}
         wb = {}
         tb = {}
@@ -96,20 +98,25 @@ def tile_lowrankconv3d_t_kernel(tc, x, U_kh, U_kw, U_kd, U_c_in, U_c_out, bias, 
 
         def load_x(c0, n):
             b, cc = divmod(c0, 8)
-            r = rawp.tile([P, 4, 2 * CHUNK], BF16, name="raw")
+            if n == 1:
+                r = headp.tile([P, 4, CHUNK], BF16, name="raw_head")
+            else:
+                r = rawp.tile([P, 4, 2 * CHUNK], BF16, name="raw")
             nc.sync.dma_start(out=r[:, :, 0 : n * CHUNK], in_=xv[b][:, :, cc * CHUNK : (cc + n) * CHUNK])
             for k in range(n):
                 raw[c0 + k] = r[:, :, k * CHUNK : (k + 1) * CHUNK]
 
-        def regroup_x(c, side, eng):
+        def regroup_x(c, side, first, count, eng):
             if c not in xg:
                 g = xgp.tile([P, CHUNK, 4], BF16, align_bytes=64, name="xg")
                 xg[c] = g
-            lo = side * SLICE
-            src = raw[c][:, :, lo : lo + SLICE].rearrange("p t (c i) -> p c t i", i=4)
-            dst = xg[c][:, lo : lo + SLICE, :].rearrange("p (c i) t -> p c t i", i=4)
+            lo = side * SLICE + first
+            src = raw[c][:, :, lo : lo + count].rearrange("p t (c i) -> p c t i", i=4)
+            dst = xg[c][:, lo : lo + count, :].rearrange("p (c i) t -> p c t i", i=4)
             if eng == "v":
                 nc.vector.tensor_copy(out=dst, in_=src)
+            elif eng == "g":
+                nc.gpsimd.tensor_scalar(out=dst, in0=src, scalar1=1.0, scalar2=0.0, op0=ALU.mult, op1=ALU.add)
             else:
                 nc.scalar.copy(out=dst, in_=src)
 
@@ -122,12 +129,14 @@ def tile_lowrankconv3d_t_kernel(tc, x, U_kh, U_kw, U_kd, U_c_in, U_c_out, bias, 
                 in_=xg[c][:, first * SLICE : first * SLICE + n, :].rearrange("p w j -> p (w j)"),
             )
 
-        def regroup_w(t):
+        def regroup_w(t, eng):
             u, h = divmod(t, 2)
-            nc.vector.tensor_copy(
-                out=w_grp[:, t * P : (t + 1) * P, :].rearrange("p (m e) j -> p m e j", e=2),
-                in_=w_raw[:].rearrange("p j (h m u e) -> p h u m e j", h=2, u=2, e=2)[:, h, u],
-            )
+            dst = w_grp[:, t * P : (t + 1) * P, :].rearrange("p (m e) j -> p m e j", e=2)
+            src = w_raw[:].rearrange("p j (h m u e) -> p h u m e j", h=2, u=2, e=2)[:, h, u]
+            if eng == "v":
+                nc.vector.tensor_copy(out=dst, in_=src)
+            else:
+                nc.scalar.copy(out=dst, in_=src)
 
         def quant_w(t):
             nc.vector.quantize_mx(
@@ -137,12 +146,17 @@ def tile_lowrankconv3d_t_kernel(tc, x, U_kh, U_kw, U_kd, U_c_in, U_c_out, bias, 
             )
 
         steps = []
+        moves = []
         for b in range(2):
             s0 = 0
             for n in GROUPS[b]:
                 for t in range(4):
+                    if n == 4 or t % 2 == 0:
+                        moves.append([])
+                    moves[-1].append(len(steps))
                     steps.append((b, s0, n, t))
                 s0 += n
+        n_moves = len(moves)
         n_steps = len(steps)
 
         def mm1(j):
@@ -193,76 +207,58 @@ def tile_lowrankconv3d_t_kernel(tc, x, U_kh, U_kw, U_kd, U_c_in, U_c_out, bias, 
             r = 16 * ns - 16
             nc.scalar.activation(out=a[:, r : r + 16, :], in_=rows(banks[-1][:, 0:SLICE]), func=ACTF.Copy, scale=c)
 
-        def h_taps(j):
+        def h_tap(j, side):
             b, s0, ns, t = steps[j]
             banks = mb[j]
             a = y1_rows(j, 0)
-            c = c_h[:, 0, t : t + 1]
+            c = c_h[:, 2 * side, t : t + 1]
             for k in range(ns // 2):
                 lo, hi = 32 * k, 32 * k + 32
-                if k == 0 and s0 == 0:
+                if side == 0 and k == 0 and s0 == 0:
                     mac(a[:, 16:32, :], a[:, 16:32, :], rows(banks[0][:, SLICE:CHUNK]), c)
-                else:
-                    mac(a[:, lo:hi, :], a[:, lo:hi, :], rows(banks[k][:]), c)
-            c = c_h[:, 2, t : t + 1]
-            for k in range(ns // 2):
-                lo, hi = 32 * k, 32 * k + 32
-                if k == ns // 2 - 1 and s0 + ns == 16:
+                elif side == 1 and k == ns // 2 - 1 and s0 + ns == 16:
                     mac(a[:, lo : lo + 16, :], a[:, lo : lo + 16, :], rows(banks[k + 1][:, 0:SLICE]), c)
                 else:
-                    mac(a[:, lo:hi, :], a[:, lo:hi, :], rows(banks[k + 1][:]), c)
+                    mac(a[:, lo:hi, :], a[:, lo:hi, :], rows(banks[k + side][:]), c)
 
         def d_tap(j, k):
             b, s0, ns, t = steps[j]
-            y2 = slices(y2_ring[j % RING], 0, ns).rearrange("p s (w d) -> p s w d", d=16)
-            off = -1 if k == 0 else 1
-            src = y1_rows(j, off)[:, 0 : 16 * ns, :].rearrange("p (s w) d -> p s w d", w=16)
-            acc = y1_rows(j, 0)[:, 0 : 16 * ns, :].rearrange("p (s w) d -> p s w d", w=16) if k == 0 else y2
-            mac(y2, acc, src, c_r[:, k, t, 1:2])
-
-        def scaled(ns):
-            return SCALED * ns // 4
+            if k == 0:
+                a = y2p.tile([P, 4 * SLICE], F32, align_bytes=64, name="y2")
+                y2[j] = a
+            v = rows(y2[j][:, 0 : ns * SLICE])
+            acc = y1_rows(j, 0)[:, 0 : 16 * ns, :] if k == 0 else v
+            mac(v, acc, y1_rows(j, -1 if k == 0 else 1)[:, 0 : 16 * ns, :], c_r[:, k, t, 1:2])
 
         def w_products(j):
             b, s0, ns, t = steps[j]
-            dst = slices(pa_ring[j % RING], 0, ns)
-            src = slices(y2_ring[j % RING], 0, ns)
+            src = y2[j][:, 0 : ns * SLICE].rearrange("p (s r) -> p s r", r=SLICE)
+            dst = slices(pa_ring[j % P_RING], 0, ns)
             c = c_r[:, 0, t, 0:1]
             if j >= n_steps - LATE:
                 nc.vector.tensor_scalar_mul(out=dst, in0=src, scalar1=c)
             else:
                 nc.gpsimd.tensor_scalar(out=dst, in0=src, scalar1=c, scalar2=0.0, op0=ALU.mult, op1=ALU.add)
-            n = scaled(ns)
-            nc.scalar.activation(
-                out=slices(pc_ring[j % RING], n, ns - n),
-                in_=slices(y2_ring[j % RING], n, ns - n),
-                func=ACTF.Copy,
-                scale=c_r[:, 1, t, 0:1],
-            )
+            dst = slices(pc_ring[j % P_RING], 0, ns)
+            nc.scalar.activation(out=dst, in_=src, func=ACTF.Copy, scale=c_r[:, 1, t, 0:1])
 
         def w_sum(j, k):
-            b, s0, ns, t = steps[j]
             bank = tbp.tile([P, CHUNK], F32, name="tb")
-            y2 = y2_ring[j % RING]
-            pa = pa_ring[j % RING]
-            pc = pc_ring[j % RING]
+            pa = pa_ring[j % P_RING]
+            pc = pc_ring[j % P_RING]
             for q in range(4):
-                o = bank[:, q * P : (q + 1) * P]
                 s = 2 * k + q // 2
+                flat = s * SLICE + (q % 2) * P
                 base = 16 + s * WSLICE + (q % 2) * P
-                nc.tensor.matmul(
-                    out=o, lhsT=y2[:, base : base + P], rhs=ident[:], is_transpose=True, start=True, stop=False
-                )
-                nc.tensor.matmul(
-                    out=o, lhsT=pa[:, base - 16 : base - 16 + P], rhs=ident[:], is_transpose=True, start=False, stop=False
-                )
-                if s < scaled(ns):
+                parts = (y2[j][:, flat : flat + P], pa[:, base - 16 : base - 16 + P], pc[:, base + 16 : base + 16 + P])
+                for i, part in enumerate(parts):
                     nc.tensor.matmul(
-                        out=o, lhsT=y2[:, base + 16 : base + 16 + P], rhs=diag[:, t, :], start=False, stop=True
-                    )
-                else:
-                    nc.tensor.matmul(
-                        out=o, lhsT=pc[:, base + 16 : base + 16 + P], rhs=ident[:], is_transpose=True, start=False, stop=True
+                        out=bank[:, q * P : (q + 1) * P],
+                        lhsT=part,
+                        rhs=ident[:],
+                        is_transpose=True,
+                        start=(i == 0),
+                        stop=(i == 2),
                     )
             tb[(j, k)] = bank
 
@@ -274,7 +270,7 @@ def tile_lowrankconv3d_t_kernel(tc, x, U_kh, U_kw, U_kd, U_c_in, U_c_out, bias, 
                 yt[c] = a
             dst = yt[c][:, :, t * P : (t + 1) * P]
             src = tb[(j, k)][:].rearrange("p (q r) -> p q r", q=4)
-            if j >= n_steps - LATE and (j + k) % 2 == 0:
+            if j >= n_steps - 2 * LATE and j % 2 == 0:
                 nc.vector.tensor_copy(out=dst, in_=src)
             else:
                 nc.scalar.copy(out=dst, in_=src)
@@ -337,145 +333,163 @@ def tile_lowrankconv3d_t_kernel(tc, x, U_kh, U_kw, U_kd, U_c_in, U_c_out, bias, 
             nc.sync.dma_start(out=ov[b][ot * P : (ot + 1) * P, cc * CHUNK : (cc + 1) * CHUNK], in_=o[:])
 
         nc.vector.memset(k_rows[:], 0.0)
+        with tc.high_priority():
+            nc.sync.dma_start(out=k_rows[0:3, :], in_=U_kh)
+            nc.sync.dma_start(out=k_rows[3:6, :], in_=U_kw)
+            nc.sync.dma_start(out=k_rows[6:9, :], in_=U_kd)
+            nc.vector.memset(warm[:], 0.0)
+            nc.scalar.copy(out=bias_f[:, 0:1], in_=warm[:])
+            make_identity(nc, ident[:])
         load_x(0, 1)
         nc.sync.dma_start(out=w_raw[:], in_=U_c_in.rearrange("(p j) r -> p j r", j=4))
-        nc.scalar.dma_start(out=k_rows[0:3, :], in_=U_kh)
-        nc.scalar.dma_start(out=k_rows[3:6, :], in_=U_kw)
-        nc.scalar.dma_start(out=k_rows[6:9, :], in_=U_kd)
         load_x(1, 1)
         load_x(2, 2)
         load_x(4, 2)
         with nc.allow_non_contiguous_dma(reason="256 bias values, one per partition and output tile"):
             nc.scalar.dma_start(out=bias_b[:], in_=bias.rearrange("(j p) -> p j", p=P))
         nc.scalar.dma_start(out=v_raw[:], in_=U_c_out.rearrange("(p j) o -> p j o", j=4))
-        make_identity(nc, ident[:])
         for n in range(RING):
             nc.gpsimd.memset(y1_ring[n][:], 0.0)
-            for ring in (y2_ring, pa_ring, pc_ring):
+        for n in range(P_RING):
+            for ring in (pa_ring, pc_ring):
                 nc.gpsimd.memset(ring[n][:, 0:16], 0.0)
                 nc.gpsimd.memset(
                     ring[n][:, 16 : 16 + 4 * WSLICE].rearrange("p (s r) -> p s r", r=WSLICE)[:, :, SLICE:WSLICE], 0.0
                 )
 
-        nc.vector.tensor_copy(out=ident_b[:], in_=ident[:, 0:16])
-        for u in range(2):
-            nc.vector.tensor_copy(
-                out=k_perm[:, 2 * u : 2 * u + 2, :].rearrange("p h (m e) -> p h m e", e=2),
-                in_=k_rows[:].rearrange("p (h m u e) -> p u h m e", h=2, u=2, e=2)[:, u],
+        with tc.high_priority():
+            nc.vector.tensor_copy(out=ident_b[:], in_=ident[:, 0:16])
+            for u in range(2):
+                nc.vector.tensor_copy(
+                    out=k_perm[:, 2 * u : 2 * u + 2, :].rearrange("p h (m e) -> p h m e", e=2),
+                    in_=k_rows[:].rearrange("p (h m u e) -> p u h m e", h=2, u=2, e=2)[:, u],
+                )
+            k_bank = wop.tile([P, 4, 16], F32, name="wo")
+            for t in range(4):
+                nc.tensor.matmul(k_bank[:, t, :], lhsT=k_perm[:, t, :], rhs=ident_b[:], start=True, stop=True)
+            nc.vector.tensor_copy(out=cf[:], in_=k_bank[:])
+            taps = cf[:, :, 3:9].rearrange("p t (a k) -> p t a k", k=3)
+            flat = cf[:, :, 3:9]
+            nc.vector.scalar_tensor_tensor(
+                out=c_abs[:].rearrange("p t a k -> p t (a k)"), in0=flat, scalar=-1.0, in1=flat, op0=ALU.mult, op1=ALU.max
             )
-        k_bank = wop.tile([P, 4, 16], F32, name="wo")
-        for t in range(4):
-            nc.tensor.matmul(k_bank[:, t, :], lhsT=k_perm[:, t, :], rhs=ident_b[:], start=True, stop=True)
-        nc.vector.tensor_copy(out=cf[:], in_=k_bank[:])
-        regroup_x(0, 0, "v")
-        regroup_x(0, 1, "a")
-        regroup_w(0)
+            nc.vector.tensor_reduce(out=c_max[:], in_=c_abs[:], op=ALU.max, axis=AX.X)
+            nc.vector.tensor_scalar(
+                out=c_max[:], in0=c_max[:], scalar1=2.0**-32, scalar2=2.0**-100, op0=ALU.mult, op1=ALU.add
+            )
+            nc.vector.tensor_tensor(out=c_small[:], in0=c_abs[:, :, :, 1], in1=c_max[:], op=ALU.is_lt)
+            nc.vector.scalar_tensor_tensor(
+                out=c_small[:], in0=c_small[:], scalar=2.0, in1=c_max[:], op0=ALU.mult, op1=ALU.mult
+            )
+            nc.vector.tensor_tensor(out=c_piv[:], in0=taps[:, :, :, 1], in1=c_small[:], op=ALU.add)
+            nc.vector.reciprocal(out=c_rec[:], in_=c_piv[:])
+            nc.vector.tensor_tensor(out=c_pp[:], in0=c_piv[:, :, 0], in1=c_piv[:, :, 1], op=ALU.mult)
+            for k in (1, 0, 2):
+                nc.vector.tensor_tensor(out=c_h[:, k, :], in0=cf[:, :, k], in1=c_pp[:], op=ALU.mult)
+            for k in range(2):
+                nc.vector.tensor_tensor(out=c_r[:, k], in0=taps[:, :, :, 2 * k], in1=c_rec[:], op=ALU.mult)
+        regroup_x(0, 0, 0, SLICE, "v")
+        regroup_x(0, 1, 0, SLICE, "a")
+        regroup_w(0, "v")
         quant_x(0, 0, 1)
         quant_w(0)
-        taps = cf[:, :, 3:9].rearrange("p t (a k) -> p t a k", k=3)
-        nc.vector.tensor_scalar_mul(out=c_abs[:], in0=taps, scalar1=-1.0)
-        nc.vector.tensor_tensor(out=c_abs[:], in0=c_abs[:], in1=taps, op=ALU.max)
-        nc.vector.tensor_reduce(out=c_max[:], in_=c_abs[:], op=ALU.max, axis=AX.X)
-        nc.vector.tensor_scalar(
-            out=c_max[:], in0=c_max[:], scalar1=2.0**-32, scalar2=2.0**-100, op0=ALU.mult, op1=ALU.add
-        )
-        nc.vector.tensor_tensor(out=c_small[:], in0=c_abs[:, :, :, 1], in1=c_max[:], op=ALU.is_lt)
-        nc.vector.scalar_tensor_tensor(
-            out=c_small[:], in0=c_small[:], scalar=2.0, in1=c_max[:], op0=ALU.mult, op1=ALU.mult
-        )
-        nc.vector.tensor_tensor(out=c_piv[:], in0=taps[:, :, :, 1], in1=c_small[:], op=ALU.add)
-        nc.vector.reciprocal(out=c_rec[:], in_=c_piv[:])
-        nc.vector.tensor_tensor(out=c_pp[:], in0=c_piv[:, :, 0], in1=c_piv[:, :, 1], op=ALU.mult)
-        for k in (1, 0, 2):
-            nc.vector.tensor_tensor(out=c_h[:, k, :], in0=cf[:, :, k], in1=c_pp[:], op=ALU.mult)
-        for k in range(2):
-            nc.vector.tensor_tensor(out=c_r[:, k], in0=taps[:, :, :, 2 * k], in1=c_rec[:], op=ALU.mult)
-        for t in range(4):
-            nc.gpsimd.tensor_scalar(
-                out=diag[:, t, :], in0=ident[:], scalar1=c_r[:, 1, t, 0:1], scalar2=0.0, op0=ALU.mult, op1=ALU.add
-            )
         quant_x(0, 1, 1)
-        regroup_x(1, 0, "v")
-        regroup_x(1, 1, "a")
+        regroup_x(1, 0, 0, SLICE, "a")
+        regroup_w(1, "a")
         quant_x(1, 0, 1)
-        regroup_w(1)
         quant_w(1)
-        quant_x(1, 1, 1)
+        regroup_x(1, 1, 0, SLICE, "a")
 
         first_use = {}
         complete = {}
-        for j, (b, s0, ns, t) in enumerate(steps):
-            for s in range(max(s0 - 1, 0), min(s0 + ns + 1, 16)):
-                first_use.setdefault(8 * b + s // 2, j)
-            for k in range(ns // 2):
-                complete[8 * b + s0 // 2 + k] = j
+        for m, js in enumerate(moves):
+            for j in js:
+                b, s0, ns, t = steps[j]
+                for s in range(max(s0 - 1, 0), min(s0 + ns + 1, 16)):
+                    first_use.setdefault(8 * b + s // 2, m)
+                for k in range(ns // 2):
+                    complete[8 * b + s0 // 2 + k] = m
         x_step = {}
         for c in reversed(range(2, N_CHUNKS)):
             at = first_use[c] - 2
-            x_step[c] = min(at, x_step[c + 1] - 2) if c + 1 in x_step else at
+            x_step[c] = max(min(at, x_step[c + 1] - 2), c - 2) if c + 1 in x_step else at
         y_step = {}
         for c in range(N_CHUNKS):
             at = complete[c] + 3
-            y_step[c] = max(at, y_step[c - 1] + 2) if c else at
-        x_quant = {max(at, -1): [] for at in x_step.values()}
+            y_step[c] = max(at, y_step[c - 1] + (2 if c < 13 else 1)) if c else at
+        x_quant = {}
         x_half = {}
         for c in range(2, N_CHUNKS):
             at = x_step[c]
-            x_quant[max(at, -1)].append(c)
+            x_quant.setdefault(max(at, -1), []).append(c)
             for side in range(2):
                 x_half.setdefault(max(at - 2 + side, -1), []).append((c, side))
         y_turn = {}
         y_quant = {}
         for c in range(N_CHUNKS):
             y_turn.setdefault(y_step[c], []).append(c)
-            y_quant.setdefault(y_step[c] + 2, []).append(c)
+            y_quant.setdefault(y_step[c] + (2 if c < 13 else 1), []).append(c)
 
-        for j in range(-1, n_steps + 7):
-            for c, side in x_half.get(j + 4, []) if j >= 0 else []:
+        def regroup_shared(c, side):
+            g = G_COLS if c > 3 else 0
+            if g:
+                regroup_x(c, side, 0, g, "g")
+            regroup_x(c, side, g, SLICE - g, "a")
+
+        load_x(6, 2)
+        for m in range(-1, n_moves + 7):
+            for c, side in x_half.get(m + 4, []) if m >= 0 else []:
                 if side == 0 and c % 2 == 0 and c > 7:
                     load_x(c, 2)
-            if j == -1:
-                load_x(6, 2)
+            if m == -1:
                 for c, side in x_half.get(-1, []):
-                    regroup_x(c, side, "a")
-            if 0 <= j - 2 < n_steps:
-                w_products(j - 2)
-            if 0 <= j < n_steps:
-                h_taps(j)
-            if j + 1 < n_steps:
-                mm1(j + 1)
-                centre(j + 1)
-            if j == -1:
+                    regroup_shared(c, side)
+            if 0 <= m - 2 < n_moves:
+                for j in moves[m - 2]:
+                    w_products(j)
+            if 0 <= m < n_moves:
+                for side in range(2):
+                    for j in moves[m]:
+                        h_tap(j, side)
+            if m + 1 < n_moves:
+                for j in moves[m + 1]:
+                    mm1(j)
+                    centre(j)
+            if m == -1:
                 for t in (2, 3):
-                    regroup_w(t)
+                    regroup_w(t, "a")
                     quant_w(t)
-                nc.vector.tensor_copy(out=v_grp[:], in_=v_raw[:].rearrange("p j o -> p o j"))
-                nc.vector.tensor_copy(out=bias_f[:], in_=bias_b[:])
+                quant_x(1, 1, 1)
+                nc.scalar.copy(out=v_grp[:], in_=v_raw[:].rearrange("p j o -> p o j"))
+                nc.scalar.copy(out=bias_f[:], in_=bias_b[:])
                 nc.vector.quantize_mx(
                     out=vq[:].bitcast(FP8X4), scales=vs[:], in_=v_grp[:].rearrange("p o j -> p (o j)")
                 )
-            for c in x_quant.get(j, []):
+            for c in x_quant.get(m, []):
                 quant_x(c, 0, 2)
-            for c in y_quant.get(j, []):
+            for c in y_quant.get(m, []):
                 quant_y(c)
-            if 0 <= j - 1 < n_steps:
-                d_tap(j - 1, 1)
-            if 0 <= j < n_steps:
-                d_tap(j, 0)
-            if 0 <= j - 2 < n_steps:
-                for k in range(steps[j - 2][2] // 2):
-                    w_sum(j - 2, k)
-                    round_y3(j - 2, k)
-            if j >= 0:
-                for c, side in x_half.get(j, []):
-                    regroup_x(c, side, "a")
-            for c in y_quant.get(j, []):
+            if 0 <= m - 1 < n_moves:
+                for j in moves[m - 1]:
+                    d_tap(j, 1)
+            if 0 <= m < n_moves:
+                for j in moves[m]:
+                    d_tap(j, 0)
+            if 0 <= m - 2 < n_moves:
+                for j in moves[m - 2]:
+                    for k in range(steps[j][2] // 2):
+                        w_sum(j, k)
+                        round_y3(j, k)
+            if m >= 0:
+                for c, side in x_half.get(m, []):
+                    regroup_shared(c, side)
+            for c in y_quant.get(m, []):
                 for ot in range(2):
                     mm2(c, ot)
                 for ot in range(2):
-                    evac(c, ot, "v" if c == N_CHUNKS - 1 and ot == 1 else "a")
-            for c in y_turn.get(j, []):
+                    evac(c, ot, "v" if c >= N_CHUNKS - 2 and ot == 1 else "a")
+            for c in y_turn.get(m, []):
                 for k in range(2):
                     turn_y3(c, k)
                 for k in range(2):
-                    gather_y3(c, k, "v" if c == N_CHUNKS - 1 and k == 1 else "a")
+                    gather_y3(c, k, "v" if c >= N_CHUNKS - 2 and k == 1 else "a")

@@ -431,65 +431,66 @@ def tile_lowrankconv3d_t_kernel(tc, x, U_kh, U_kw, U_kd, U_c_in, U_c_out, bias, 
             y_quant.setdefault(y_step[c] + (2 if c < 13 else 1), []).append(c)
 
         def regroup_shared(c, side):
-            g = G_COLS if c > 3 else 0
+            g = 0
             if g:
                 regroup_x(c, side, 0, g, "g")
             regroup_x(c, side, g, SLICE - g, "a")
 
-        load_x(6, 2)
-        for m in range(-1, n_moves + 7):
-            for c, side in x_half.get(m + 4, []) if m >= 0 else []:
-                if side == 0 and c % 2 == 0 and c > 7:
-                    load_x(c, 2)
-            if m == -1:
-                for c, side in x_half.get(-1, []):
-                    regroup_shared(c, side)
-            if 0 <= m - 2 < n_moves:
-                for j in moves[m - 2]:
-                    w_products(j)
-            if 0 <= m < n_moves:
-                for side in range(2):
+        with tc.manual_schedule(engines={mybir.EngineType.DVE, mybir.EngineType.Pool}):
+            load_x(6, 2)
+            for m in range(-1, n_moves + 7):
+                for c, side in x_half.get(m + 4, []) if m >= 0 else []:
+                    if side == 0 and c % 2 == 0 and c > 7:
+                        load_x(c, 2)
+                if m == -1:
+                    for c, side in x_half.get(-1, []):
+                        regroup_shared(c, side)
+                if 0 <= m - 2 < n_moves:
+                    for j in moves[m - 2]:
+                        w_products(j)
+                if 0 <= m < n_moves:
+                    for side in range(2):
+                        for j in moves[m]:
+                            h_tap(j, side)
+                if m + 1 < n_moves:
+                    for j in moves[m + 1]:
+                        mm1(j)
+                        centre(j)
+                if m == -1:
+                    for t in (2, 3):
+                        regroup_w(t, "a")
+                        quant_w(t)
+                    quant_x(1, 1, 1)
+                    nc.scalar.copy(out=v_grp[:], in_=v_raw[:].rearrange("p j o -> p o j"))
+                    nc.scalar.copy(out=bias_f[:], in_=bias_b[:])
+                    nc.vector.quantize_mx(
+                        out=vq[:].bitcast(FP8X4), scales=vs[:], in_=v_grp[:].rearrange("p o j -> p (o j)")
+                    )
+                for c in x_quant.get(m, []):
+                    quant_x(c, 0, 2)
+                for c in y_quant.get(m, []):
+                    quant_y(c)
+                if 0 <= m - 1 < n_moves:
+                    for j in moves[m - 1]:
+                        d_tap(j, 1)
+                if 0 <= m < n_moves:
                     for j in moves[m]:
-                        h_tap(j, side)
-            if m + 1 < n_moves:
-                for j in moves[m + 1]:
-                    mm1(j)
-                    centre(j)
-            if m == -1:
-                for t in (2, 3):
-                    regroup_w(t, "a")
-                    quant_w(t)
-                quant_x(1, 1, 1)
-                nc.scalar.copy(out=v_grp[:], in_=v_raw[:].rearrange("p j o -> p o j"))
-                nc.scalar.copy(out=bias_f[:], in_=bias_b[:])
-                nc.vector.quantize_mx(
-                    out=vq[:].bitcast(FP8X4), scales=vs[:], in_=v_grp[:].rearrange("p o j -> p (o j)")
-                )
-            for c in x_quant.get(m, []):
-                quant_x(c, 0, 2)
-            for c in y_quant.get(m, []):
-                quant_y(c)
-            if 0 <= m - 1 < n_moves:
-                for j in moves[m - 1]:
-                    d_tap(j, 1)
-            if 0 <= m < n_moves:
-                for j in moves[m]:
-                    d_tap(j, 0)
-            if 0 <= m - 2 < n_moves:
-                for j in moves[m - 2]:
-                    for k in range(steps[j][2] // 2):
-                        w_sum(j, k)
-                        round_y3(j, k)
-            if m >= 0:
-                for c, side in x_half.get(m, []):
-                    regroup_shared(c, side)
-            for c in y_quant.get(m, []):
-                for ot in range(2):
-                    mm2(c, ot)
-                for ot in range(2):
-                    evac(c, ot, "v" if c >= N_CHUNKS - 2 and ot == 1 else "a")
-            for c in y_turn.get(m, []):
-                for k in range(2):
-                    turn_y3(c, k)
-                for k in range(2):
-                    gather_y3(c, k, "v" if c >= N_CHUNKS - 2 and k == 1 else "a")
+                        d_tap(j, 0)
+                if 0 <= m - 2 < n_moves:
+                    for j in moves[m - 2]:
+                        for k in range(steps[j][2] // 2):
+                            w_sum(j, k)
+                            round_y3(j, k)
+                if m >= 0:
+                    for c, side in x_half.get(m, []):
+                        regroup_shared(c, side)
+                for c in y_quant.get(m, []):
+                    for ot in range(2):
+                        mm2(c, ot)
+                    for ot in range(2):
+                        evac(c, ot, "v" if c >= N_CHUNKS - 2 and ot == 1 else "a")
+                for c in y_turn.get(m, []):
+                    for k in range(2):
+                        turn_y3(c, k)
+                    for k in range(2):
+                        gather_y3(c, k, "v" if c >= N_CHUNKS - 2 and k == 1 else "a")

@@ -243,7 +243,10 @@ def tile_lowrankconv3d_t_kernel(tc, x, U_kh, U_kw, U_kd, U_c_in, U_c_out, bias, 
             nc.scalar.activation(out=dst, in_=src, func=ACTF.Copy, scale=c_r[:, 1, t, 0:1])
 
         def w_sum(j, k):
-            bank = tbp.tile([P, CHUNK], F32, name="tb")
+            if j >= n_steps - LATE:
+                bank = mbp.tile([P, CHUNK], F32, name="mb")
+            else:
+                bank = tbp.tile([P, CHUNK], F32, name="tb")
             pa = pa_ring[j % P_RING]
             pc = pc_ring[j % P_RING]
             for q in range(4):
@@ -332,8 +335,8 @@ def tile_lowrankconv3d_t_kernel(tc, x, U_kh, U_kw, U_kd, U_c_in, U_c_out, bias, 
                 )
             nc.sync.dma_start(out=ov[b][ot * P : (ot + 1) * P, cc * CHUNK : (cc + 1) * CHUNK], in_=o[:])
 
-        nc.vector.memset(k_rows[:], 0.0)
         with tc.high_priority():
+            nc.gpsimd.memset(k_rows[:], 0.0)
             nc.sync.dma_start(out=k_rows[0:3, :], in_=U_kh)
             nc.sync.dma_start(out=k_rows[3:6, :], in_=U_kw)
             nc.sync.dma_start(out=k_rows[6:9, :], in_=U_kd)
@@ -357,7 +360,7 @@ def tile_lowrankconv3d_t_kernel(tc, x, U_kh, U_kw, U_kd, U_c_in, U_c_out, bias, 
                     ring[n][:, 16 : 16 + 4 * WSLICE].rearrange("p (s r) -> p s r", r=WSLICE)[:, :, SLICE:WSLICE], 0.0
                 )
 
-        with tc.high_priority():
+        with tc.manual_schedule(engines={mybir.EngineType.DVE, mybir.EngineType.Pool, mybir.EngineType.PE}):
             nc.vector.tensor_copy(out=ident_b[:], in_=ident[:, 0:16])
             for u in range(2):
                 nc.vector.tensor_copy(
@@ -367,6 +370,12 @@ def tile_lowrankconv3d_t_kernel(tc, x, U_kh, U_kw, U_kd, U_c_in, U_c_out, bias, 
             k_bank = wop.tile([P, 4, 16], F32, name="wo")
             for t in range(4):
                 nc.tensor.matmul(k_bank[:, t, :], lhsT=k_perm[:, t, :], rhs=ident_b[:], start=True, stop=True)
+            regroup_x(0, 1, 0, SLICE, "a")
+            regroup_x(0, 0, 0, SLICE, "v")
+            regroup_w(0, "v")
+            regroup_w(1, "a")
+            quant_x(0, 0, 1)
+            quant_w(0)
             nc.vector.tensor_copy(out=cf[:], in_=k_bank[:])
             taps = cf[:, :, 3:9].rearrange("p t (a k) -> p t a k", k=3)
             flat = cf[:, :, 3:9]
@@ -382,23 +391,19 @@ def tile_lowrankconv3d_t_kernel(tc, x, U_kh, U_kw, U_kd, U_c_in, U_c_out, bias, 
                 out=c_small[:], in0=c_small[:], scalar=2.0, in1=c_max[:], op0=ALU.mult, op1=ALU.mult
             )
             nc.vector.tensor_tensor(out=c_piv[:], in0=taps[:, :, :, 1], in1=c_small[:], op=ALU.add)
-            nc.vector.reciprocal(out=c_rec[:], in_=c_piv[:])
             nc.vector.tensor_tensor(out=c_pp[:], in0=c_piv[:, :, 0], in1=c_piv[:, :, 1], op=ALU.mult)
             for k in (1, 0, 2):
                 nc.vector.tensor_tensor(out=c_h[:, k, :], in0=cf[:, :, k], in1=c_pp[:], op=ALU.mult)
+            quant_x(0, 1, 1)
+            regroup_x(1, 0, 0, SLICE, "v")
+            quant_x(1, 0, 1)
+            quant_w(1)
+            nc.vector.reciprocal(out=c_rec[:], in_=c_piv[:])
             for k in range(2):
                 nc.vector.tensor_tensor(out=c_r[:, k], in0=taps[:, :, :, 2 * k], in1=c_rec[:], op=ALU.mult)
-        regroup_x(0, 0, 0, SLICE, "v")
-        regroup_x(0, 1, 0, SLICE, "a")
-        regroup_w(0, "v")
-        quant_x(0, 0, 1)
-        quant_w(0)
-        quant_x(0, 1, 1)
-        regroup_x(1, 0, 0, SLICE, "a")
-        regroup_w(1, "a")
-        quant_x(1, 0, 1)
-        quant_w(1)
-        regroup_x(1, 1, 0, SLICE, "a")
+            for j in moves[0]:
+                mm1(j)
+                centre(j)
 
         first_use = {}
         complete = {}
@@ -431,7 +436,7 @@ def tile_lowrankconv3d_t_kernel(tc, x, U_kh, U_kw, U_kd, U_c_in, U_c_out, bias, 
             y_quant.setdefault(y_step[c] + (2 if c < 13 else 1), []).append(c)
 
         def regroup_shared(c, side):
-            g = 0
+            g = G_COLS if c > 3 else 0
             if g:
                 regroup_x(c, side, 0, g, "g")
             regroup_x(c, side, g, SLICE - g, "a")
@@ -442,9 +447,6 @@ def tile_lowrankconv3d_t_kernel(tc, x, U_kh, U_kw, U_kd, U_c_in, U_c_out, bias, 
                 for c, side in x_half.get(m + 4, []) if m >= 0 else []:
                     if side == 0 and c % 2 == 0 and c > 7:
                         load_x(c, 2)
-                if m == -1:
-                    for c, side in x_half.get(-1, []):
-                        regroup_shared(c, side)
                 if 0 <= m - 2 < n_moves:
                     for j in moves[m - 2]:
                         w_products(j)
@@ -452,17 +454,24 @@ def tile_lowrankconv3d_t_kernel(tc, x, U_kh, U_kw, U_kd, U_c_in, U_c_out, bias, 
                     for side in range(2):
                         for j in moves[m]:
                             h_tap(j, side)
-                if m + 1 < n_moves:
+                if m == 0:
+                    for t in (2, 3):
+                        quant_w(t)
+                    quant_x(1, 1, 1)
+                if 0 < m + 1 < n_moves:
                     for j in moves[m + 1]:
                         mm1(j)
                         centre(j)
                 if m == -1:
                     for t in (2, 3):
                         regroup_w(t, "a")
-                        quant_w(t)
-                    quant_x(1, 1, 1)
+                    regroup_x(1, 1, 0, SLICE, "a")
+                    for c, side in x_half.get(-1, []):
+                        regroup_shared(c, side)
+                if m == 1:
                     nc.scalar.copy(out=v_grp[:], in_=v_raw[:].rearrange("p j o -> p o j"))
                     nc.scalar.copy(out=bias_f[:], in_=bias_b[:])
+                if m == 3:
                     nc.vector.quantize_mx(
                         out=vq[:].bitcast(FP8X4), scales=vs[:], in_=v_grp[:].rearrange("p o j -> p (o j)")
                     )

@@ -91,6 +91,7 @@ def tile_lowrankconv3d_t_kernel(tc, x, U_kh, U_kw, U_kd, U_c_in, U_c_out, bias, 
         yt = {}
         wb = {}
         tb = {}
+        last_half = {}
         yg = {}
         yq = {}
         ys = {}
@@ -240,7 +241,11 @@ def tile_lowrankconv3d_t_kernel(tc, x, U_kh, U_kw, U_kd, U_c_in, U_c_out, bias, 
             else:
                 nc.gpsimd.tensor_scalar(out=dst, in0=src, scalar1=c, scalar2=0.0, op0=ALU.mult, op1=ALU.add)
             dst = slices(pc_ring[j % P_RING], 0, ns)
-            nc.scalar.activation(out=dst, in_=src, func=ACTF.Copy, scale=c_r[:, 1, t, 0:1])
+            c = c_r[:, 1, t, 0:1]
+            if j >= n_steps - LATE:
+                nc.vector.tensor_scalar_mul(out=dst, in0=src, scalar1=c)
+            else:
+                nc.scalar.activation(out=dst, in_=src, func=ACTF.Copy, scale=c)
 
         def w_sum(j, k):
             if j >= n_steps - LATE:
@@ -278,8 +283,37 @@ def tile_lowrankconv3d_t_kernel(tc, x, U_kh, U_kw, U_kd, U_c_in, U_c_out, bias, 
             else:
                 nc.scalar.copy(out=dst, in_=src)
 
+        def w_sum_half(k):
+            bank = mbp.tile([P, CHUNK], F32, name="mb")
+            for i, j in enumerate(moves[-1]):
+                pa = pa_ring[j % P_RING]
+                pc = pc_ring[j % P_RING]
+                for q in range(2):
+                    flat = k * SLICE + q * P
+                    base = 16 + k * WSLICE + q * P
+                    parts = (
+                        y2[j][:, flat : flat + P],
+                        pa[:, base - 16 : base - 16 + P],
+                        pc[:, base + 16 : base + 16 + P],
+                    )
+                    o = bank[:, (2 * i + q) * P : (2 * i + q + 1) * P]
+                    for n, part in enumerate(parts):
+                        nc.tensor.matmul(out=o, lhsT=part, rhs=ident[:], is_transpose=True, start=(n == 0), stop=(n == 2))
+            last_half[k] = bank
+
+        def round_half(c, k, eng):
+            dst = yt[c][:, 2 * k : 2 * k + 2, 2 * P : 4 * P].rearrange("p q (i r) -> p q i r", i=2)
+            src = last_half[k][:].rearrange("p (i q r) -> p q i r", i=2, q=2)
+            if eng == "v":
+                nc.vector.tensor_copy(out=dst, in_=src)
+            else:
+                nc.scalar.copy(out=dst, in_=src)
+
         def turn_y3(c, k):
-            bank = wop.tile([P, CHUNK], F32, name="wo")
+            if c == N_CHUNKS - 1:
+                bank = mbp.tile([P, CHUNK], F32, name="mb")
+            else:
+                bank = wop.tile([P, CHUNK], F32, name="wo")
             for q in range(2):
                 words = yt[c][:, 2 * k + q, :].bitcast(F32)
                 for u in range(2):
@@ -304,47 +338,59 @@ def tile_lowrankconv3d_t_kernel(tc, x, U_kh, U_kw, U_kd, U_c_in, U_c_out, bias, 
             else:
                 nc.scalar.copy(out=dst, in_=src)
 
-        def quant_y(c):
-            q = yqp.tile([P, CHUNK], U32, align_bytes=64, name="yq")
-            sc = yqp.tile([P, CHUNK], U8, align_bytes=64, name="ys")
-            nc.vector.quantize_mx(out=q[:].bitcast(FP8X4), scales=sc[:], in_=yg[c][:].rearrange("p w j -> p (w j)"))
-            yq[c] = q
-            ys[c] = sc
+        def quant_y(c, k, n):
+            if c not in yq:
+                q = yqp.tile([P, CHUNK], U32, align_bytes=64, name="yq")
+                sc = yqp.tile([P, CHUNK], U8, align_bytes=64, name="ys")
+                yq[c] = q
+                ys[c] = sc
+            lo = k * SLICE
+            hi = lo + n * SLICE
+            nc.vector.quantize_mx(
+                out=yq[c][:, lo:hi].bitcast(FP8X4),
+                scales=ys[c][:, lo:hi],
+                in_=yg[c][:, lo:hi, :].rearrange("p w j -> p (w j)"),
+            )
 
-        def mm2(c, ot):
-            bank = wop.tile([P, CHUNK], F32, name="wo")
+        def mm2(c, ot, k, n):
+            if k:
+                bank = tbp.tile([P, CHUNK], F32, name="tb")
+            else:
+                bank = wop.tile([P, CHUNK], F32, name="wo")
+            lo = k * SLICE
+            hi = lo + n * SLICE
             nc.tensor.matmul_mx(
-                out=bank[:],
+                out=bank[:, 0 : n * SLICE],
                 lhsT=vq[:, ot * P : (ot + 1) * P].bitcast(FP8X4),
                 lhsT_scale=vs[:, ot * P : (ot + 1) * P],
-                rhs=yq[c][:].bitcast(FP8X4),
-                rhs_scale=ys[c][:],
+                rhs=yq[c][:, lo:hi].bitcast(FP8X4),
+                rhs_scale=ys[c][:, lo:hi],
                 start=True,
                 stop=True,
             )
-            po[(c, ot)] = bank
+            po[(c, ot, k)] = bank
 
-        def evac(c, ot, eng):
+        def evac(c, ot, k, n, eng):
             b, cc = divmod(c, 8)
             o = osp.tile([P, CHUNK], F32, name="osb")
+            dst = o[:, 0 : n * SLICE]
+            src = po[(c, ot, k)][:, 0 : n * SLICE]
             if eng == "v":
-                nc.vector.tensor_scalar_add(out=o[:], in0=po[(c, ot)][:], scalar1=bias_f[:, ot : ot + 1])
+                nc.vector.tensor_scalar_add(out=dst, in0=src, scalar1=bias_f[:, ot : ot + 1])
             else:
-                nc.scalar.activation(
-                    out=o[:], in_=po[(c, ot)][:], func=ACTF.Identity, bias=bias_f[:, ot : ot + 1], scale=1.0
-                )
-            nc.sync.dma_start(out=ov[b][ot * P : (ot + 1) * P, cc * CHUNK : (cc + 1) * CHUNK], in_=o[:])
+                nc.scalar.activation(out=dst, in_=src, func=ACTF.Identity, bias=bias_f[:, ot : ot + 1], scale=1.0)
+            lo = cc * CHUNK + k * SLICE
+            nc.sync.dma_start(out=ov[b][ot * P : (ot + 1) * P, lo : lo + n * SLICE], in_=dst)
 
-        with tc.high_priority():
-            nc.gpsimd.memset(k_rows[:], 0.0)
-            nc.sync.dma_start(out=k_rows[0:3, :], in_=U_kh)
-            nc.sync.dma_start(out=k_rows[3:6, :], in_=U_kw)
-            nc.sync.dma_start(out=k_rows[6:9, :], in_=U_kd)
-            nc.vector.memset(warm[:], 0.0)
-            nc.scalar.copy(out=bias_f[:, 0:1], in_=warm[:])
-            make_identity(nc, ident[:])
+        nc.vector.memset(k_rows[:], 0.0)
+        nc.vector.memset(warm[:], 0.0)
+        nc.scalar.copy(out=bias_f[:, 0:1], in_=warm[:])
+        make_identity(nc, ident[:])
         load_x(0, 1)
         nc.sync.dma_start(out=w_raw[:], in_=U_c_in.rearrange("(p j) r -> p j r", j=4))
+        nc.sync.dma_start(out=k_rows[0:3, :], in_=U_kh)
+        nc.scalar.dma_start(out=k_rows[3:6, :], in_=U_kw)
+        nc.scalar.dma_start(out=k_rows[6:9, :], in_=U_kd)
         load_x(1, 1)
         load_x(2, 2)
         load_x(4, 2)
@@ -359,51 +405,6 @@ def tile_lowrankconv3d_t_kernel(tc, x, U_kh, U_kw, U_kd, U_c_in, U_c_out, bias, 
                 nc.gpsimd.memset(
                     ring[n][:, 16 : 16 + 4 * WSLICE].rearrange("p (s r) -> p s r", r=WSLICE)[:, :, SLICE:WSLICE], 0.0
                 )
-
-        with tc.manual_schedule(engines={mybir.EngineType.DVE, mybir.EngineType.Pool, mybir.EngineType.PE}):
-            nc.vector.tensor_copy(out=ident_b[:], in_=ident[:, 0:16])
-            for u in range(2):
-                nc.vector.tensor_copy(
-                    out=k_perm[:, 2 * u : 2 * u + 2, :].rearrange("p h (m e) -> p h m e", e=2),
-                    in_=k_rows[:].rearrange("p (h m u e) -> p u h m e", h=2, u=2, e=2)[:, u],
-                )
-            k_bank = wop.tile([P, 4, 16], F32, name="wo")
-            for t in range(4):
-                nc.tensor.matmul(k_bank[:, t, :], lhsT=k_perm[:, t, :], rhs=ident_b[:], start=True, stop=True)
-            regroup_x(0, 1, 0, SLICE, "a")
-            regroup_x(0, 0, 0, SLICE, "v")
-            regroup_w(0, "v")
-            regroup_w(1, "a")
-            quant_x(0, 0, 1)
-            quant_w(0)
-            nc.vector.tensor_copy(out=cf[:], in_=k_bank[:])
-            taps = cf[:, :, 3:9].rearrange("p t (a k) -> p t a k", k=3)
-            flat = cf[:, :, 3:9]
-            nc.vector.scalar_tensor_tensor(
-                out=c_abs[:].rearrange("p t a k -> p t (a k)"), in0=flat, scalar=-1.0, in1=flat, op0=ALU.mult, op1=ALU.max
-            )
-            nc.vector.tensor_reduce(out=c_max[:], in_=c_abs[:], op=ALU.max, axis=AX.X)
-            nc.vector.tensor_scalar(
-                out=c_max[:], in0=c_max[:], scalar1=2.0**-32, scalar2=2.0**-100, op0=ALU.mult, op1=ALU.add
-            )
-            nc.vector.tensor_tensor(out=c_small[:], in0=c_abs[:, :, :, 1], in1=c_max[:], op=ALU.is_lt)
-            nc.vector.scalar_tensor_tensor(
-                out=c_small[:], in0=c_small[:], scalar=2.0, in1=c_max[:], op0=ALU.mult, op1=ALU.mult
-            )
-            nc.vector.tensor_tensor(out=c_piv[:], in0=taps[:, :, :, 1], in1=c_small[:], op=ALU.add)
-            nc.vector.tensor_tensor(out=c_pp[:], in0=c_piv[:, :, 0], in1=c_piv[:, :, 1], op=ALU.mult)
-            for k in (1, 0, 2):
-                nc.vector.tensor_tensor(out=c_h[:, k, :], in0=cf[:, :, k], in1=c_pp[:], op=ALU.mult)
-            quant_x(0, 1, 1)
-            regroup_x(1, 0, 0, SLICE, "v")
-            quant_x(1, 0, 1)
-            quant_w(1)
-            nc.vector.reciprocal(out=c_rec[:], in_=c_piv[:])
-            for k in range(2):
-                nc.vector.tensor_tensor(out=c_r[:, k], in0=taps[:, :, :, 2 * k], in1=c_rec[:], op=ALU.mult)
-            for j in moves[0]:
-                mm1(j)
-                centre(j)
 
         first_use = {}
         complete = {}
@@ -431,7 +432,7 @@ def tile_lowrankconv3d_t_kernel(tc, x, U_kh, U_kw, U_kd, U_c_in, U_c_out, bias, 
                 x_half.setdefault(max(at - 2 + side, -1), []).append((c, side))
         y_turn = {}
         y_quant = {}
-        for c in range(N_CHUNKS):
+        for c in range(N_CHUNKS - 1):
             y_turn.setdefault(y_step[c], []).append(c)
             y_quant.setdefault(y_step[c] + (2 if c < 13 else 1), []).append(c)
 
@@ -441,65 +442,139 @@ def tile_lowrankconv3d_t_kernel(tc, x, U_kh, U_kw, U_kd, U_c_in, U_c_out, bias, 
                 regroup_x(c, side, 0, g, "g")
             regroup_x(c, side, g, SLICE - g, "a")
 
-        with tc.manual_schedule(engines={mybir.EngineType.DVE, mybir.EngineType.Pool}):
-            load_x(6, 2)
-            for m in range(-1, n_moves + 7):
-                for c, side in x_half.get(m + 4, []) if m >= 0 else []:
-                    if side == 0 and c % 2 == 0 and c > 7:
-                        load_x(c, 2)
-                if 0 <= m - 2 < n_moves:
-                    for j in moves[m - 2]:
-                        w_products(j)
-                if 0 <= m < n_moves:
-                    for side in range(2):
-                        for j in moves[m]:
-                            h_tap(j, side)
-                if m == 0:
-                    for t in (2, 3):
-                        quant_w(t)
-                    quant_x(1, 1, 1)
-                if 0 < m + 1 < n_moves:
-                    for j in moves[m + 1]:
-                        mm1(j)
-                        centre(j)
-                if m == -1:
-                    for t in (2, 3):
-                        regroup_w(t, "a")
-                    regroup_x(1, 1, 0, SLICE, "a")
-                    for c, side in x_half.get(-1, []):
-                        regroup_shared(c, side)
-                if m == 1:
-                    nc.scalar.copy(out=v_grp[:], in_=v_raw[:].rearrange("p j o -> p o j"))
-                    nc.scalar.copy(out=bias_f[:], in_=bias_b[:])
-                if m == 3:
-                    nc.vector.quantize_mx(
-                        out=vq[:].bitcast(FP8X4), scales=vs[:], in_=v_grp[:].rearrange("p o j -> p (o j)")
-                    )
-                for c in x_quant.get(m, []):
-                    quant_x(c, 0, 2)
-                for c in y_quant.get(m, []):
-                    quant_y(c)
-                if 0 <= m - 1 < n_moves:
-                    for j in moves[m - 1]:
-                        d_tap(j, 1)
-                if 0 <= m < n_moves:
+        def move(m):
+            for c, side in x_half.get(m + 4, []) if m >= 0 else []:
+                if side == 0 and c % 2 == 0 and c > 7:
+                    load_x(c, 2)
+            if 0 <= m - 2 < n_moves - 1:
+                for j in moves[m - 2]:
+                    w_products(j)
+            if 0 <= m < n_moves:
+                for side in range(2):
                     for j in moves[m]:
-                        d_tap(j, 0)
-                if 0 <= m - 2 < n_moves:
-                    for j in moves[m - 2]:
-                        for k in range(steps[j][2] // 2):
-                            w_sum(j, k)
-                            round_y3(j, k)
-                if m >= 0:
-                    for c, side in x_half.get(m, []):
-                        regroup_shared(c, side)
-                for c in y_quant.get(m, []):
-                    for ot in range(2):
-                        mm2(c, ot)
-                    for ot in range(2):
-                        evac(c, ot, "v" if c >= N_CHUNKS - 2 and ot == 1 else "a")
-                for c in y_turn.get(m, []):
-                    for k in range(2):
-                        turn_y3(c, k)
-                    for k in range(2):
-                        gather_y3(c, k, "v" if c >= N_CHUNKS - 2 and k == 1 else "a")
+                        h_tap(j, side)
+            if m == 0:
+                for t in (2, 3):
+                    quant_w(t)
+                quant_x(1, 1, 1)
+            if 0 < m + 1 < n_moves:
+                for j in moves[m + 1]:
+                    mm1(j)
+                    centre(j)
+            if m == -1:
+                for t in (2, 3):
+                    regroup_w(t, "a")
+                regroup_x(1, 1, 0, SLICE, "a")
+                for c, side in x_half.get(-1, []):
+                    regroup_shared(c, side)
+            if m == 1:
+                nc.scalar.copy(out=v_grp[:], in_=v_raw[:].rearrange("p j o -> p o j"))
+                nc.scalar.copy(out=bias_f[:], in_=bias_b[:])
+            if m == 3:
+                nc.vector.quantize_mx(
+                    out=vq[:].bitcast(FP8X4), scales=vs[:], in_=v_grp[:].rearrange("p o j -> p (o j)")
+                )
+            for c in x_quant.get(m, []):
+                quant_x(c, 0, 2)
+            for c in y_quant.get(m, []):
+                quant_y(c, 0, 2)
+            if 0 <= m - 1 < n_moves:
+                for j in moves[m - 1]:
+                    d_tap(j, 1)
+                if m == n_moves:
+                    for j in moves[m - 1]:
+                        w_products(j)
+            if 0 <= m < n_moves:
+                for j in moves[m]:
+                    d_tap(j, 0)
+            if 0 <= m - 2 < n_moves - 1:
+                for j in moves[m - 2]:
+                    for k in range(steps[j][2] // 2):
+                        w_sum(j, k)
+                        round_y3(j, k)
+            if m >= 0:
+                for c, side in x_half.get(m, []):
+                    regroup_shared(c, side)
+            for c in y_quant.get(m, []):
+                for ot in range(2):
+                    mm2(c, ot, 0, 2)
+                for ot in range(2):
+                    evac(c, ot, 0, 2, "v" if c >= N_CHUNKS - 4 and ot == 1 else "a")
+            for c in y_turn.get(m, []):
+                for k in range(2):
+                    turn_y3(c, k)
+                for k in range(2):
+                    gather_y3(c, k, "v" if c >= N_CHUNKS - 2 and k == 1 else "a")
+
+        load_x(6, 2)
+        head_engines = {mybir.EngineType.DVE, mybir.EngineType.Pool, mybir.EngineType.PE, mybir.EngineType.Activation}
+        with tc.manual_schedule(engines=head_engines):
+            regroup_x(0, 1, 0, SLICE, "a")
+            regroup_x(0, 0, 0, SLICE, "v")
+            regroup_w(0, "v")
+            regroup_w(1, "a")
+            quant_x(0, 0, 1)
+            quant_w(0)
+            regroup_x(1, 0, 0, SLICE, "v")
+            quant_x(0, 1, 1)
+            quant_w(1)
+            quant_x(1, 0, 1)
+            nc.vector.tensor_copy(out=ident_b[:], in_=ident[:, 0:16])
+            for u in range(2):
+                nc.vector.tensor_copy(
+                    out=k_perm[:, 2 * u : 2 * u + 2, :].rearrange("p h (m e) -> p h m e", e=2),
+                    in_=k_rows[:].rearrange("p (h m u e) -> p u h m e", h=2, u=2, e=2)[:, u],
+                )
+            k_bank = wop.tile([P, 4, 16], F32, name="wo")
+            for t in range(4):
+                nc.tensor.matmul(k_bank[:, t, :], lhsT=k_perm[:, t, :], rhs=ident_b[:], start=True, stop=True)
+            nc.vector.tensor_copy(out=cf[:], in_=k_bank[:])
+            taps = cf[:, :, 3:9].rearrange("p t (a k) -> p t a k", k=3)
+            flat = cf[:, :, 3:9]
+            nc.vector.scalar_tensor_tensor(
+                out=c_abs[:].rearrange("p t a k -> p t (a k)"),
+                in0=flat,
+                scalar=-1.0,
+                in1=flat,
+                op0=ALU.mult,
+                op1=ALU.max,
+            )
+            nc.vector.tensor_reduce(out=c_max[:], in_=c_abs[:], op=ALU.max, axis=AX.X)
+            nc.vector.tensor_scalar(
+                out=c_max[:], in0=c_max[:], scalar1=2.0**-32, scalar2=2.0**-100, op0=ALU.mult, op1=ALU.add
+            )
+            nc.vector.tensor_tensor(out=c_small[:], in0=c_abs[:, :, :, 1], in1=c_max[:], op=ALU.is_lt)
+            nc.vector.scalar_tensor_tensor(
+                out=c_small[:], in0=c_small[:], scalar=2.0, in1=c_max[:], op0=ALU.mult, op1=ALU.mult
+            )
+            nc.vector.tensor_tensor(out=c_piv[:], in0=taps[:, :, :, 1], in1=c_small[:], op=ALU.add)
+            nc.vector.tensor_tensor(out=c_pp[:], in0=c_piv[:, :, 0], in1=c_piv[:, :, 1], op=ALU.mult)
+            for k in (1, 0, 2):
+                nc.vector.tensor_tensor(out=c_h[:, k, :], in0=cf[:, :, k], in1=c_pp[:], op=ALU.mult)
+            nc.vector.reciprocal(out=c_rec[:], in_=c_piv[:])
+            for k in range(2):
+                nc.vector.tensor_tensor(out=c_r[:, k], in0=taps[:, :, :, 2 * k], in1=c_rec[:], op=ALU.mult)
+            for j in moves[0]:
+                mm1(j)
+                centre(j)
+            for m in range(-1, 1):
+                move(m)
+        with tc.manual_schedule(engines={mybir.EngineType.DVE, mybir.EngineType.Pool}):
+            for m in range(1, n_moves + 3):
+                move(m)
+            c = N_CHUNKS - 1
+            for k in range(2):
+                w_sum_half(k)
+                round_half(c, k, "av"[k])
+            for k in range(2):
+                turn_y3(c, k)
+            gather_y3(c, 0, "a")
+            quant_y(c, 0, 1)
+            gather_y3(c, 1, "v")
+            quant_y(c, 1, 1)
+            for k in range(2):
+                for ot in range(2):
+                    mm2(c, ot, k, 1)
+            for k in range(2):
+                for ot in range(2):
+                    evac(c, ot, k, 1, "av"[ot])

@@ -418,7 +418,11 @@ def tile_lowrankconv3d_t_kernel(tc, x, U_kh, U_kw, U_kd, U_c_in, U_c_out, bias, 
         x_step = {}
         for c in reversed(range(2, N_CHUNKS)):
             at = first_use[c] - 2
-            x_step[c] = max(min(at, x_step[c + 1] - 2), c - 2) if c + 1 in x_step else at
+            if c < 8:
+                at = min(at, c - 2)
+            elif c + 1 in x_step:
+                at = min(at, x_step[c + 1] - 2)
+            x_step[c] = at
         y_step = {}
         for c in range(N_CHUNKS):
             at = complete[c] + 3
@@ -437,7 +441,7 @@ def tile_lowrankconv3d_t_kernel(tc, x, U_kh, U_kw, U_kd, U_c_in, U_c_out, bias, 
             y_quant.setdefault(y_step[c] + (2 if c < 13 else 1), []).append(c)
 
         def regroup_shared(c, side):
-            g = G_COLS if c > 3 else 0
+            g = G_COLS if c > 7 else 0
             if g:
                 regroup_x(c, side, 0, g, "g")
             regroup_x(c, side, g, SLICE - g, "a")
@@ -549,8 +553,12 @@ def tile_lowrankconv3d_t_kernel(tc, x, U_kh, U_kw, U_kd, U_c_in, U_c_out, bias, 
             )
             nc.vector.tensor_tensor(out=c_piv[:], in0=taps[:, :, :, 1], in1=c_small[:], op=ALU.add)
             nc.vector.tensor_tensor(out=c_pp[:], in0=c_piv[:, :, 0], in1=c_piv[:, :, 1], op=ALU.mult)
-            for k in (1, 0, 2):
-                nc.vector.tensor_tensor(out=c_h[:, k, :], in0=cf[:, :, k], in1=c_pp[:], op=ALU.mult)
+            nc.vector.tensor_tensor(
+                out=c_h[:],
+                in0=cf[:].rearrange("p t k -> p k t")[:, 0:3, :],
+                in1=c_pp[:].unsqueeze(1).to_broadcast([P, 3, 4]),
+                op=ALU.mult,
+            )
             nc.vector.reciprocal(out=c_rec[:], in_=c_piv[:])
             for k in range(2):
                 nc.vector.tensor_tensor(out=c_r[:, k], in0=taps[:, :, :, 2 * k], in1=c_rec[:], op=ALU.mult)

@@ -23,7 +23,7 @@ DROW = 20
 WSLICE = 272
 RING = 6
 P_RING = 4
-LATE = 2
+DIRECT = 4
 G_COLS = 128
 
 
@@ -56,6 +56,8 @@ def tile_lowrankconv3d_t_kernel(tc, x, U_kh, U_kw, U_kd, U_c_in, U_c_out, bias, 
         v_grp = const.tile([P, 256, 4], BF16, align_bytes=64, name="v_grp")
         vq = const.tile([P, 256], U32, align_bytes=64, name="vq")
         vs = const.tile([P, 256], U8, align_bytes=64, name="vs")
+        dq = const.tile([P, 256], U32, align_bytes=64, name="dq")
+        ds = const.tile([P, 256], U8, align_bytes=64, name="ds")
         ident = const.tile([P, P], F32, align_bytes=64, name="ident")
         ident_b = const.tile([P, 16], BF16, name="ident_b")
         k_rows = const.tile([P, 512], BF16, name="k_rows")
@@ -91,7 +93,8 @@ def tile_lowrankconv3d_t_kernel(tc, x, U_kh, U_kw, U_kd, U_c_in, U_c_out, bias, 
         yt = {}
         wb = {}
         tb = {}
-        last_half = {}
+        yd = {}
+        right = {}
         yg = {}
         yq = {}
         ys = {}
@@ -227,31 +230,60 @@ def tile_lowrankconv3d_t_kernel(tc, x, U_kh, U_kw, U_kd, U_c_in, U_c_out, bias, 
             if k == 0:
                 a = y2p.tile([P, 4 * SLICE], F32, align_bytes=64, name="y2")
                 y2[j] = a
+                if j >= n_steps - DIRECT:
+                    nc.vector.memset(a[:, 0 : 3 * WSLICE].rearrange("p (s r) -> p s r", r=WSLICE)[:, :, 0:16], 0.0)
+            if j >= n_steps - DIRECT:
+                for s in range(2):
+                    v = rows(padded(j, 0)[:, s, :])
+                    acc = y1_rows(j, 0)[:, 16 * s : 16 * s + 16, :] if k == 0 else v
+                    mac(v, acc, y1_rows(j, -1 if k == 0 else 1)[:, 16 * s : 16 * s + 16, :], c_r[:, k, t, 1:2])
+                return
             v = rows(y2[j][:, 0 : ns * SLICE])
             acc = y1_rows(j, 0)[:, 0 : 16 * ns, :] if k == 0 else v
             mac(v, acc, y1_rows(j, -1 if k == 0 else 1)[:, 0 : 16 * ns, :], c_r[:, k, t, 1:2])
+
+        def padded(j, off):
+            v = y2[j][:, 16 + off : 16 + off + 2 * WSLICE].rearrange("p (s r) -> p s r", r=WSLICE)
+            return v[:, :, 0:SLICE]
+
+        def w_direct(j, side):
+            c, t = N_CHUNKS - 1, steps[j][3]
+            if c not in yd:
+                a = ytp.tile([P, 4, 512], BF16, align_bytes=64, name="yt")
+                yd[c] = a
+            if side:
+                o = y2p.tile([P, 4 * SLICE], F32, align_bytes=64, name="y2")
+                right[j] = o
+            o = right[j][:, 0:CHUNK].rearrange("p (s r) -> p s r", r=SLICE)
+            if side:
+                mac(o, padded(j, 0), padded(j, 16), c_r[:, 1, t, 0:1])
+            else:
+                mac(yd[c][:, t, :].rearrange("p (s r) -> p s r", r=SLICE), o, padded(j, -16), c_r[:, 0, t, 0:1])
+
+        def gather_direct(c, k, eng):
+            if c not in yg:
+                g = xgp.tile([P, CHUNK, 4], BF16, align_bytes=64, name="xg")
+                yg[c] = g
+            lo = k * SLICE
+            src = yd[c][:, :, lo : lo + SLICE].rearrange("p t (c i) -> p c t i", i=4)
+            dst = yg[c][:, lo : lo + SLICE, :].rearrange("p (c i) t -> p c t i", i=4)
+            if eng == "v":
+                nc.vector.tensor_copy(out=dst, in_=src)
+            else:
+                nc.scalar.copy(out=dst, in_=src)
 
         def w_products(j):
             b, s0, ns, t = steps[j]
             src = y2[j][:, 0 : ns * SLICE].rearrange("p (s r) -> p s r", r=SLICE)
             dst = slices(pa_ring[j % P_RING], 0, ns)
             c = c_r[:, 0, t, 0:1]
-            if j >= n_steps - LATE:
-                nc.vector.tensor_scalar_mul(out=dst, in0=src, scalar1=c)
-            else:
-                nc.gpsimd.tensor_scalar(out=dst, in0=src, scalar1=c, scalar2=0.0, op0=ALU.mult, op1=ALU.add)
+            nc.gpsimd.tensor_scalar(out=dst, in0=src, scalar1=c, scalar2=0.0, op0=ALU.mult, op1=ALU.add)
             dst = slices(pc_ring[j % P_RING], 0, ns)
             c = c_r[:, 1, t, 0:1]
-            if j >= n_steps - LATE:
-                nc.vector.tensor_scalar_mul(out=dst, in0=src, scalar1=c)
-            else:
-                nc.scalar.activation(out=dst, in_=src, func=ACTF.Copy, scale=c)
+            nc.scalar.activation(out=dst, in_=src, func=ACTF.Copy, scale=c)
 
         def w_sum(j, k):
-            if j >= n_steps - LATE:
-                bank = mbp.tile([P, CHUNK], F32, name="mb")
-            else:
-                bank = tbp.tile([P, CHUNK], F32, name="tb")
+            bank = tbp.tile([P, CHUNK], F32, name="tb")
             pa = pa_ring[j % P_RING]
             pc = pc_ring[j % P_RING]
             for q in range(4):
@@ -278,39 +310,10 @@ def tile_lowrankconv3d_t_kernel(tc, x, U_kh, U_kw, U_kd, U_c_in, U_c_out, bias, 
                 yt[c] = a
             dst = yt[c][:, :, t * P : (t + 1) * P]
             src = tb[(j, k)][:].rearrange("p (q r) -> p q r", q=4)
-            if j >= n_steps - 2 * LATE and j % 2 == 0:
-                nc.vector.tensor_copy(out=dst, in_=src)
-            else:
-                nc.scalar.copy(out=dst, in_=src)
-
-        def w_sum_half(k):
-            bank = mbp.tile([P, CHUNK], F32, name="mb")
-            for i, j in enumerate(moves[-1]):
-                pa = pa_ring[j % P_RING]
-                pc = pc_ring[j % P_RING]
-                for q in range(2):
-                    flat = k * SLICE + q * P
-                    base = 16 + k * WSLICE + q * P
-                    parts = (
-                        y2[j][:, flat : flat + P],
-                        pa[:, base - 16 : base - 16 + P],
-                        pc[:, base + 16 : base + 16 + P],
-                    )
-                    o = bank[:, (2 * i + q) * P : (2 * i + q + 1) * P]
-                    for n, part in enumerate(parts):
-                        nc.tensor.matmul(out=o, lhsT=part, rhs=ident[:], is_transpose=True, start=(n == 0), stop=(n == 2))
-            last_half[k] = bank
-
-        def round_half(c, k, eng):
-            dst = yt[c][:, 2 * k : 2 * k + 2, 2 * P : 4 * P].rearrange("p q (i r) -> p q i r", i=2)
-            src = last_half[k][:].rearrange("p (i q r) -> p q i r", i=2, q=2)
-            if eng == "v":
-                nc.vector.tensor_copy(out=dst, in_=src)
-            else:
-                nc.scalar.copy(out=dst, in_=src)
+            nc.scalar.copy(out=dst, in_=src)
 
         def turn_y3(c, k):
-            if c == N_CHUNKS - 1:
+            if c == N_CHUNKS - 2:
                 bank = mbp.tile([P, CHUNK], F32, name="mb")
             else:
                 bank = wop.tile([P, CHUNK], F32, name="wo")
@@ -353,16 +356,17 @@ def tile_lowrankconv3d_t_kernel(tc, x, U_kh, U_kw, U_kd, U_c_in, U_c_out, bias, 
             )
 
         def mm2(c, ot, k, n):
-            if k:
-                bank = tbp.tile([P, CHUNK], F32, name="tb")
+            if c == N_CHUNKS - 1:
+                bank = mbp.tile([P, CHUNK], F32, name="mb")
             else:
                 bank = wop.tile([P, CHUNK], F32, name="wo")
             lo = k * SLICE
             hi = lo + n * SLICE
+            q, sc = (dq, ds) if c == N_CHUNKS - 1 else (vq, vs)
             nc.tensor.matmul_mx(
                 out=bank[:, 0 : n * SLICE],
-                lhsT=vq[:, ot * P : (ot + 1) * P].bitcast(FP8X4),
-                lhsT_scale=vs[:, ot * P : (ot + 1) * P],
+                lhsT=q[:, ot * P : (ot + 1) * P].bitcast(FP8X4),
+                lhsT_scale=sc[:, ot * P : (ot + 1) * P],
                 rhs=yq[c][:, lo:hi].bitcast(FP8X4),
                 rhs_scale=ys[c][:, lo:hi],
                 start=True,
@@ -387,11 +391,11 @@ def tile_lowrankconv3d_t_kernel(tc, x, U_kh, U_kw, U_kd, U_c_in, U_c_out, bias, 
         nc.scalar.copy(out=bias_f[:, 0:1], in_=warm[:])
         make_identity(nc, ident[:])
         load_x(0, 1)
-        nc.sync.dma_start(out=w_raw[:], in_=U_c_in.rearrange("(p j) r -> p j r", j=4))
         nc.sync.dma_start(out=k_rows[0:3, :], in_=U_kh)
-        nc.scalar.dma_start(out=k_rows[3:6, :], in_=U_kw)
-        nc.scalar.dma_start(out=k_rows[6:9, :], in_=U_kd)
+        nc.sync.dma_start(out=k_rows[3:6, :], in_=U_kw)
+        nc.sync.dma_start(out=k_rows[6:9, :], in_=U_kd)
         load_x(1, 1)
+        nc.sync.dma_start(out=w_raw[:], in_=U_c_in.rearrange("(p j) r -> p j r", j=4))
         load_x(2, 2)
         load_x(4, 2)
         with nc.allow_non_contiguous_dma(reason="256 bias values, one per partition and output tile"):
@@ -441,7 +445,7 @@ def tile_lowrankconv3d_t_kernel(tc, x, U_kh, U_kw, U_kd, U_c_in, U_c_out, bias, 
             y_quant.setdefault(y_step[c] + (2 if c < 13 else 1), []).append(c)
 
         def regroup_shared(c, side):
-            g = G_COLS if c > 7 else 0
+            g = G_COLS if c > 4 else 0
             if g:
                 regroup_x(c, side, 0, g, "g")
             regroup_x(c, side, g, SLICE - g, "a")
@@ -450,26 +454,22 @@ def tile_lowrankconv3d_t_kernel(tc, x, U_kh, U_kw, U_kd, U_c_in, U_c_out, bias, 
             for c, side in x_half.get(m + 4, []) if m >= 0 else []:
                 if side == 0 and c % 2 == 0 and c > 7:
                     load_x(c, 2)
-            if 0 <= m - 2 < n_moves - 1:
+            if 0 <= m - 2 < n_moves - 2:
                 for j in moves[m - 2]:
                     w_products(j)
             if 0 <= m < n_moves:
                 for side in range(2):
                     for j in moves[m]:
                         h_tap(j, side)
-            if m == 0:
-                for t in (2, 3):
-                    quant_w(t)
-                quant_x(1, 1, 1)
             if 0 < m + 1 < n_moves:
                 for j in moves[m + 1]:
                     mm1(j)
                     centre(j)
             if m == -1:
-                for t in (2, 3):
-                    regroup_w(t, "a")
-                regroup_x(1, 1, 0, SLICE, "a")
-                for c, side in x_half.get(-1, []):
+                for c, side in x_half.get(-1, [])[:2]:
+                    regroup_shared(c, side)
+            if m == 0:
+                for c, side in x_half.get(-1, [])[2:]:
                     regroup_shared(c, side)
             if m == 1:
                 nc.scalar.copy(out=v_grp[:], in_=v_raw[:].rearrange("p j o -> p o j"))
@@ -478,20 +478,46 @@ def tile_lowrankconv3d_t_kernel(tc, x, U_kh, U_kw, U_kd, U_c_in, U_c_out, bias, 
                 nc.vector.quantize_mx(
                     out=vq[:].bitcast(FP8X4), scales=vs[:], in_=v_grp[:].rearrange("p o j -> p (o j)")
                 )
-            for c in x_quant.get(m, []):
-                quant_x(c, 0, 2)
-            for c in y_quant.get(m, []):
-                quant_y(c, 0, 2)
-            if 0 <= m - 1 < n_moves:
+            if m == 5:
+                rows_out = U_c_out.rearrange("(h m u e) o -> h e m u o", h=2, u=2, e=2)
+                for h in range(2):
+                    for e in range(2):
+                        nc.sync.dma_start(out=v_raw[e:P:2, h:4:2, :], in_=rows_out[h, e])
+            if m == 9:
+                nc.scalar.copy(out=v_grp[:], in_=v_raw[:].rearrange("p j o -> p o j"))
+            if m == 11:
+                nc.vector.quantize_mx(
+                    out=dq[:].bitcast(FP8X4), scales=ds[:], in_=v_grp[:].rearrange("p o j -> p (o j)")
+                )
+            if m == n_moves:
                 for j in moves[m - 1]:
                     d_tap(j, 1)
-                if m == n_moves:
-                    for j in moves[m - 1]:
-                        w_products(j)
+            for c in x_quant.get(m, []) if m > 1 else []:
+                quant_x(c, 0, 2)
+            if m < n_moves:
+                for c in y_quant.get(m, []):
+                    quant_y(c, 0, 2)
+            if m == n_moves:
+                for i, c in ((0, N_CHUNKS - 4), (2, N_CHUNKS - 3)):
+                    quant_y(c, 0, 2)
+                    for side in (1, 0):
+                        for j in range(n_steps - DIRECT + i, n_steps - DIRECT + i + 2):
+                            w_direct(j, side)
+                gather_direct(N_CHUNKS - 1, 1, "a")
+                gather_direct(N_CHUNKS - 1, 0, "v")
+            if m == n_moves + 1:
+                quant_y(N_CHUNKS - 1, 0, 1)
+                quant_y(N_CHUNKS - 2, 0, 2)
+                quant_y(N_CHUNKS - 1, 1, 1)
+            if 0 <= m - 1 < n_moves - 1:
+                for j in moves[m - 1]:
+                    d_tap(j, 1)
             if 0 <= m < n_moves:
                 for j in moves[m]:
                     d_tap(j, 0)
-            if 0 <= m - 2 < n_moves - 1:
+            for c in x_quant.get(m, []) if 0 <= m <= 1 else []:
+                quant_x(c, 0, 2)
+            if 0 <= m - 2 < n_moves - 2:
                 for j in moves[m - 2]:
                     for k in range(steps[j][2] // 2):
                         w_sum(j, k)
@@ -503,26 +529,18 @@ def tile_lowrankconv3d_t_kernel(tc, x, U_kh, U_kw, U_kd, U_c_in, U_c_out, bias, 
                 for ot in range(2):
                     mm2(c, ot, 0, 2)
                 for ot in range(2):
-                    evac(c, ot, 0, 2, "v" if c >= N_CHUNKS - 4 and ot == 1 else "a")
+                    evac(c, ot, 0, 2, "a")
             for c in y_turn.get(m, []):
                 for k in range(2):
                     turn_y3(c, k)
                 for k in range(2):
-                    gather_y3(c, k, "v" if c >= N_CHUNKS - 2 and k == 1 else "a")
+                    gather_y3(c, k, "a")
 
         load_x(6, 2)
         head_engines = {mybir.EngineType.DVE, mybir.EngineType.Pool, mybir.EngineType.PE, mybir.EngineType.Activation}
         with tc.manual_schedule(engines=head_engines):
             regroup_x(0, 1, 0, SLICE, "a")
             regroup_x(0, 0, 0, SLICE, "v")
-            regroup_w(0, "v")
-            regroup_w(1, "a")
-            quant_x(0, 0, 1)
-            quant_w(0)
-            regroup_x(1, 0, 0, SLICE, "v")
-            quant_x(0, 1, 1)
-            quant_w(1)
-            quant_x(1, 0, 1)
             nc.vector.tensor_copy(out=ident_b[:], in_=ident[:, 0:16])
             for u in range(2):
                 nc.vector.tensor_copy(
@@ -532,9 +550,13 @@ def tile_lowrankconv3d_t_kernel(tc, x, U_kh, U_kw, U_kd, U_c_in, U_c_out, bias, 
             k_bank = wop.tile([P, 4, 16], F32, name="wo")
             for t in range(4):
                 nc.tensor.matmul(k_bank[:, t, :], lhsT=k_perm[:, t, :], rhs=ident_b[:], start=True, stop=True)
+            quant_x(0, 0, 1)
+            regroup_x(1, 1, 0, SLICE, "a")
+            quant_x(0, 1, 1)
             nc.vector.tensor_copy(out=cf[:], in_=k_bank[:])
             taps = cf[:, :, 3:9].rearrange("p t (a k) -> p t a k", k=3)
             flat = cf[:, :, 3:9]
+            regroup_x(1, 0, 0, SLICE, "v")
             nc.vector.scalar_tensor_tensor(
                 out=c_abs[:].rearrange("p t a k -> p t (a k)"),
                 in0=flat,
@@ -543,14 +565,21 @@ def tile_lowrankconv3d_t_kernel(tc, x, U_kh, U_kw, U_kd, U_c_in, U_c_out, bias, 
                 op0=ALU.mult,
                 op1=ALU.max,
             )
+            quant_x(1, 0, 1)
             nc.vector.tensor_reduce(out=c_max[:], in_=c_abs[:], op=ALU.max, axis=AX.X)
+            for t in (2, 3):
+                regroup_w(t, "a")
+            regroup_w(0, "v")
             nc.vector.tensor_scalar(
                 out=c_max[:], in0=c_max[:], scalar1=2.0**-32, scalar2=2.0**-100, op0=ALU.mult, op1=ALU.add
             )
+            quant_w(0)
             nc.vector.tensor_tensor(out=c_small[:], in0=c_abs[:, :, :, 1], in1=c_max[:], op=ALU.is_lt)
+            regroup_w(1, "v")
             nc.vector.scalar_tensor_tensor(
                 out=c_small[:], in0=c_small[:], scalar=2.0, in1=c_max[:], op0=ALU.mult, op1=ALU.mult
             )
+            quant_w(1)
             nc.vector.tensor_tensor(out=c_piv[:], in0=taps[:, :, :, 1], in1=c_small[:], op=ALU.add)
             nc.vector.tensor_tensor(out=c_pp[:], in0=c_piv[:, :, 0], in1=c_piv[:, :, 1], op=ALU.mult)
             nc.vector.tensor_tensor(
@@ -560,6 +589,9 @@ def tile_lowrankconv3d_t_kernel(tc, x, U_kh, U_kw, U_kd, U_c_in, U_c_out, bias, 
                 op=ALU.mult,
             )
             nc.vector.reciprocal(out=c_rec[:], in_=c_piv[:])
+            quant_w(2)
+            quant_w(3)
+            quant_x(1, 1, 1)
             for k in range(2):
                 nc.vector.tensor_tensor(out=c_r[:, k], in0=taps[:, :, :, 2 * k], in1=c_rec[:], op=ALU.mult)
             for j in moves[0]:
@@ -572,17 +604,8 @@ def tile_lowrankconv3d_t_kernel(tc, x, U_kh, U_kw, U_kd, U_c_in, U_c_out, bias, 
                 move(m)
             c = N_CHUNKS - 1
             for k in range(2):
-                w_sum_half(k)
-                round_half(c, k, "av"[k])
-            for k in range(2):
-                turn_y3(c, k)
-            gather_y3(c, 0, "a")
-            quant_y(c, 0, 1)
-            gather_y3(c, 1, "v")
-            quant_y(c, 1, 1)
-            for k in range(2):
                 for ot in range(2):
                     mm2(c, ot, k, 1)
             for k in range(2):
                 for ot in range(2):
-                    evac(c, ot, k, 1, "av"[ot])
+                    evac(c, ot, k, 1, "va"[ot])

@@ -94,7 +94,6 @@ def tile_lowrankconv3d_t_kernel(tc, x, U_kh, U_kw, U_kd, U_c_in, U_c_out, bias, 
         wb = {}
         tb = {}
         yd = {}
-        right = {}
         yg = {}
         yq = {}
         ys = {}
@@ -163,12 +162,21 @@ def tile_lowrankconv3d_t_kernel(tc, x, U_kh, U_kw, U_kd, U_c_in, U_c_out, bias, 
         n_moves = len(moves)
         n_steps = len(steps)
 
-        def mm1(j):
+        def first_group(j):
             b, s0, ns, t = steps[j]
-            banks = []
-            for k in range(ns // 2 + 1):
+            return b == 0 and s0 == 0 and ns == 2
+
+        def mm1(j):
+            for k in range(steps[j][2] // 2 + 1):
+                mm1_bank(j, k)
+
+        def mm1_bank(j, k):
+            b, s0, ns, t = steps[j]
+            if True:
                 lo, o0, n = s0 - 1 + 2 * k, 0, CHUNK
-                if lo < 0:
+                if first_group(j):
+                    lo, n = 2 * k, CHUNK - k * SLICE
+                elif lo < 0:
                     lo, o0, n = 0, SLICE, SLICE
                 elif lo == 15:
                     n = SLICE
@@ -183,8 +191,7 @@ def tile_lowrankconv3d_t_kernel(tc, x, U_kh, U_kw, U_kd, U_c_in, U_c_out, bias, 
                     start=True,
                     stop=True,
                 )
-                banks.append(bank)
-            mb[j] = banks
+                mb.setdefault(j, []).append(bank)
 
         def y1_rows(j, off):
             v = y1_ring[j % RING][:, 4 + off : 4 + off + 64 * DROW].rearrange("p (q e) -> p q e", e=DROW)
@@ -205,6 +212,9 @@ def tile_lowrankconv3d_t_kernel(tc, x, U_kh, U_kw, U_kd, U_c_in, U_c_out, bias, 
             banks = mb[j]
             a = y1_rows(j, 0)
             c = c_h[:, 1, t : t + 1]
+            if first_group(j):
+                nc.scalar.activation(out=a[:, 0:32, :], in_=rows(banks[0][:]), func=ACTF.Copy, scale=c)
+                return
             nc.scalar.activation(out=a[:, 0:16, :], in_=rows(banks[0][:, SLICE:CHUNK]), func=ACTF.Copy, scale=c)
             for k in range(1, ns // 2):
                 nc.scalar.activation(out=a[:, 32 * k - 16 : 32 * k + 16, :], in_=rows(banks[k][:]), func=ACTF.Copy, scale=c)
@@ -216,6 +226,13 @@ def tile_lowrankconv3d_t_kernel(tc, x, U_kh, U_kw, U_kd, U_c_in, U_c_out, bias, 
             banks = mb[j]
             a = y1_rows(j, 0)
             c = c_h[:, 2 * side, t : t + 1]
+            if first_group(j):
+                if side == 0:
+                    mac(a[:, 16:32, :], a[:, 16:32, :], rows(banks[0][:, 0:SLICE]), c)
+                else:
+                    mac(a[:, 0:16, :], a[:, 0:16, :], rows(banks[0][:, SLICE:CHUNK]), c)
+                    mac(a[:, 16:32, :], a[:, 16:32, :], rows(banks[1][:, 0:SLICE]), c)
+                return
             for k in range(ns // 2):
                 lo, hi = 32 * k, 32 * k + 32
                 if side == 0 and k == 0 and s0 == 0:
@@ -246,19 +263,16 @@ def tile_lowrankconv3d_t_kernel(tc, x, U_kh, U_kw, U_kd, U_c_in, U_c_out, bias, 
             v = y2[j][:, 16 + off : 16 + off + 2 * WSLICE].rearrange("p (s r) -> p s r", r=WSLICE)
             return v[:, :, 0:SLICE]
 
-        def w_direct(j, side):
+        def w_direct(j, s, side):
             c, t = N_CHUNKS - 1, steps[j][3]
             if c not in yd:
                 a = ytp.tile([P, 4, 512], BF16, align_bytes=64, name="yt")
                 yd[c] = a
+            o = y2[j][:, 3 * SLICE : 4 * SLICE]
             if side:
-                o = y2p.tile([P, 4 * SLICE], F32, align_bytes=64, name="y2")
-                right[j] = o
-            o = right[j][:, 0:CHUNK].rearrange("p (s r) -> p s r", r=SLICE)
-            if side:
-                mac(o, padded(j, 0), padded(j, 16), c_r[:, 1, t, 0:1])
+                mac(o, padded(j, 0)[:, s, :], padded(j, 16)[:, s, :], c_r[:, 1, t, 0:1])
             else:
-                mac(yd[c][:, t, :].rearrange("p (s r) -> p s r", r=SLICE), o, padded(j, -16), c_r[:, 0, t, 0:1])
+                mac(yd[c][:, t, s * SLICE : (s + 1) * SLICE], o, padded(j, -16)[:, s, :], c_r[:, 0, t, 0:1])
 
         def gather_direct(c, k, eng):
             if c not in yg:
@@ -376,8 +390,15 @@ def tile_lowrankconv3d_t_kernel(tc, x, U_kh, U_kw, U_kd, U_c_in, U_c_out, bias, 
 
         def evac(c, ot, k, n, eng):
             b, cc = divmod(c, 8)
-            o = osp.tile([P, CHUNK], F32, name="osb")
-            dst = o[:, 0 : n * SLICE]
+            if n == 2:
+                o = osp.tile([P, CHUNK], F32, name="osb")
+                dst = o[:]
+            else:
+                if (c, "out") not in raw:
+                    r = rawp.tile([P, 4, 2 * CHUNK], BF16, name="raw")
+                    raw[(c, "out")] = r[:].rearrange("p j w -> p (j w)").bitcast(F32)
+                lo = (2 * k + ot) * SLICE
+                dst = raw[(c, "out")][:, lo : lo + SLICE]
             src = po[(c, ot, k)][:, 0 : n * SLICE]
             if eng == "v":
                 nc.vector.tensor_scalar_add(out=dst, in0=src, scalar1=bias_f[:, ot : ot + 1])
@@ -394,21 +415,21 @@ def tile_lowrankconv3d_t_kernel(tc, x, U_kh, U_kw, U_kd, U_c_in, U_c_out, bias, 
         nc.sync.dma_start(out=k_rows[0:3, :], in_=U_kh)
         nc.sync.dma_start(out=k_rows[3:6, :], in_=U_kw)
         nc.sync.dma_start(out=k_rows[6:9, :], in_=U_kd)
-        load_x(1, 1)
         nc.sync.dma_start(out=w_raw[:], in_=U_c_in.rearrange("(p j) r -> p j r", j=4))
+        load_x(1, 1)
         load_x(2, 2)
         load_x(4, 2)
         with nc.allow_non_contiguous_dma(reason="256 bias values, one per partition and output tile"):
             nc.scalar.dma_start(out=bias_b[:], in_=bias.rearrange("(j p) -> p j", p=P))
         nc.scalar.dma_start(out=v_raw[:], in_=U_c_out.rearrange("(p j) o -> p j o", j=4))
         for n in range(RING):
-            nc.gpsimd.memset(y1_ring[n][:], 0.0)
+            rows_of = y1_ring[n][:, 8 : 8 + 64 * DROW].rearrange("p (q e) -> p q e", e=DROW)
+            nc.vector.memset(y1_ring[n][:, 0:4], 0.0)
+            nc.vector.memset(rows_of[:, :, 12:16], 0.0)
         for n in range(P_RING):
             for ring in (pa_ring, pc_ring):
-                nc.gpsimd.memset(ring[n][:, 0:16], 0.0)
-                nc.gpsimd.memset(
-                    ring[n][:, 16 : 16 + 4 * WSLICE].rearrange("p (s r) -> p s r", r=WSLICE)[:, :, SLICE:WSLICE], 0.0
-                )
+                nc.vector.memset(ring[n][:, 0 : 4 * WSLICE].rearrange("p (s r) -> p s r", r=WSLICE)[:, :, 0:16], 0.0)
+                nc.vector.memset(ring[n][:, 4 * WSLICE : 4 * WSLICE + 16], 0.0)
 
         first_use = {}
         complete = {}
@@ -462,10 +483,18 @@ def tile_lowrankconv3d_t_kernel(tc, x, U_kh, U_kw, U_kd, U_c_in, U_c_out, bias, 
                     for j in moves[m]:
                         h_tap(j, side)
             if 0 < m + 1 < n_moves:
-                for j in moves[m + 1]:
-                    mm1(j)
-                    centre(j)
+                if m == 0:
+                    for k in range(2):
+                        for j in moves[1]:
+                            mm1_bank(j, k)
+                    for j in moves[1]:
+                        centre(j)
+                else:
+                    for j in moves[m + 1]:
+                        mm1(j)
+                        centre(j)
             if m == -1:
+                regroup_x(1, 1, 0, SLICE, "g")
                 for c, side in x_half.get(-1, [])[:2]:
                     regroup_shared(c, side)
             if m == 0:
@@ -498,15 +527,17 @@ def tile_lowrankconv3d_t_kernel(tc, x, U_kh, U_kw, U_kd, U_c_in, U_c_out, bias, 
                 for c in y_quant.get(m, []):
                     quant_y(c, 0, 2)
             if m == n_moves:
-                for i, c in ((0, N_CHUNKS - 4), (2, N_CHUNKS - 3)):
-                    quant_y(c, 0, 2)
-                    for side in (1, 0):
-                        for j in range(n_steps - DIRECT + i, n_steps - DIRECT + i + 2):
-                            w_direct(j, side)
-                gather_direct(N_CHUNKS - 1, 1, "a")
-                gather_direct(N_CHUNKS - 1, 0, "v")
+                for s in range(2):
+                    quant_y(N_CHUNKS - 4 + s, 0, 2)
+                    for i in range(0, DIRECT, 2):
+                        for side in (1, 0):
+                            for j in range(n_steps - DIRECT + i, n_steps - DIRECT + i + 2):
+                                w_direct(j, s, side)
+                    if s == 0:
+                        gather_direct(N_CHUNKS - 1, 0, "a")
             if m == n_moves + 1:
                 quant_y(N_CHUNKS - 1, 0, 1)
+                gather_direct(N_CHUNKS - 1, 1, "v")
                 quant_y(N_CHUNKS - 2, 0, 2)
                 quant_y(N_CHUNKS - 1, 1, 1)
             if 0 <= m - 1 < n_moves - 1:
@@ -515,6 +546,8 @@ def tile_lowrankconv3d_t_kernel(tc, x, U_kh, U_kw, U_kd, U_c_in, U_c_out, bias, 
             if 0 <= m < n_moves:
                 for j in moves[m]:
                     d_tap(j, 0)
+            if m == 0:
+                quant_x(1, 1, 1)
             for c in x_quant.get(m, []) if 0 <= m <= 1 else []:
                 quant_x(c, 0, 2)
             if 0 <= m - 2 < n_moves - 2:
@@ -551,12 +584,13 @@ def tile_lowrankconv3d_t_kernel(tc, x, U_kh, U_kw, U_kd, U_c_in, U_c_out, bias, 
             for t in range(4):
                 nc.tensor.matmul(k_bank[:, t, :], lhsT=k_perm[:, t, :], rhs=ident_b[:], start=True, stop=True)
             quant_x(0, 0, 1)
-            regroup_x(1, 1, 0, SLICE, "a")
+            for t in (2, 3):
+                regroup_w(t, "a")
             quant_x(0, 1, 1)
             nc.vector.tensor_copy(out=cf[:], in_=k_bank[:])
             taps = cf[:, :, 3:9].rearrange("p t (a k) -> p t a k", k=3)
             flat = cf[:, :, 3:9]
-            regroup_x(1, 0, 0, SLICE, "v")
+            regroup_w(0, "v")
             nc.vector.scalar_tensor_tensor(
                 out=c_abs[:].rearrange("p t a k -> p t (a k)"),
                 in0=flat,
@@ -565,21 +599,17 @@ def tile_lowrankconv3d_t_kernel(tc, x, U_kh, U_kw, U_kd, U_c_in, U_c_out, bias, 
                 op0=ALU.mult,
                 op1=ALU.max,
             )
-            quant_x(1, 0, 1)
+            quant_w(0)
             nc.vector.tensor_reduce(out=c_max[:], in_=c_abs[:], op=ALU.max, axis=AX.X)
-            for t in (2, 3):
-                regroup_w(t, "a")
-            regroup_w(0, "v")
+            regroup_w(1, "v")
             nc.vector.tensor_scalar(
                 out=c_max[:], in0=c_max[:], scalar1=2.0**-32, scalar2=2.0**-100, op0=ALU.mult, op1=ALU.add
             )
-            quant_w(0)
+            quant_w(1)
             nc.vector.tensor_tensor(out=c_small[:], in0=c_abs[:, :, :, 1], in1=c_max[:], op=ALU.is_lt)
-            regroup_w(1, "v")
             nc.vector.scalar_tensor_tensor(
                 out=c_small[:], in0=c_small[:], scalar=2.0, in1=c_max[:], op0=ALU.mult, op1=ALU.mult
             )
-            quant_w(1)
             nc.vector.tensor_tensor(out=c_piv[:], in0=taps[:, :, :, 1], in1=c_small[:], op=ALU.add)
             nc.vector.tensor_tensor(out=c_pp[:], in0=c_piv[:, :, 0], in1=c_piv[:, :, 1], op=ALU.mult)
             nc.vector.tensor_tensor(
@@ -589,13 +619,16 @@ def tile_lowrankconv3d_t_kernel(tc, x, U_kh, U_kw, U_kd, U_c_in, U_c_out, bias, 
                 op=ALU.mult,
             )
             nc.vector.reciprocal(out=c_rec[:], in_=c_piv[:])
+            regroup_x(1, 0, 0, SLICE, "a")
             quant_w(2)
             quant_w(3)
-            quant_x(1, 1, 1)
             for k in range(2):
                 nc.vector.tensor_tensor(out=c_r[:, k], in0=taps[:, :, :, 2 * k], in1=c_rec[:], op=ALU.mult)
+            quant_x(1, 0, 1)
+            for k in range(2):
+                for j in moves[0]:
+                    mm1_bank(j, k)
             for j in moves[0]:
-                mm1(j)
                 centre(j)
             for m in range(-1, 1):
                 move(m)
@@ -608,4 +641,4 @@ def tile_lowrankconv3d_t_kernel(tc, x, U_kh, U_kw, U_kd, U_c_in, U_c_out, bias, 
                     mm2(c, ot, k, 1)
             for k in range(2):
                 for ot in range(2):
-                    evac(c, ot, k, 1, "va"[ot])
+                    evac(c, ot, k, 1, "v")

@@ -72,6 +72,7 @@ def tile_lowrankconv3d_t_kernel(tc, x, U_kh, U_kw, U_kd, U_c_in, U_c_out, bias, 
         c_h = const.tile([P, 3, 4], F32, name="c_h")
         c_r = const.tile([P, 2, 4, 2], F32, name="c_r")
         warm = const.tile([P, 1], F32, name="warm")
+        seen = const.tile([P, 1], F32, name="seen")
         bias_b = const.tile([P, 2], BF16, name="bias_b")
         bias_f = const.tile([P, 2], F32, name="bias_f")
         y1_ring = []
@@ -255,9 +256,11 @@ def tile_lowrankconv3d_t_kernel(tc, x, U_kh, U_kw, U_kd, U_c_in, U_c_out, bias, 
                     acc = y1_rows(j, 0)[:, 16 * s : 16 * s + 16, :] if k == 0 else v
                     mac(v, acc, y1_rows(j, -1 if k == 0 else 1)[:, 16 * s : 16 * s + 16, :], c_r[:, k, t, 1:2])
                 return
-            v = rows(y2[j][:, 0 : ns * SLICE])
-            acc = y1_rows(j, 0)[:, 0 : 16 * ns, :] if k == 0 else v
-            mac(v, acc, y1_rows(j, -1 if k == 0 else 1)[:, 0 : 16 * ns, :], c_r[:, k, t, 1:2])
+            for s in range(0, ns, 2):
+                v = rows(y2[j][:, s * SLICE : (s + 2) * SLICE])
+                lo, hi = 16 * s, 16 * s + 32
+                acc = y1_rows(j, 0)[:, lo:hi, :] if k == 0 else v
+                mac(v, acc, y1_rows(j, -1 if k == 0 else 1)[:, lo:hi, :], c_r[:, k, t, 1:2])
 
         def padded(j, off):
             v = y2[j][:, 16 + off : 16 + off + 2 * WSLICE].rearrange("p (s r) -> p s r", r=WSLICE)
@@ -476,6 +479,15 @@ def tile_lowrankconv3d_t_kernel(tc, x, U_kh, U_kw, U_kd, U_c_in, U_c_out, bias, 
                 if side == 0 and c % 2 == 0 and c > 7:
                     load_x(c, 2)
             if 0 <= m - 2 < n_moves - 2:
+                if m - 1 < n_moves:
+                    nc.gpsimd.tensor_scalar(
+                        out=seen[:],
+                        in0=y2[moves[m - 1][-1]][:, 0:1],
+                        scalar1=1.0,
+                        scalar2=0.0,
+                        op0=ALU.mult,
+                        op1=ALU.add,
+                    )
                 for j in moves[m - 2]:
                     w_products(j)
             if 0 <= m < n_moves:
@@ -494,7 +506,7 @@ def tile_lowrankconv3d_t_kernel(tc, x, U_kh, U_kw, U_kd, U_c_in, U_c_out, bias, 
                         mm1(j)
                         centre(j)
             if m == -1:
-                regroup_x(1, 1, 0, SLICE, "g")
+                regroup_x(1, 1, 0, SLICE, "v")
                 for c, side in x_half.get(-1, [])[:2]:
                     regroup_shared(c, side)
             if m == 0:

@@ -40,7 +40,7 @@ def tile_lowrankconv3d_t_kernel(tc, x, U_kh, U_kw, U_kd, U_c_in, U_c_out, bias, 
         y2p = ctx.enter_context(tc.tile_pool(name="y2p", bufs=RING))
         ytp = ctx.enter_context(tc.tile_pool(name="ytp", bufs=3))
         ygp = ctx.enter_context(tc.tile_pool(name="ygp", bufs=2))
-        yqp = ctx.enter_context(tc.tile_pool(name="yqp", bufs=2))
+        yqp = ctx.enter_context(tc.tile_pool(name="yqp", bufs=3))
         osp = ctx.enter_context(tc.tile_pool(name="osp", bufs=6))
         mbp = ctx.enter_context(tc.psum_pool(name="mbp", bufs=4))
         tbp = ctx.enter_context(tc.psum_pool(name="tbp", bufs=2))
@@ -60,7 +60,7 @@ def tile_lowrankconv3d_t_kernel(tc, x, U_kh, U_kw, U_kd, U_c_in, U_c_out, bias, 
         ds = const.tile([P, 256], U8, align_bytes=64, name="ds")
         ident = const.tile([P, P], F32, align_bytes=64, name="ident")
         ident_b = const.tile([P, 16], BF16, name="ident_b")
-        k_rows = const.tile([P, 512], BF16, name="k_rows")
+        k_rows = const.tile([9, 512], BF16, name="k_rows")
         k_perm = const.tile([P, 4, P], BF16, name="k_perm")
         cf = const.tile([P, 4, 16], F32, name="cf")
         c_abs = const.tile([P, 4, 2, 3], F32, name="c_abs")
@@ -410,14 +410,18 @@ def tile_lowrankconv3d_t_kernel(tc, x, U_kh, U_kw, U_kd, U_c_in, U_c_out, bias, 
             lo = cc * CHUNK + k * SLICE
             nc.sync.dma_start(out=ov[b][ot * P : (ot + 1) * P, lo : lo + n * SLICE], in_=dst)
 
-        nc.vector.memset(k_rows[:], 0.0)
+        nc.vector.memset(k_perm[:], 0.0)
         nc.vector.memset(warm[:], 0.0)
         nc.scalar.copy(out=bias_f[:, 0:1], in_=warm[:])
         make_identity(nc, ident[:])
-        load_x(0, 1)
         nc.sync.dma_start(out=k_rows[0:3, :], in_=U_kh)
         nc.sync.dma_start(out=k_rows[3:6, :], in_=U_kw)
         nc.sync.dma_start(out=k_rows[6:9, :], in_=U_kd)
+        r = headp.tile([P, 4, CHUNK], BF16, name="raw_head")
+        for side in range(2):
+            lo = side * SLICE
+            nc.sync.dma_start(out=r[:, :, lo : lo + SLICE], in_=xv[0][:, :, lo : lo + SLICE])
+        raw[0] = r[:]
         nc.sync.dma_start(out=w_raw[:], in_=U_c_in.rearrange("(p j) r -> p j r", j=4))
         load_x(1, 1)
         load_x(2, 2)
@@ -452,9 +456,9 @@ def tile_lowrankconv3d_t_kernel(tc, x, U_kh, U_kw, U_kd, U_c_in, U_c_out, bias, 
                 at = min(at, x_step[c + 1] - 2)
             x_step[c] = at
         y_step = {}
-        for c in range(N_CHUNKS):
-            at = complete[c] + 3
-            y_step[c] = max(at, y_step[c - 1] + (2 if c < 13 else 1)) if c else at
+        for c in range(N_CHUNKS - 1):
+            at = complete[c] + (3 if c < 14 else 2)
+            y_step[c] = max(at, y_step[c - 1] + (2 if c < 13 else 14 - c)) if c else at
         x_quant = {}
         x_half = {}
         for c in range(2, N_CHUNKS):
@@ -469,7 +473,7 @@ def tile_lowrankconv3d_t_kernel(tc, x, U_kh, U_kw, U_kd, U_c_in, U_c_out, bias, 
             y_quant.setdefault(y_step[c] + (2 if c < 13 else 1), []).append(c)
 
         def regroup_shared(c, side):
-            g = G_COLS if c > 4 else 0
+            g = G_COLS if c > 2 else 0
             if g:
                 regroup_x(c, side, 0, g, "g")
             regroup_x(c, side, g, SLICE - g, "a")
@@ -545,12 +549,12 @@ def tile_lowrankconv3d_t_kernel(tc, x, U_kh, U_kw, U_kd, U_c_in, U_c_out, bias, 
                         for side in (1, 0):
                             for j in range(n_steps - DIRECT + i, n_steps - DIRECT + i + 2):
                                 w_direct(j, s, side)
+                        if s == 1 and i == 0:
+                            quant_y(N_CHUNKS - 2, 0, 2)
+                            quant_y(N_CHUNKS - 1, 0, 1)
                     if s == 0:
                         gather_direct(N_CHUNKS - 1, 0, "a")
-            if m == n_moves + 1:
-                quant_y(N_CHUNKS - 1, 0, 1)
                 gather_direct(N_CHUNKS - 1, 1, "v")
-                quant_y(N_CHUNKS - 2, 0, 2)
                 quant_y(N_CHUNKS - 1, 1, 1)
             if 0 <= m - 1 < n_moves - 1:
                 for j in moves[m - 1]:
@@ -585,24 +589,22 @@ def tile_lowrankconv3d_t_kernel(tc, x, U_kh, U_kw, U_kd, U_c_in, U_c_out, bias, 
         head_engines = {mybir.EngineType.DVE, mybir.EngineType.Pool, mybir.EngineType.PE, mybir.EngineType.Activation}
         with tc.manual_schedule(engines=head_engines):
             regroup_x(0, 1, 0, SLICE, "a")
-            regroup_x(0, 0, 0, SLICE, "v")
             nc.vector.tensor_copy(out=ident_b[:], in_=ident[:, 0:16])
             for u in range(2):
                 nc.vector.tensor_copy(
-                    out=k_perm[:, 2 * u : 2 * u + 2, :].rearrange("p h (m e) -> p h m e", e=2),
+                    out=k_perm[0:9, 2 * u : 2 * u + 2, :].rearrange("p h (m e) -> p h m e", e=2),
                     in_=k_rows[:].rearrange("p (h m u e) -> p u h m e", h=2, u=2, e=2)[:, u],
                 )
             k_bank = wop.tile([P, 4, 16], F32, name="wo")
             for t in range(4):
                 nc.tensor.matmul(k_bank[:, t, :], lhsT=k_perm[:, t, :], rhs=ident_b[:], start=True, stop=True)
-            quant_x(0, 0, 1)
-            for t in (2, 3):
+            regroup_x(0, 0, 0, SLICE, "v")
+            for t in range(1, 4):
                 regroup_w(t, "a")
-            quant_x(0, 1, 1)
             nc.vector.tensor_copy(out=cf[:], in_=k_bank[:])
             taps = cf[:, :, 3:9].rearrange("p t (a k) -> p t a k", k=3)
             flat = cf[:, :, 3:9]
-            regroup_w(0, "v")
+            quant_x(0, 0, 1)
             nc.vector.scalar_tensor_tensor(
                 out=c_abs[:].rearrange("p t a k -> p t (a k)"),
                 in0=flat,
@@ -611,32 +613,33 @@ def tile_lowrankconv3d_t_kernel(tc, x, U_kh, U_kw, U_kd, U_c_in, U_c_out, bias, 
                 op0=ALU.mult,
                 op1=ALU.max,
             )
-            quant_w(0)
             nc.vector.tensor_reduce(out=c_max[:], in_=c_abs[:], op=ALU.max, axis=AX.X)
-            regroup_w(1, "v")
             nc.vector.tensor_scalar(
                 out=c_max[:], in0=c_max[:], scalar1=2.0**-32, scalar2=2.0**-100, op0=ALU.mult, op1=ALU.add
             )
-            quant_w(1)
             nc.vector.tensor_tensor(out=c_small[:], in0=c_abs[:, :, :, 1], in1=c_max[:], op=ALU.is_lt)
             nc.vector.scalar_tensor_tensor(
                 out=c_small[:], in0=c_small[:], scalar=2.0, in1=c_max[:], op0=ALU.mult, op1=ALU.mult
             )
+            regroup_w(0, "v")
             nc.vector.tensor_tensor(out=c_piv[:], in0=taps[:, :, :, 1], in1=c_small[:], op=ALU.add)
+            quant_w(0)
             nc.vector.tensor_tensor(out=c_pp[:], in0=c_piv[:, :, 0], in1=c_piv[:, :, 1], op=ALU.mult)
+            quant_x(0, 1, 1)
             nc.vector.tensor_tensor(
                 out=c_h[:],
                 in0=cf[:].rearrange("p t k -> p k t")[:, 0:3, :],
                 in1=c_pp[:].unsqueeze(1).to_broadcast([P, 3, 4]),
                 op=ALU.mult,
             )
+            quant_w(1)
             nc.vector.reciprocal(out=c_rec[:], in_=c_piv[:])
-            regroup_x(1, 0, 0, SLICE, "a")
-            quant_w(2)
-            quant_w(3)
+            regroup_x(1, 0, 0, SLICE, "v")
             for k in range(2):
                 nc.vector.tensor_tensor(out=c_r[:, k], in0=taps[:, :, :, 2 * k], in1=c_rec[:], op=ALU.mult)
             quant_x(1, 0, 1)
+            quant_w(2)
+            quant_w(3)
             for k in range(2):
                 for j in moves[0]:
                     mm1_bank(j, k)
@@ -653,4 +656,4 @@ def tile_lowrankconv3d_t_kernel(tc, x, U_kh, U_kw, U_kd, U_c_in, U_c_out, bias, 
                     mm2(c, ot, k, 1)
             for k in range(2):
                 for ot in range(2):
-                    evac(c, ot, k, 1, "v")
+                    evac(c, ot, k, 1, "v" if k == 1 and ot == 0 else "a")

@@ -473,7 +473,7 @@ def tile_lowrankconv3d_t_kernel(tc, x, U_kh, U_kw, U_kd, U_c_in, U_c_out, bias, 
             y_quant.setdefault(y_step[c] + (2 if c < 13 else 1), []).append(c)
 
         def regroup_shared(c, side):
-            g = G_COLS if c > 2 else 0
+            g = G_COLS if c > 7 else 0
             if g:
                 regroup_x(c, side, 0, g, "g")
             regroup_x(c, side, g, SLICE - g, "a")

@@ -473,7 +473,7 @@ def tile_lowrankconv3d_t_kernel(tc, x, U_kh, U_kw, U_kd, U_c_in, U_c_out, bias, 
             y_quant.setdefault(y_step[c] + (2 if c < 13 else 1), []).append(c)
 
         def regroup_shared(c, side):
-            g = G_COLS if c > 7 else 0
+            g = G_COLS if c > 4 else 0
             if g:
                 regroup_x(c, side, 0, g, "g")
             regroup_x(c, side, g, SLICE - g, "a")

from contextlib import ExitStack

import concourse.mybir as mybir
from concourse.masks import make_identity

FLOPS = 2 * 512 * 512 * 8192 + 2 * 512 * 256 * 8192 + 2 * 9 * 512 * 8192

F32 = mybir.dt.float32
BF16 = mybir.dt.bfloat16
U32 = mybir.dt.uint32
U8 = mybir.dt.uint8
FP8X4 = mybir.dt.float8_e4m3fn_x4
ACTF = mybir.ActivationFunctionType
ALU = mybir.AluOpType
AX = mybir.AxisListType

P = 128
SLICE = 256
CHUNK = 512
N_CHUNKS = 16
GROUPS = ((2, 2, 4, 4, 4), (4, 4, 4, 2, 2))
DROW = 20
WSLICE = 272
RING = 6
P_RING = 4
DIRECT = 4
G_COLS = 128


def tile_lowrankconv3d_t_kernel(tc, x, U_kh, U_kw, U_kd, U_c_in, U_c_out, bias, out):
    nc = tc.nc
    xv = [x[b].rearrange("(p j) h w d -> p j (h w d)", j=4) for b in range(2)]
    ov = [out[b].rearrange("o h w d -> o (h w d)") for b in range(2)]

    with ExitStack() as ctx:
        const = ctx.enter_context(tc.tile_pool(name="const", bufs=1))
        rawp = ctx.enter_context(tc.tile_pool(name="rawp", bufs=3))
        headp = ctx.enter_context(tc.tile_pool(name="headp", bufs=2))
        xgp = ctx.enter_context(tc.tile_pool(name="xgp", bufs=3))
        y2p = ctx.enter_context(tc.tile_pool(name="y2p", bufs=RING))
        ytp = ctx.enter_context(tc.tile_pool(name="ytp", bufs=3))
        ygp = ctx.enter_context(tc.tile_pool(name="ygp", bufs=2))
        yqp = ctx.enter_context(tc.tile_pool(name="yqp", bufs=3))
        osp = ctx.enter_context(tc.tile_pool(name="osp", bufs=6))
        mbp = ctx.enter_context(tc.psum_pool(name="mbp", bufs=4))
        tbp = ctx.enter_context(tc.psum_pool(name="tbp", bufs=2))
        wop = ctx.enter_context(tc.psum_pool(name="wop", bufs=2))

        xq = const.tile([P, N_CHUNKS * CHUNK], U32, align_bytes=64, name="xq")
        xs = const.tile([P, N_CHUNKS * CHUNK], U8, align_bytes=64, name="xs")
        w_raw = const.tile([P, 4, 512], BF16, name="w_raw")
        w_grp = const.tile([P, 512, 4], BF16, align_bytes=64, name="w_grp")
        wq = const.tile([P, 512], U32, align_bytes=64, name="wq")
        ws = const.tile([P, 512], U8, align_bytes=64, name="ws")
        v_raw = const.tile([P, 4, 256], BF16, name="v_raw")
        v_grp = const.tile([P, 256, 4], BF16, align_bytes=64, name="v_grp")
        vq = const.tile([P, 256], U32, align_bytes=64, name="vq")
        vs = const.tile([P, 256], U8, align_bytes=64, name="vs")
        dq = const.tile([P, 256], U32, align_bytes=64, name="dq")
        ds = const.tile([P, 256], U8, align_bytes=64, name="ds")
        ident = const.tile([P, P], F32, align_bytes=64, name="ident")
        ident_b = const.tile([P, 16], BF16, name="ident_b")
        k_rows = const.tile([9, 512], BF16, name="k_rows")
        k_perm = const.tile([P, 4, P], BF16, name="k_perm")
        cf = const.tile([P, 4, 16], F32, name="cf")
        c_abs = const.tile([P, 4, 2, 3], F32, name="c_abs")
        c_max = const.tile([P, 4, 2], F32, name="c_max")
        c_small = const.tile([P, 4, 2], F32, name="c_small")
        c_piv = const.tile([P, 4, 2], F32, name="c_piv")
        c_rec = const.tile([P, 4, 2], F32, name="c_rec")
        c_pp = const.tile([P, 4], F32, name="c_pp")
        c_h = const.tile([P, 3, 4], F32, name="c_h")
        c_r = const.tile([P, 2, 4, 2], F32, name="c_r")
        warm = const.tile([P, 1], F32, name="warm")
        seen = const.tile([P, 1], F32, name="seen")
        bias_b = const.tile([P, 2], BF16, name="bias_b")
        bias_f = const.tile([P, 2], F32, name="bias_f")
        y1_ring = []
        pa_ring = []
        pc_ring = []
        for n in range(RING):
            a = const.tile([P, 8 + 64 * DROW], F32, align_bytes=64, name=f"y1_{n}")
            y1_ring.append(a)
        for n in range(P_RING):
            a = const.tile([P, 16 + 4 * WSLICE], F32, align_bytes=64, name=f"pa_{n}")
            pa_ring.append(a)
            a = const.tile([P, 16 + 4 * WSLICE], F32, align_bytes=64, name=f"pc_{n}")
            pc_ring.append(a)

        raw = {}
        xg = {}
        mb = {}
        y2 = {}
        yt = {}
        wb = {}
        tb = {}
        yd = {}
        yg = {}
        yq = {}
        ys = {}
        po = {}

        def load_x(c0, n):
            b, cc = divmod(c0, 8)
            if n == 1:
                r = headp.tile([P, 4, CHUNK], BF16, name="raw_head")
            else:
                r = rawp.tile([P, 4, 2 * CHUNK], BF16, name="raw")
            nc.sync.dma_start(out=r[:, :, 0 : n * CHUNK], in_=xv[b][:, :, cc * CHUNK : (cc + n) * CHUNK])
            for k in range(n):
                raw[c0 + k] = r[:, :, k * CHUNK : (k + 1) * CHUNK]

        def regroup_x(c, side, first, count, eng):
            if c not in xg:
                g = xgp.tile([P, CHUNK, 4], BF16, align_bytes=64, name="xg")
                xg[c] = g
            lo = side * SLICE + first
            src = raw[c][:, :, lo : lo + count].rearrange("p t (c i) -> p c t i", i=4)
            dst = xg[c][:, lo : lo + count, :].rearrange("p (c i) t -> p c t i", i=4)
            if eng == "v":
                nc.vector.tensor_copy(out=dst, in_=src)
            elif eng == "g":
                nc.gpsimd.tensor_scalar(out=dst, in0=src, scalar1=1.0, scalar2=0.0, op0=ALU.mult, op1=ALU.add)
            else:
                nc.scalar.copy(out=dst, in_=src)

        def quant_x(c, first, count):
            c0 = c * CHUNK + first * SLICE
            n = count * SLICE
            nc.vector.quantize_mx(
                out=xq[:, c0 : c0 + n].bitcast(FP8X4),
                scales=xs[:, c0 : c0 + n],
                in_=xg[c][:, first * SLICE : first * SLICE + n, :].rearrange("p w j -> p (w j)"),
            )

        def regroup_w(t, eng):
            u, h = divmod(t, 2)
            dst = w_grp[:, t * P : (t + 1) * P, :].rearrange("p (m e) j -> p m e j", e=2)
            src = w_raw[:].rearrange("p j (h m u e) -> p h u m e j", h=2, u=2, e=2)[:, h, u]
            if eng == "v":
                nc.vector.tensor_copy(out=dst, in_=src)
            else:
                nc.scalar.copy(out=dst, in_=src)

        def quant_w(t):
            nc.vector.quantize_mx(
                out=wq[:, t * P : (t + 1) * P].bitcast(FP8X4),
                scales=ws[:, t * P : (t + 1) * P],
                in_=w_grp[:, t * P : (t + 1) * P, :].rearrange("p r j -> p (r j)"),
            )

        steps = []
        moves = []
        for b in range(2):
            s0 = 0
            for n in GROUPS[b]:
                for t in range(4):
                    if n == 4 or t % 2 == 0:
                        moves.append([])
                    moves[-1].append(len(steps))
                    steps.append((b, s0, n, t))
                s0 += n
        n_moves = len(moves)
        n_steps = len(steps)

        def first_group(j):
            b, s0, ns, t = steps[j]
            return b == 0 and s0 == 0 and ns == 2

        def mm1(j):
            for k in range(steps[j][2] // 2 + 1):
                mm1_bank(j, k)

        def mm1_bank(j, k):
            b, s0, ns, t = steps[j]
            if True:
                lo, o0, n = s0 - 1 + 2 * k, 0, CHUNK
                if first_group(j):
                    lo, n = 2 * k, CHUNK - k * SLICE
                elif lo < 0:
                    lo, o0, n = 0, SLICE, SLICE
                elif lo == 15:
                    n = SLICE
                c0 = b * 4096 + lo * SLICE
                bank = mbp.tile([P, CHUNK], F32, name="mb")
                nc.tensor.matmul_mx(
                    out=bank[:, o0 : o0 + n],
                    lhsT=wq[:, t * P : (t + 1) * P].bitcast(FP8X4),
                    lhsT_scale=ws[:, t * P : (t + 1) * P],
                    rhs=xq[:, c0 : c0 + n].bitcast(FP8X4),
                    rhs_scale=xs[:, c0 : c0 + n],
                    start=True,
                    stop=True,
                )
                mb.setdefault(j, []).append(bank)

        def y1_rows(j, off):
            v = y1_ring[j % RING][:, 4 + off : 4 + off + 64 * DROW].rearrange("p (q e) -> p q e", e=DROW)
            return v[:, :, 0:16]

        def rows(v):
            return v.rearrange("p (q d) -> p q d", d=16)

        def slices(tile, first, count):
            v = tile[:, 16 : 16 + 4 * WSLICE].rearrange("p (s r) -> p s r", r=WSLICE)
            return v[:, first : first + count, 0:SLICE]

        def mac(dst, acc, src, c):
            nc.vector.scalar_tensor_tensor(out=dst, in0=src, scalar=c, in1=acc, op0=ALU.mult, op1=ALU.add)

        def centre(j):
            b, s0, ns, t = steps[j]
            banks = mb[j]
            a = y1_rows(j, 0)
            c = c_h[:, 1, t : t + 1]
            if first_group(j):
                nc.scalar.activation(out=a[:, 0:32, :], in_=rows(banks[0][:]), func=ACTF.Copy, scale=c)
                return
            nc.scalar.activation(out=a[:, 0:16, :], in_=rows(banks[0][:, SLICE:CHUNK]), func=ACTF.Copy, scale=c)
            for k in range(1, ns // 2):
                nc.scalar.activation(out=a[:, 32 * k - 16 : 32 * k + 16, :], in_=rows(banks[k][:]), func=ACTF.Copy, scale=c)
            r = 16 * ns - 16
            nc.scalar.activation(out=a[:, r : r + 16, :], in_=rows(banks[-1][:, 0:SLICE]), func=ACTF.Copy, scale=c)

        def h_tap(j, side):
            b, s0, ns, t = steps[j]
            banks = mb[j]
            a = y1_rows(j, 0)
            c = c_h[:, 2 * side, t : t + 1]
            if first_group(j):
                if side == 0:
                    mac(a[:, 16:32, :], a[:, 16:32, :], rows(banks[0][:, 0:SLICE]), c)
                else:
                    mac(a[:, 0:16, :], a[:, 0:16, :], rows(banks[0][:, SLICE:CHUNK]), c)
                    mac(a[:, 16:32, :], a[:, 16:32, :], rows(banks[1][:, 0:SLICE]), c)
                return
            for k in range(ns // 2):
                lo, hi = 32 * k, 32 * k + 32
                if side == 0 and k == 0 and s0 == 0:
                    mac(a[:, 16:32, :], a[:, 16:32, :], rows(banks[0][:, SLICE:CHUNK]), c)
                elif side == 1 and k == ns // 2 - 1 and s0 + ns == 16:
                    mac(a[:, lo : lo + 16, :], a[:, lo : lo + 16, :], rows(banks[k + 1][:, 0:SLICE]), c)
                else:
                    mac(a[:, lo:hi, :], a[:, lo:hi, :], rows(banks[k + side][:]), c)

        def d_tap(j, k):
            b, s0, ns, t = steps[j]
            if k == 0:
                a = y2p.tile([P, 4 * SLICE], F32, align_bytes=64, name="y2")
                y2[j] = a
                if j >= n_steps - DIRECT:
                    nc.vector.memset(a[:, 0 : 3 * WSLICE].rearrange("p (s r) -> p s r", r=WSLICE)[:, :, 0:16], 0.0)
            if j >= n_steps - DIRECT:
                for s in range(2):
                    v = rows(padded(j, 0)[:, s, :])
                    acc = y1_rows(j, 0)[:, 16 * s : 16 * s + 16, :] if k == 0 else v
                    mac(v, acc, y1_rows(j, -1 if k == 0 else 1)[:, 16 * s : 16 * s + 16, :], c_r[:, k, t, 1:2])
                return
            for s in range(0, ns, 2):
                v = rows(y2[j][:, s * SLICE : (s + 2) * SLICE])
                lo, hi = 16 * s, 16 * s + 32
                acc = y1_rows(j, 0)[:, lo:hi, :] if k == 0 else v
                mac(v, acc, y1_rows(j, -1 if k == 0 else 1)[:, lo:hi, :], c_r[:, k, t, 1:2])

        def padded(j, off):
            v = y2[j][:, 16 + off : 16 + off + 2 * WSLICE].rearrange("p (s r) -> p s r", r=WSLICE)
            return v[:, :, 0:SLICE]

        def w_direct(j, s, side):
            c, t = N_CHUNKS - 1, steps[j][3]
            if c not in yd:
                a = ytp.tile([P, 4, 512], BF16, align_bytes=64, name="yt")
                yd[c] = a
            o = y2[j][:, 3 * SLICE : 4 * SLICE]
            if side:
                mac(o, padded(j, 0)[:, s, :], padded(j, 16)[:, s, :], c_r[:, 1, t, 0:1])
            else:
                mac(yd[c][:, t, s * SLICE : (s + 1) * SLICE], o, padded(j, -16)[:, s, :], c_r[:, 0, t, 0:1])

        def gather_direct(c, k, eng):
            if c not in yg:
                g = xgp.tile([P, CHUNK, 4], BF16, align_bytes=64, name="xg")
                yg[c] = g
            lo = k * SLICE
            src = yd[c][:, :, lo : lo + SLICE].rearrange("p t (c i) -> p c t i", i=4)
            dst = yg[c][:, lo : lo + SLICE, :].rearrange("p (c i) t -> p c t i", i=4)
            if eng == "v":
                nc.vector.tensor_copy(out=dst, in_=src)
            else:
                nc.scalar.copy(out=dst, in_=src)

        def w_products(j):
            b, s0, ns, t = steps[j]
            src = y2[j][:, 0 : ns * SLICE].rearrange("p (s r) -> p s r", r=SLICE)
            dst = slices(pa_ring[j % P_RING], 0, ns)
            c = c_r[:, 0, t, 0:1]
            nc.gpsimd.tensor_scalar(out=dst, in0=src, scalar1=c, scalar2=0.0, op0=ALU.mult, op1=ALU.add)
            dst = slices(pc_ring[j % P_RING], 0, ns)
            c = c_r[:, 1, t, 0:1]
            nc.scalar.activation(out=dst, in_=src, func=ACTF.Copy, scale=c)

        def w_sum(j, k):
            bank = tbp.tile([P, CHUNK], F32, name="tb")
            pa = pa_ring[j % P_RING]
            pc = pc_ring[j % P_RING]
            for q in range(4):
                s = 2 * k + q // 2
                flat = s * SLICE + (q % 2) * P
                base = 16 + s * WSLICE + (q % 2) * P
                parts = (y2[j][:, flat : flat + P], pa[:, base - 16 : base - 16 + P], pc[:, base + 16 : base + 16 + P])
                for i, part in enumerate(parts):
                    nc.tensor.matmul(
                        out=bank[:, q * P : (q + 1) * P],
                        lhsT=part,
                        rhs=ident[:],
                        is_transpose=True,
                        start=(i == 0),
                        stop=(i == 2),
                    )
            tb[(j, k)] = bank

        def round_y3(j, k):
            b, s0, ns, t = steps[j]
            c = 8 * b + s0 // 2 + k
            if c not in yt:
                a = ytp.tile([P, 4, 512], BF16, align_bytes=64, name="yt")
                yt[c] = a
            dst = yt[c][:, :, t * P : (t + 1) * P]
            src = tb[(j, k)][:].rearrange("p (q r) -> p q r", q=4)
            nc.scalar.copy(out=dst, in_=src)

        def turn_y3(c, k):
            if c == N_CHUNKS - 2:
                bank = mbp.tile([P, CHUNK], F32, name="mb")
            else:
                bank = wop.tile([P, CHUNK], F32, name="wo")
            for q in range(2):
                words = yt[c][:, 2 * k + q, :].bitcast(F32)
                for u in range(2):
                    nc.tensor.transpose(
                        bank[:, (2 * q + u) * P : (2 * q + u + 1) * P], words[:, u * P : (u + 1) * P], ident[:]
                    )
            wb[(c, k)] = bank

        def gather_y3(c, k, eng):
            if c not in yg:
                g = ygp.tile([P, CHUNK, 4], BF16, align_bytes=64, name="yg")
                yg[c] = g
            dst = (
                yg[c][:, k * SLICE : (k + 1) * SLICE, :]
                .rearrange("p n j -> p (n j)")
                .bitcast(F32)
                .rearrange("p (q n u) -> p q n u", q=2, u=2)
            )
            src = wb[(c, k)][:].rearrange("p (q u n) -> p q n u", q=2, u=2)
            if eng == "v":
                nc.vector.tensor_copy(out=dst, in_=src)
            else:
                nc.scalar.copy(out=dst, in_=src)

        def quant_y(c, k, n):
            if c not in yq:
                q = yqp.tile([P, CHUNK], U32, align_bytes=64, name="yq")
                sc = yqp.tile([P, CHUNK], U8, align_bytes=64, name="ys")
                yq[c] = q
                ys[c] = sc
            lo = k * SLICE
            hi = lo + n * SLICE
            nc.vector.quantize_mx(
                out=yq[c][:, lo:hi].bitcast(FP8X4),
                scales=ys[c][:, lo:hi],
                in_=yg[c][:, lo:hi, :].rearrange("p w j -> p (w j)"),
            )

        def mm2(c, ot, k, n):
            if c == N_CHUNKS - 1:
                bank = mbp.tile([P, CHUNK], F32, name="mb")
            else:
                bank = wop.tile([P, CHUNK], F32, name="wo")
            lo = k * SLICE
            hi = lo + n * SLICE
            q, sc = (dq, ds) if c == N_CHUNKS - 1 else (vq, vs)
            nc.tensor.matmul_mx(
                out=bank[:, 0 : n * SLICE],
                lhsT=q[:, ot * P : (ot + 1) * P].bitcast(FP8X4),
                lhsT_scale=sc[:, ot * P : (ot + 1) * P],
                rhs=yq[c][:, lo:hi].bitcast(FP8X4),
                rhs_scale=ys[c][:, lo:hi],
                start=True,
                stop=True,
            )
            po[(c, ot, k)] = bank

        def evac(c, ot, k, n, eng):
            b, cc = divmod(c, 8)
            if n == 2:
                o = osp.tile([P, CHUNK], F32, name="osb")
                dst = o[:]
            else:
                if (c, "out") not in raw:
                    r = rawp.tile([P, 4, 2 * CHUNK], BF16, name="raw")
                    raw[(c, "out")] = r[:].rearrange("p j w -> p (j w)").bitcast(F32)
                lo = (2 * k + ot) * SLICE
                dst = raw[(c, "out")][:, lo : lo + SLICE]
            src = po[(c, ot, k)][:, 0 : n * SLICE]
            if eng == "v":
                nc.vector.tensor_scalar_add(out=dst, in0=src, scalar1=bias_f[:, ot : ot + 1])
            else:
                nc.scalar.activation(out=dst, in_=src, func=ACTF.Identity, bias=bias_f[:, ot : ot + 1], scale=1.0)
            lo = cc * CHUNK + k * SLICE
            nc.sync.dma_start(out=ov[b][ot * P : (ot + 1) * P, lo : lo + n * SLICE], in_=dst)

        nc.vector.memset(k_perm[:], 0.0)
        nc.vector.memset(warm[:], 0.0)
        nc.scalar.copy(out=bias_f[:, 0:1], in_=warm[:])
        make_identity(nc, ident[:])
        nc.sync.dma_start(out=k_rows[0:3, :], in_=U_kh)
        nc.sync.dma_start(out=k_rows[3:6, :], in_=U_kw)
        nc.sync.dma_start(out=k_rows[6:9, :], in_=U_kd)
        r = headp.tile([P, 4, CHUNK], BF16, name="raw_head")
        for side in range(2):
            lo = side * SLICE
            nc.sync.dma_start(out=r[:, :, lo : lo + SLICE], in_=xv[0][:, :, lo : lo + SLICE])
        raw[0] = r[:]
        nc.sync.dma_start(out=w_raw[:], in_=U_c_in.rearrange("(p j) r -> p j r", j=4))
        load_x(1, 1)
        load_x(2, 2)
        load_x(4, 2)
        with nc.allow_non_contiguous_dma(reason="256 bias values, one per partition and output tile"):
            nc.scalar.dma_start(out=bias_b[:], in_=bias.rearrange("(j p) -> p j", p=P))
        nc.scalar.dma_start(out=v_raw[:], in_=U_c_out.rearrange("(p j) o -> p j o", j=4))
        for n in range(RING):
            rows_of = y1_ring[n][:, 8 : 8 + 64 * DROW].rearrange("p (q e) -> p q e", e=DROW)
            nc.vector.memset(y1_ring[n][:, 0:4], 0.0)
            nc.vector.memset(rows_of[:, :, 12:16], 0.0)
        for n in range(P_RING):
            for ring in (pa_ring, pc_ring):
                nc.vector.memset(ring[n][:, 0 : 4 * WSLICE].rearrange("p (s r) -> p s r", r=WSLICE)[:, :, 0:16], 0.0)
                nc.vector.memset(ring[n][:, 4 * WSLICE : 4 * WSLICE + 16], 0.0)

        first_use = {}
        complete = {}
        for m, js in enumerate(moves):
            for j in js:
                b, s0, ns, t = steps[j]
                for s in range(max(s0 - 1, 0), min(s0 + ns + 1, 16)):
                    first_use.setdefault(8 * b + s // 2, m)
                for k in range(ns // 2):
                    complete[8 * b + s0 // 2 + k] = m
        x_step = {}
        for c in reversed(range(2, N_CHUNKS)):
            at = first_use[c] - 2
            if c < 8:
                at = min(at, c - 2)
            elif c + 1 in x_step:
                at = min(at, x_step[c + 1] - 2)
            x_step[c] = at
        y_step = {}
        for c in range(N_CHUNKS - 1):
            at = complete[c] + (3 if c < 14 else 2)
            y_step[c] = max(at, y_step[c - 1] + (2 if c < 13 else 14 - c)) if c else at
        x_quant = {}
        x_half = {}
        for c in range(2, N_CHUNKS):
            at = x_step[c]
            x_quant.setdefault(max(at, -1), []).append(c)
            for side in range(2):
                x_half.setdefault(max(at - 2 + side, -1), []).append((c, side))
        y_turn = {}
        y_quant = {}
        for c in range(N_CHUNKS - 1):
            y_turn.setdefault(y_step[c], []).append(c)
            y_quant.setdefault(y_step[c] + (2 if c < 13 else 1), []).append(c)

        def regroup_shared(c, side):
            g = G_COLS if c > 4 else 0
            if g:
                regroup_x(c, side, 0, g, "g")
            regroup_x(c, side, g, SLICE - g, "a")

        def move(m):
            for c, side in x_half.get(m + 4, []) if m >= 0 else []:
                if side == 0 and c % 2 == 0 and c > 7:
                    load_x(c, 2)
            if 0 <= m - 2 < n_moves - 2:
                if m - 1 < n_moves:
                    nc.gpsimd.tensor_scalar(
                        out=seen[:],
                        in0=y2[moves[m - 1][-1]][:, 0:1],
                        scalar1=1.0,
                        scalar2=0.0,
                        op0=ALU.mult,
                        op1=ALU.add,
                    )
                for j in moves[m - 2]:
                    w_products(j)
            if 0 <= m < n_moves:
                for side in range(2):
                    for j in moves[m]:
                        h_tap(j, side)
            if 0 < m + 1 < n_moves:
                if m == 0:
                    for k in range(2):
                        for j in moves[1]:
                            mm1_bank(j, k)
                    for j in moves[1]:
                        centre(j)
                else:
                    for j in moves[m + 1]:
                        mm1(j)
                        centre(j)
            if m == -1:
                regroup_x(1, 1, 0, SLICE, "v")
                for c, side in x_half.get(-1, [])[:2]:
                    regroup_shared(c, side)
            if m == 0:
                for c, side in x_half.get(-1, [])[2:]:
                    regroup_shared(c, side)
            if m == 1:
                nc.scalar.copy(out=v_grp[:], in_=v_raw[:].rearrange("p j o -> p o j"))
                nc.scalar.copy(out=bias_f[:], in_=bias_b[:])
            if m == 3:
                nc.vector.quantize_mx(
                    out=vq[:].bitcast(FP8X4), scales=vs[:], in_=v_grp[:].rearrange("p o j -> p (o j)")
                )
            if m == 5:
                rows_out = U_c_out.rearrange("(h m u e) o -> h e m u o", h=2, u=2, e=2)
                for h in range(2):
                    for e in range(2):
                        nc.sync.dma_start(out=v_raw[e:P:2, h:4:2, :], in_=rows_out[h, e])
            if m == 9:
                nc.scalar.copy(out=v_grp[:], in_=v_raw[:].rearrange("p j o -> p o j"))
            if m == 11:
                nc.vector.quantize_mx(
                    out=dq[:].bitcast(FP8X4), scales=ds[:], in_=v_grp[:].rearrange("p o j -> p (o j)")
                )
            if m == n_moves:
                for j in moves[m - 1]:
                    d_tap(j, 1)
            for c in x_quant.get(m, []) if m > 1 else []:
                quant_x(c, 0, 2)
            if m < n_moves:
                for c in y_quant.get(m, []):
                    quant_y(c, 0, 2)
            if m == n_moves:
                for s in range(2):
                    quant_y(N_CHUNKS - 4 + s, 0, 2)
                    for i in range(0, DIRECT, 2):
                        for side in (1, 0):
                            for j in range(n_steps - DIRECT + i, n_steps - DIRECT + i + 2):
                                w_direct(j, s, side)
                        if s == 1 and i == 0:
                            quant_y(N_CHUNKS - 2, 0, 2)
                            quant_y(N_CHUNKS - 1, 0, 1)
                    if s == 0:
                        gather_direct(N_CHUNKS - 1, 0, "a")
                gather_direct(N_CHUNKS - 1, 1, "v")
                quant_y(N_CHUNKS - 1, 1, 1)
            if 0 <= m - 1 < n_moves - 1:
                for j in moves[m - 1]:
                    d_tap(j, 1)
            if 0 <= m < n_moves:
                for j in moves[m]:
                    d_tap(j, 0)
            if m == 0:
                quant_x(1, 1, 1)
            for c in x_quant.get(m, []) if 0 <= m <= 1 else []:
                quant_x(c, 0, 2)
            if 0 <= m - 2 < n_moves - 2:
                for j in moves[m - 2]:
                    for k in range(steps[j][2] // 2):
                        w_sum(j, k)
                        round_y3(j, k)
            if m >= 0:
                for c, side in x_half.get(m, []):
                    regroup_shared(c, side)
            for c in y_quant.get(m, []):
                for ot in range(2):
                    mm2(c, ot, 0, 2)
                for ot in range(2):
                    evac(c, ot, 0, 2, "a")
            for c in y_turn.get(m, []):
                for k in range(2):
                    turn_y3(c, k)
                for k in range(2):
                    gather_y3(c, k, "a")

        load_x(6, 2)
        head_engines = {mybir.EngineType.DVE, mybir.EngineType.Pool, mybir.EngineType.PE, mybir.EngineType.Activation}
        with tc.manual_schedule(engines=head_engines):
            regroup_x(0, 1, 0, SLICE, "a")
            nc.vector.tensor_copy(out=ident_b[:], in_=ident[:, 0:16])
            for u in range(2):
                nc.vector.tensor_copy(
                    out=k_perm[0:9, 2 * u : 2 * u + 2, :].rearrange("p h (m e) -> p h m e", e=2),
                    in_=k_rows[:].rearrange("p (h m u e) -> p u h m e", h=2, u=2, e=2)[:, u],
                )
            k_bank = wop.tile([P, 4, 16], F32, name="wo")
            for t in range(4):
                nc.tensor.matmul(k_bank[:, t, :], lhsT=k_perm[:, t, :], rhs=ident_b[:], start=True, stop=True)
            regroup_x(0, 0, 0, SLICE, "v")
            for t in range(1, 4):
                regroup_w(t, "a")
            nc.vector.tensor_copy(out=cf[:], in_=k_bank[:])
            taps = cf[:, :, 3:9].rearrange("p t (a k) -> p t a k", k=3)
            flat = cf[:, :, 3:9]
            quant_x(0, 0, 1)
            nc.vector.scalar_tensor_tensor(
                out=c_abs[:].rearrange("p t a k -> p t (a k)"),
                in0=flat,
                scalar=-1.0,
                in1=flat,
                op0=ALU.mult,
                op1=ALU.max,
            )
            nc.vector.tensor_reduce(out=c_max[:], in_=c_abs[:], op=ALU.max, axis=AX.X)
            nc.vector.tensor_scalar(
                out=c_max[:], in0=c_max[:], scalar1=2.0**-32, scalar2=2.0**-100, op0=ALU.mult, op1=ALU.add
            )
            nc.vector.tensor_tensor(out=c_small[:], in0=c_abs[:, :, :, 1], in1=c_max[:], op=ALU.is_lt)
            nc.vector.scalar_tensor_tensor(
                out=c_small[:], in0=c_small[:], scalar=2.0, in1=c_max[:], op0=ALU.mult, op1=ALU.mult
            )
            regroup_w(0, "v")
            nc.vector.tensor_tensor(out=c_piv[:], in0=taps[:, :, :, 1], in1=c_small[:], op=ALU.add)
            quant_w(0)
            nc.vector.tensor_tensor(out=c_pp[:], in0=c_piv[:, :, 0], in1=c_piv[:, :, 1], op=ALU.mult)
            quant_x(0, 1, 1)
            nc.vector.tensor_tensor(
                out=c_h[:],
                in0=cf[:].rearrange("p t k -> p k t")[:, 0:3, :],
                in1=c_pp[:].unsqueeze(1).to_broadcast([P, 3, 4]),
                op=ALU.mult,
            )
            quant_w(1)
            nc.vector.reciprocal(out=c_rec[:], in_=c_piv[:])
            regroup_x(1, 0, 0, SLICE, "v")
            for k in range(2):
                nc.vector.tensor_tensor(out=c_r[:, k], in0=taps[:, :, :, 2 * k], in1=c_rec[:], op=ALU.mult)
            quant_x(1, 0, 1)
            quant_w(2)
            quant_w(3)
            for k in range(2):
                for j in moves[0]:
                    mm1_bank(j, k)
            for j in moves[0]:
                centre(j)
            for m in range(-1, 1):
                move(m)
        with tc.manual_schedule(engines={mybir.EngineType.DVE, mybir.EngineType.Pool}):
            for m in range(1, n_moves + 3):
                move(m)
            c = N_CHUNKS - 1
            for k in range(2):
                for ot in range(2):
                    mm2(c, ot, k, 1)
            for k in range(2):
                for ot in range(2):
                    evac(c, ot, k, 1, "v" if k == 1 and ot == 0 else "a")
